import numpy as np
import ml_dtypes


def mxq(x, axis, fmt="e4m3"):
    dtype, down = {"e4m3": (ml_dtypes.float8_e4m3fn, 7), "e5m2": (ml_dtypes.float8_e5m2, 14)}[fmt]
    v = np.moveaxis(np.asarray(x, np.float32).astype(ml_dtypes.bfloat16).astype(np.float64), axis, -1)
    blocks = v.reshape(v.shape[:-1] + (-1, 32))
    amax = np.abs(blocks).max(-1, keepdims=True)
    byte = np.maximum(np.where(amax > 0, np.frexp(amax)[1] - 1 + 127, 0) - down, 1)
    scale = np.exp2(byte - 127.0)
    codes = (blocks / scale).astype(np.float32).astype(dtype).astype(np.float64)
    return np.moveaxis((codes * scale).reshape(v.shape), -1, axis)


WIDE = False


def mx_kscale(k):
    if not WIDE:
        return np.ones(k)
    levels = np.array([18, -18])
    if k % 512:
        return np.exp2(np.random.permutation(np.resize(levels, k // 32))).repeat(32)
    a = np.empty((k // 512, 16))
    for p in range(k // 512):
        a[p, :8] = np.random.permutation(np.resize(levels, 8))
        for g in range(8):
            far = levels[np.abs(levels - a[p, g]) >= 10]
            a[p, g + 8] = far[np.random.randint(len(far))]
    return np.exp2(a.ravel()).repeat(32)


BF16 = ml_dtypes.bfloat16


def bf(x):
    return np.asarray(x, np.float32).astype(BF16)


def f64(x):
    return np.asarray(x).astype(np.float64)


B, S, DIM, HDIM = 2, 512, 512, 2048
T = B * S


def setup_inputs():
    s = mx_kscale(T).reshape(B, S, 1)
    u = mx_kscale(DIM)
    v = mx_kscale(HDIM)
    x0 = bf(np.random.standard_normal((B, S, DIM)))
    W1_0 = bf(np.random.standard_normal((HDIM, DIM)) * (1.0 / np.sqrt(DIM)))
    W2_0 = bf(np.random.standard_normal((HDIM, DIM)) * (1.0 / np.sqrt(HDIM)))
    g = bf(2.0 * np.random.standard_normal((B, S, DIM)) * np.exp2(np.random.randint(-6, 1, (B, S, 1))) / s * u)
    pre = f64(x0) @ f64(W1_0).T
    return {"x": bf(f64(x0) * s),
            "W1": bf(f64(W1_0) / v[:, None]),
            "W2": bf(f64(W2_0) * v[:, None] / u[None, :]),
            "pre": np.asarray(pre, np.float32),
            "grad_out": g}


def reference(x, W1, W2, pre, grad_out):
    xf = f64(x).reshape(T, DIM)
    g = f64(grad_out).reshape(T, DIM)
    zf = f64(pre).reshape(T, HDIM)
    dh = mxq(g, 1, "e5m2") @ mxq(f64(W2), 1, "e4m3").T
    dz1 = dh * (2.0 * np.maximum(zf, 0.0))
    dx = mxq(dz1, 1, "e5m2") @ mxq(f64(W1), 0, "e4m3")
    dW1 = mxq(dz1, 0, "e5m2").T @ mxq(xf, 0, "e4m3")
    return dx.reshape(B, S, DIM), dW1

@@ -1,0 +1,333 @@
+from contextlib import ExitStack
+
+import concourse.mybir as mybir
+from concourse.masks import make_identity
+
+BATCH, SEQ, DIM, HIDDEN = 2, 512, 512, 2048
+P = 128
+PACK = 4
+PASS = P * PACK
+HALF = HIDDEN // 2
+FLOPS = 3 * 2 * BATCH * SEQ * DIM * HIDDEN
+
+F32 = mybir.dt.float32
+BF16 = mybir.dt.bfloat16
+U32 = mybir.dt.uint32
+U8 = mybir.dt.uint8
+E4M3 = mybir.dt.float8_e4m3fn_x4
+E5M2 = mybir.dt.float8_e5m2_x4
+MULT, ADD, MAX = mybir.AluOpType.mult, mybir.AluOpType.add, mybir.AluOpType.max
+COPY = mybir.ActivationFunctionType.Copy
+
+SCHEDULE = (
+    "load_g.01 load_w2.01 load_g.00 load_w2.00 load_x.0 flip_g.01v flip_w2.010s flip_w2.011v flip_g.00s",
+    "  load_g.10 group_x.00v quant_w2.01 quant_g.00 load_g.11 flip_w2.001v group_x.01s load_pre.0001",
+    "  flip_w2.000s quant_g.01 quant_x.0 flip_g.11s dh.0010 load_pre.0011 quant_w2.00 load_x.1 dh.0001",
+    "dz.0010",
+    "dz.0001 group_x.11s dh.0000 flip_g.10s dh.0011 dh.0012 load_w2.12 load_pre.0021 group_x.10g",
+    "dz.0000 flip.000s load_pre.0031",
+    "dz.0011 quant_x.1 load_pre.1022 flip_w2.101s quant_g.11 dh.0002 load_pre.1002 dh.0003 flip_w2.100s",
+    "  flip_w2.111s quant_g.10",
+    "dz.0012 dh.0013",
+    "dz.0002 load_pre.0102",
+    "dz.0003 quant_w2.10 dh.1003 group_t.00002s flip.002s",
+    "dz.0013 group_t.00012g flip_w2.110s dh.1013",
+    "dz.1003 dh.1002 flip.001s",
+    "dz.1013 group_t.00102s dh.1000",
+    "dz.1002 dh.1001 flip.103s dh.1011 quant_t.0002",
+    "dz.1001",
+    "dz.1000 flip.003s group_t.00112g group_t.10012s load_w1.0 load_w1.1 dw_pass.020",
+    "dz.1011 load_pre.0122 dh.1010 quant_w2.11 dh.1012 flip.101s group_t.10002g group_w1.00s dh.0101",
+    "  group_w1.01s",
+    "dz.1012",
+    "dz.1010",
+    "dz.0101 dh.0111 load_pre.1122 dw_pass.000 quant_t.0012 dh.0103 flip.100s quant_t.1002 load_w1.2",
+    "  dw_pass.120 quant_h.00004 dw_pass.021 load_pre.1102 quant_h.00104 dw_out.02s",
+    "dz.0111 dh.0113",
+    "dz.0103 flip.102s dw_pass.001 load_w1.3 dh.0100",
+    "dz.0113 dw_pass.030 group_t.10102g dw_pass.031",
+    "dz.0100 group_w1.11g dh.0102 group_t.10112s",
+    "dz.0102 quant_t.1012 dw_out.00s flip.011s group_w1.10s dh.1113 dh.0110 quant_w1.0",
+    "dz.1113 flip.013s",
+    "dz.0110 group_t.01012g dw_pass.100 dw_pass.010 dw_pass.121 dw_pass.011 dh.1102 group_t.01002g dh.1112",
+    "  dw_pass.101 dh.1103 dw_out.12s",
+    "dz.1112 dw_out.10s flip.010s",
+    "dz.1102",
+    "dz.1103 quant_h.10004 dw_pass.130 dh.0112 dh.1110 quant_h.10104 dw_out.01s dw_out.03s dh.1111",
+    "  quant_w1.1 group_w1.20g",
+    "dz.0112 dw_pass.131",
+    "dz.1110 group_w1.21s flip.113s flip.112s dx_pass.030 dx_pass.031 dx_pass.110",
+    "dz.1111 dx_pass.111 dh.1100",
+    "dz.1100 dw_out.13s flip.012s dh.1101 group_w1.30s",
+    "dz.1101 group_w1.31g quant_w1.2 quant_h.01004 quant_h.01104 quant_h.11022 dw_pass.110 dx_pass.130",
+    "  dx_pass.000 dx_pass.001 quant_w1.3 dw_pass.111 flip.110s quant_h.11122 flip.111s quant_h.11002",
+    "  dx_pass.120 dx_pass.121 dx_pass.100 dx_pass.002 dx_pass.020 dx_pass.032 dw_out.11s dx_pass.122",
+    "  group_t.11012s dx_pass.003 dx_pass.033 dx_out.00v dx_pass.101 dx_pass.123 dx_pass.112 dx_pass.102",
+    "  quant_h.11102 dx_pass.103 dx_out.03s group_t.11002v dx_pass.113 dx_out.12s dx_pass.131 dx_out.10s",
+    "  dx_pass.132 dx_pass.133 quant_t.0102 quant_t.1102 dw_pass.200 dx_out.11s dw_pass.230 group_t.11100g",
+    "  dx_out.13v dw_pass.201 dw_pass.231 dw_pass.220 dw_pass.210 dw_pass.221 dw_out.20v dw_out.23v",
+    "  dx_pass.021 group_t.01112g dw_out.22v dx_pass.022 group_t.11111s dx_pass.023 dx_pass.010",
+    "  group_t.11101s dw_pass.211 dx_pass.011 group_t.01102s dx_pass.012 group_t.11110v quant_t.0112",
+    "  dx_pass.013 dw_pass.310 quant_t.1110 dw_pass.311 dx_out.02s quant_t.1111 dw_pass.330 dw_out.21s",
+    "  dx_out.01s dw_pass.331 dw_pass.320 dw_pass.321 dw_pass.300 dw_out.31v dw_out.33v dw_out.32v",
+    "  dw_pass.301 dw_out.30v",
+)
+
+OTHER_BANKS = {
+    ("dw", 0, 1): ("flipped", 2),
+    ("dw", 1, 1): ("dh", 3),
+    ("dw", 2, 0): ("dh", 3),
+    ("dw", 2, 2): ("dh", 3),
+    ("dw", 2, 3): ("dh", 3),
+    ("dw", 3, 0): ("dh", 3),
+    ("dw", 3, 1): ("flipped", 2),
+    ("dw", 3, 3): ("flipped", 2),
+    ("dx", 0, 0): ("dh", 3),
+    ("dx", 0, 2): ("flipped", 2),
+    ("dx", 1, 0): ("flipped", 2),
+    ("dx", 1, 2): ("dh", 3),
+}
+
+
+def tile_mlp_v_kernel(tc, x, w1, w2, pre, grad_out, out_0, out_1):
+    nc = tc.nc
+    with ExitStack() as ctx:
+        keep = ctx.enter_context(tc.tile_pool(name="keep", bufs=1))
+        stream = ctx.enter_context(tc.tile_pool(name="stream", bufs=2))
+        psum = ctx.enter_context(tc.psum_pool(name="psum", bufs=2))
+        ctx.enter_context(tc.manual_schedule())
+
+        ident = keep.tile([P, P], F32, name="ident")
+        make_identity(nc, ident[:])
+        warm = keep.tile([P, 1], F32, name="warm")
+        nc.vector.memset(warm[:], 0.0)
+        nc.scalar.activation(out=warm[:], in_=warm[:], func=COPY, scale=2.0)
+
+        raw = {}
+        pre_rows = {}
+        grouped = {}
+        dz = {}
+        banks = {}
+        codes = {}
+
+        def load_g(b, half):
+            if ("g", b) not in raw:
+                raw["g", b] = keep.tile([P, 4, DIM], BF16, name="g_raw%d" % b)
+            j = slice(2 * half, 2 * half + 2)
+            src = grad_out[b].rearrange("(p j) d -> p j d", j=4)
+            nc.sync.dma_start(out=raw["g", b][:, j, :], in_=src[:, j, :])
+
+        def load_x(b):
+            raw["x", b] = stream.tile([P, 4, DIM], BF16, name="xw_raw", bufs=4)
+            nc.sync.dma_start(out=raw["x", b][:], in_=x[b].rearrange("(p j) d -> p j d", j=4))
+
+        def load_w1(q):
+            raw["w1", q] = stream.tile([P, 4, DIM], BF16, name="xw_raw", bufs=4)
+            src = w1[PASS * q : PASS * q + PASS, :].rearrange("(p t) d -> p t d", t=4)
+            nc.sync.dma_start(out=raw["w1", q][:], in_=src)
+
+        def load_w2(c, u):
+            if ("v", c) not in raw:
+                raw["v", c] = stream.tile([P, 2, 2, 2, DIM], BF16, name="w2_raw", bufs=2)
+            rows = w2[HALF * c : HALF * c + HALF, :]
+            if u == 2:
+                nc.sync.dma_start(
+                    out=raw["v", c][:].rearrange("p s u e d -> p s (u e d)"),
+                    in_=rows.rearrange("(s p f) d -> p s (f d)", s=2, f=4),
+                )
+            else:
+                nc.sync.dma_start(
+                    out=raw["v", c][:].rearrange("p s u e d -> p s u (e d)")[:, :, u, :],
+                    in_=rows.rearrange("(s p u e) d -> p s u (e d)", s=2, u=2, e=2)[:, :, u, :],
+                )
+
+        def load_pre(b, c, j, n):
+            if (b, c, j // 2) not in pre_rows:
+                pre_rows[b, c, j // 2] = stream.tile([P, 2, HALF], F32, name="pre_rows", bufs=5)
+            src = pre[b].rearrange("(p j) h -> p j h", j=4)
+            nc.sync.dma_start(
+                out=pre_rows[b, c, j // 2][:, j % 2 : j % 2 + n, :],
+                in_=src[:, j : j + n, HALF * c : HALF * c + HALF],
+            )
+
+        def copy_words(engine, out, in_):
+            if engine == "s":
+                nc.scalar.copy(out=out, in_=in_)
+            else:
+                nc.vector.tensor_copy(out=out, in_=in_)
+
+        def interleave(engine, out, in_):
+            out = out.rearrange("p (c i t) -> p c t i", i=4, t=4)
+            if engine == "s":
+                nc.scalar.copy(out=out, in_=in_)
+            elif engine == "v":
+                nc.vector.tensor_copy(out=out, in_=in_)
+            else:
+                nc.gpsimd.tensor_scalar(out=out, in0=in_, scalar1=1.0, scalar2=0.0, op0=MULT, op1=ADD)
+
+        def group_tile(key, name, bufs, passes=1):
+            if key not in grouped:
+                grouped[key] = stream.tile([P, passes * PACK * PASS], BF16, name=name, bufs=bufs, align_bytes=64)
+            return grouped[key]
+
+        def quantise(key, dtype, src, lo, hi, base=0):
+            if key not in codes:
+                label = "_".join([str(k) for k in key])
+                codes[key] = (
+                    keep.tile([P, PASS], U32, name="codes_" + label, align_bytes=64),
+                    keep.tile([P, PASS], U8, name="scales_" + label, align_bytes=64),
+                )
+            words, scales = codes[key]
+            nc.vector.quantize_mx(
+                out=words[:, lo:hi].bitcast(dtype),
+                scales=scales[:, lo:hi],
+                in_=src[:, base + PACK * lo : base + PACK * hi],
+            )
+
+        def transposes(views):
+            bank = psum.tile([P, 4, P], F32, name="flipped", bufs=2)
+            for i in range(4):
+                nc.tensor.transpose(bank[:, i, :], views[i], ident[:])
+            return bank
+
+        def multiply(out, left, m, right, start, stop):
+            cols = slice(P * m, P * m + P)
+            nc.tensor.matmul_mx(
+                out=out,
+                lhsT=codes[left][0][:, cols].bitcast(E5M2),
+                lhsT_scale=codes[left][1][:, cols],
+                rhs=codes[right][0][:].bitcast(E4M3),
+                rhs_scale=codes[right][1][:],
+                start=start,
+                stop=stop,
+            )
+
+        def flip_g(b, half, engine):
+            dst = group_tile(("g", b), "grouped_gv", 3)
+            words = raw["g", b][:].bitcast(F32)
+            bank = transposes([words[:, 2 * half + i // 2, i % 2 :: 2] for i in range(4)])
+            copy_words(
+                engine,
+                out=dst[:].bitcast(F32)[:, PASS * half : PASS * half + PASS].rearrange(
+                    "k (j n v) -> k j n v", j=2, v=2
+                ),
+                in_=bank[:].rearrange("k (j v) n -> k j n v", v=2),
+            )
+
+        def quant_g(b, half):
+            quantise(("g", b), E5M2, grouped["g", b], 2 * P * half, 2 * P * half + 2 * P)
+
+        def flip_w2(c, u, s, engine):
+            dst = group_tile(("v", c, u), "grouped_gv", 3)
+            words = raw["v", c][:].bitcast(F32)
+            bank = transposes([words[:, s, u, i // 2, i % 2 :: 2] for i in range(4)])
+            copy_words(
+                engine,
+                out=dst[:].bitcast(F32)[:, PASS * s : PASS * s + PASS].rearrange("k (n i) -> k n i", i=4),
+                in_=bank[:].rearrange("k i n -> k n i"),
+            )
+
+        def quant_w2(c, u):
+            quantise(("v", c, u), E4M3, grouped["v", c, u], 0, PASS)
+
+        def group_xw(what, i, half, engine):
+            dst = group_tile((what, i), "grouped_xw", 2)
+            cols = slice(2 * P * half, 2 * P * half + 2 * P)
+            interleave(
+                engine,
+                out=dst[:, PACK * cols.start : PACK * cols.stop],
+                in_=raw[what, i][:, :, cols].rearrange("p t (c i) -> p c t i", i=4),
+            )
+
+        def make_dh(b, c, u, j):
+            bank = psum.tile([P, PASS], F32, name="dh", bufs=3)
+            multiply(bank[:], ("g", b), j, ("v", c, u), True, True)
+            banks["dh", b, c, u, j] = bank
+
+        def make_dz(b, c, u, j):
+            if (b, c, u) not in dz:
+                dz[b, c, u] = stream.tile([P, 4, PASS], BF16, name="dz", bufs=4, align_bytes=64)
+            rows = pre_rows[b, c, j // 2][:, j % 2, :].rearrange("p (n u e) -> p n u e", u=2, e=2)
+            nc.vector.scalar_tensor_tensor(
+                out=dz[b, c, u][:, j, :].rearrange("p (n e) -> p n e", e=2),
+                in0=rows[:, :, u, :],
+                scalar=0.0,
+                in1=banks["dh", b, c, u, j][:].rearrange("p (n e) -> p n e", e=2),
+                op0=MAX,
+                op1=MULT,
+            )
+
+        def flip_dz(b, c, j, engine):
+            dst = group_tile(("h", b, c), "grouped_h", 2, passes=2)
+            words = [dz[b, c, u][:, j, :].bitcast(F32) for u in range(2)]
+            bank = transposes([words[i % 2][:, P * (i // 2) : P * (i // 2) + P] for i in range(4)])
+            copy_words(
+                engine,
+                out=dst[:].bitcast(F32).rearrange("k (s n u) -> k s n u", s=2, u=2)[:, :, P * j : P * j + P, :],
+                in_=bank[:].rearrange("k (s u) n -> k s n u", u=2),
+            )
+
+        def quant_h(b, c, s, j, n):
+            quantise(("h", b, 2 * c + s), E5M2, grouped["h", b, c], P * j, P * (j + n), PACK * PASS * s)
+
+        def group_t(b, c, u, e, s, engine):
+            dst = group_tile(("t", b, c, u), "grouped_t", 3)
+            first, n = (2 * P * e, 2 * P) if s == 2 else (2 * P * e + P * s, P)
+            src = dz[b, c, u][:].rearrange("p t (c i e) -> p e c t i", i=4, e=2)[:, e, :, :, :]
+            runs = slice(0, 2 * P // 4) if s == 2 else slice(P // 4 * s, P // 4 * (s + 1))
+            interleave(engine, out=dst[:, PACK * first : PACK * (first + n)], in_=src[:, runs, :, :])
+
+        def quant_t(b, c, u, e):
+            lo, hi = (0, PASS) if e == 2 else (2 * P * e, 2 * P * e + 2 * P)
+            quantise(("t", b, 2 * c + u), E5M2, grouped["t", b, c, u], lo, hi)
+
+        def add_pass(kind, a, m, q):
+            if q == 0:
+                tag, bufs = OTHER_BANKS.get((kind, a, m), ("out", 3))
+                banks[kind, a, m] = psum.tile([P, 4, P], F32, name=tag, bufs=bufs)[:].rearrange("p a b -> p (a b)")
+            left, right, last = (("h", a, q), ("w1", q), 3) if kind == "dx" else (("t", q, a), ("x", q), 1)
+            multiply(banks[kind, a, m], left, m, right, q == 0, q == last)
+
+        def leave(kind, a, m, engine):
+            out = stream.tile([P, DIM], F32, name="out_rows", bufs=8)
+            if engine == "s":
+                nc.scalar.activation(out=out[:], in_=banks[kind, a, m], func=COPY, scale=2.0)
+            else:
+                nc.vector.tensor_scalar(out=out[:], in0=banks[kind, a, m], scalar1=2.0, scalar2=None, op0=MULT)
+            if kind == "dx":
+                dst = out_0[a].rearrange("(p j) d -> p j d", j=4)[:, m, :]
+            else:
+                c, u, e, s = a // 2, a % 2, m // 2, m % 2
+                first = HALF * c + PASS * s
+                dst = out_1[first : first + PASS, :].rearrange("(p f) d -> p f d", f=4)[:, 2 * u + e, :]
+            nc.sync.dma_start(out=dst, in_=out[:])
+
+        steps = {
+            "load_g": load_g,
+            "load_x": load_x,
+            "load_w1": load_w1,
+            "load_w2": load_w2,
+            "load_pre": load_pre,
+            "flip_g": flip_g,
+            "quant_g": quant_g,
+            "flip_w2": flip_w2,
+            "quant_w2": quant_w2,
+            "group_x": lambda b, half, engine: group_xw("x", b, half, engine),
+            "quant_x": lambda b: quantise(("x", b), E4M3, grouped["x", b], 0, PASS),
+            "group_w1": lambda q, half, engine: group_xw("w1", q, half, engine),
+            "quant_w1": lambda q: quantise(("w1", q), E4M3, grouped["w1", q], 0, PASS),
+            "dh": make_dh,
+            "dz": make_dz,
+            "flip": flip_dz,
+            "quant_h": quant_h,
+            "group_t": group_t,
+            "quant_t": quant_t,
+            "dx_pass": lambda b, j, q: add_pass("dx", b, j, q),
+            "dx_out": lambda b, j, engine: leave("dx", b, j, engine),
+            "dw_pass": lambda cu, m, b: add_pass("dw", cu, m, b),
+            "dw_out": lambda cu, m, engine: leave("dw", cu, m, engine),
+        }
+        for row in SCHEDULE:
+            for word in row.split():
+                name, arguments = word.split(".")
+                steps[name](*[a if a in "svg" else int(a) for a in arguments])

@@ -7,7 +7,6 @@ BATCH, SEQ, DIM, HIDDEN = 2, 512, 512, 2048
 P = 128
 PACK = 4
 PASS = P * PACK
-HALF = HIDDEN // 2
 FLOPS = 3 * 2 * BATCH * SEQ * DIM * HIDDEN
 
 F32 = mybir.dt.float32
@@ -19,74 +18,13 @@ E5M2 = mybir.dt.float8_e5m2_x4
 MULT, ADD, MAX = mybir.AluOpType.mult, mybir.AluOpType.add, mybir.AluOpType.max
 COPY = mybir.ActivationFunctionType.Copy
 
-SCHEDULE = (
-    "load_g.01 load_w2.01 load_g.00 load_w2.00 load_x.0 flip_g.01v flip_w2.010s flip_w2.011v flip_g.00s",
-    "  load_g.10 group_x.00v quant_w2.01 quant_g.00 load_g.11 flip_w2.001v group_x.01s load_pre.0001",
-    "  flip_w2.000s quant_g.01 quant_x.0 flip_g.11s dh.0010 load_pre.0011 quant_w2.00 load_x.1 dh.0001",
-    "dz.0010",
-    "dz.0001 group_x.11s dh.0000 flip_g.10s dh.0011 dh.0012 load_w2.12 load_pre.0021 group_x.10g",
-    "dz.0000 flip.000s load_pre.0031",
-    "dz.0011 quant_x.1 load_pre.1022 flip_w2.101s quant_g.11 dh.0002 load_pre.1002 dh.0003 flip_w2.100s",
-    "  flip_w2.111s quant_g.10",
-    "dz.0012 dh.0013",
-    "dz.0002 load_pre.0102",
-    "dz.0003 quant_w2.10 dh.1003 group_t.00002s flip.002s",
-    "dz.0013 group_t.00012g flip_w2.110s dh.1013",
-    "dz.1003 dh.1002 flip.001s",
-    "dz.1013 group_t.00102s dh.1000",
-    "dz.1002 dh.1001 flip.103s dh.1011 quant_t.0002",
-    "dz.1001",
-    "dz.1000 flip.003s group_t.00112g group_t.10012s load_w1.0 load_w1.1 dw_pass.020",
-    "dz.1011 load_pre.0122 dh.1010 quant_w2.11 dh.1012 flip.101s group_t.10002g group_w1.00s dh.0101",
-    "  group_w1.01s",
-    "dz.1012",
-    "dz.1010",
-    "dz.0101 dh.0111 load_pre.1122 dw_pass.000 quant_t.0012 dh.0103 flip.100s quant_t.1002 load_w1.2",
-    "  dw_pass.120 quant_h.00004 dw_pass.021 load_pre.1102 quant_h.00104 dw_out.02s",
-    "dz.0111 dh.0113",
-    "dz.0103 flip.102s dw_pass.001 load_w1.3 dh.0100",
-    "dz.0113 dw_pass.030 group_t.10102g dw_pass.031",
-    "dz.0100 group_w1.11g dh.0102 group_t.10112s",
-    "dz.0102 quant_t.1012 dw_out.00s flip.011s group_w1.10s dh.1113 dh.0110 quant_w1.0",
-    "dz.1113 flip.013s",
-    "dz.0110 group_t.01012g dw_pass.100 dw_pass.010 dw_pass.121 dw_pass.011 dh.1102 group_t.01002g dh.1112",
-    "  dw_pass.101 dh.1103 dw_out.12s",
-    "dz.1112 dw_out.10s flip.010s",
-    "dz.1102",
-    "dz.1103 quant_h.10004 dw_pass.130 dh.0112 dh.1110 quant_h.10104 dw_out.01s dw_out.03s dh.1111",
-    "  quant_w1.1 group_w1.20g",
-    "dz.0112 dw_pass.131",
-    "dz.1110 group_w1.21s flip.113s flip.112s dx_pass.030 dx_pass.031 dx_pass.110",
-    "dz.1111 dx_pass.111 dh.1100",
-    "dz.1100 dw_out.13s flip.012s dh.1101 group_w1.30s",
-    "dz.1101 group_w1.31g quant_w1.2 quant_h.01004 quant_h.01104 quant_h.11022 dw_pass.110 dx_pass.130",
-    "  dx_pass.000 dx_pass.001 quant_w1.3 dw_pass.111 flip.110s quant_h.11122 flip.111s quant_h.11002",
-    "  dx_pass.120 dx_pass.121 dx_pass.100 dx_pass.002 dx_pass.020 dx_pass.032 dw_out.11s dx_pass.122",
-    "  group_t.11012s dx_pass.003 dx_pass.033 dx_out.00v dx_pass.101 dx_pass.123 dx_pass.112 dx_pass.102",
-    "  quant_h.11102 dx_pass.103 dx_out.03s group_t.11002v dx_pass.113 dx_out.12s dx_pass.131 dx_out.10s",
-    "  dx_pass.132 dx_pass.133 quant_t.0102 quant_t.1102 dw_pass.200 dx_out.11s dw_pass.230 group_t.11100g",
-    "  dx_out.13v dw_pass.201 dw_pass.231 dw_pass.220 dw_pass.210 dw_pass.221 dw_out.20v dw_out.23v",
-    "  dx_pass.021 group_t.01112g dw_out.22v dx_pass.022 group_t.11111s dx_pass.023 dx_pass.010",
-    "  group_t.11101s dw_pass.211 dx_pass.011 group_t.01102s dx_pass.012 group_t.11110v quant_t.0112",
-    "  dx_pass.013 dw_pass.310 quant_t.1110 dw_pass.311 dx_out.02s quant_t.1111 dw_pass.330 dw_out.21s",
-    "  dx_out.01s dw_pass.331 dw_pass.320 dw_pass.321 dw_pass.300 dw_out.31v dw_out.33v dw_out.32v",
-    "  dw_pass.301 dw_out.30v",
-)
-
-OTHER_BANKS = {
-    ("dw", 0, 1): ("flipped", 2),
-    ("dw", 1, 1): ("dh", 3),
-    ("dw", 2, 0): ("dh", 3),
-    ("dw", 2, 2): ("dh", 3),
-    ("dw", 2, 3): ("dh", 3),
-    ("dw", 3, 0): ("dh", 3),
-    ("dw", 3, 1): ("flipped", 2),
-    ("dw", 3, 3): ("flipped", 2),
-    ("dx", 0, 0): ("dh", 3),
-    ("dx", 0, 2): ("flipped", 2),
-    ("dx", 1, 0): ("flipped", 2),
-    ("dx", 1, 2): ("dh", 3),
-}
+DH_BANKS = (0, 1, 2, 3)
+FLIP_BANKS = (4, 5, 6, 7)
+SUM_BANKS = FLIP_BANKS
+SLABS = 8
+PRE_BUFS = {1: 4, 2: 10}
+DZ_BUFS = 6
+GROUP_BUFS = {"words": 4, "rows": 2, "pool": 1}
 
 
 def tile_mlp_v_kernel(tc, x, w1, w2, pre, grad_out, out_0, out_1):
@@ -94,61 +32,53 @@ def tile_mlp_v_kernel(tc, x, w1, w2, pre, grad_out, out_0, out_1):
     with ExitStack() as ctx:
         keep = ctx.enter_context(tc.tile_pool(name="keep", bufs=1))
         stream = ctx.enter_context(tc.tile_pool(name="stream", bufs=2))
-        psum = ctx.enter_context(tc.psum_pool(name="psum", bufs=2))
+        psum = ctx.enter_context(tc.psum_pool(name="psum", bufs=1))
         ctx.enter_context(tc.manual_schedule())
 
         ident = keep.tile([P, P], F32, name="ident")
         make_identity(nc, ident[:])
-        warm = keep.tile([P, 1], F32, name="warm")
-        nc.vector.memset(warm[:], 0.0)
-        nc.scalar.activation(out=warm[:], in_=warm[:], func=COPY, scale=2.0)
 
         raw = {}
-        pre_rows = {}
         grouped = {}
         dz = {}
         banks = {}
         codes = {}
+        staged = {}
+        turns = {}
+
+        def bank(ring, key):
+            n = turns.get(ring, 0)
+            turns[ring] = n + 1
+            banks[key] = psum.tile([P, PASS], F32, name="bank%d" % ring[n % len(ring)])
+            return banks[key]
+
+        def slab(dtype, shape):
+            return stream.tile([P] + shape, dtype, name="slab", bufs=SLABS)
 
         def load_g(b, half):
-            if ("g", b) not in raw:
-                raw["g", b] = keep.tile([P, 4, DIM], BF16, name="g_raw%d" % b)
-            j = slice(2 * half, 2 * half + 2)
+            raw["g", b, half] = keep.tile([P, 2, DIM], BF16, name="g_raw%d%d" % (b, half))
             src = grad_out[b].rearrange("(p j) d -> p j d", j=4)
-            nc.sync.dma_start(out=raw["g", b][:, j, :], in_=src[:, j, :])
+            nc.sync.dma_start(out=raw["g", b, half][:], in_=src[:, 2 * half : 2 * half + 2, :])
 
-        def load_x(b):
-            raw["x", b] = stream.tile([P, 4, DIM], BF16, name="xw_raw", bufs=4)
-            nc.sync.dma_start(out=raw["x", b][:], in_=x[b].rearrange("(p j) d -> p j d", j=4))
+        def load_w2(q, u):
+            raw["w2", q, u] = stream.tile([P, 2, DIM], BF16, name="w2_raw", bufs=4)
+            src = w2[PASS * q : PASS * q + PASS, :].rearrange("(p t) d -> p t d", t=4)
+            nc.sync.dma_start(out=raw["w2", q, u][:], in_=src[:, 2 * u : 2 * u + 2, :])
 
-        def load_w1(q):
-            raw["w1", q] = stream.tile([P, 4, DIM], BF16, name="xw_raw", bufs=4)
-            src = w1[PASS * q : PASS * q + PASS, :].rearrange("(p t) d -> p t d", t=4)
-            nc.sync.dma_start(out=raw["w1", q][:], in_=src)
-
-        def load_w2(c, u):
-            if ("v", c) not in raw:
-                raw["v", c] = stream.tile([P, 2, 2, 2, DIM], BF16, name="w2_raw", bufs=2)
-            rows = w2[HALF * c : HALF * c + HALF, :]
-            if u == 2:
-                nc.sync.dma_start(
-                    out=raw["v", c][:].rearrange("p s u e d -> p s (u e d)"),
-                    in_=rows.rearrange("(s p f) d -> p s (f d)", s=2, f=4),
-                )
+        def load_rows(what, i):
+            if what == "x":
+                raw[what, i] = slab(BF16, [4, DIM])
             else:
-                nc.sync.dma_start(
-                    out=raw["v", c][:].rearrange("p s u e d -> p s u (e d)")[:, :, u, :],
-                    in_=rows.rearrange("(s p u e) d -> p s u (e d)", s=2, u=2, e=2)[:, :, u, :],
-                )
+                raw[what, i] = stream.tile([P, 4, DIM], BF16, name="pre_rows2", bufs=PRE_BUFS[2])
+            rows = x[i] if what == "x" else w1[PASS * i : PASS * i + PASS, :]
+            nc.sync.dma_start(out=raw[what, i][:], in_=rows.rearrange("(p t) d -> p t d", t=4))
 
-        def load_pre(b, c, j, n):
-            if (b, c, j // 2) not in pre_rows:
-                pre_rows[b, c, j // 2] = stream.tile([P, 2, HALF], F32, name="pre_rows", bufs=5)
+        def load_pre(q, b, j, n):
+            tile = stream.tile([P, n, PASS], F32, name="pre_rows%d" % n, bufs=PRE_BUFS[n])
             src = pre[b].rearrange("(p j) h -> p j h", j=4)
-            nc.sync.dma_start(
-                out=pre_rows[b, c, j // 2][:, j % 2 : j % 2 + n, :],
-                in_=src[:, j : j + n, HALF * c : HALF * c + HALF],
-            )
+            nc.sync.dma_start(out=tile[:], in_=src[:, j : j + n, PASS * q : PASS * q + PASS])
+            for i in range(n):
+                raw["pre", q, b, j + i] = tile[:, i, :]
 
         def copy_words(engine, out, in_):
             if engine == "s":
@@ -165,12 +95,12 @@ def tile_mlp_v_kernel(tc, x, w1, w2, pre, grad_out, out_0, out_1):
             else:
                 nc.gpsimd.tensor_scalar(out=out, in0=in_, scalar1=1.0, scalar2=0.0, op0=MULT, op1=ADD)
 
-        def group_tile(key, name, bufs, passes=1):
+        def group_tile(key, name):
             if key not in grouped:
-                grouped[key] = stream.tile([P, passes * PACK * PASS], BF16, name=name, bufs=bufs, align_bytes=64)
+                grouped[key] = stream.tile([P, PACK * PASS], BF16, name=name, bufs=GROUP_BUFS[name], align_bytes=64)
             return grouped[key]
 
-        def quantise(key, dtype, src, lo, hi, base=0):
+        def quantise(key, lo=0, hi=PASS):
             if key not in codes:
                 label = "_".join([str(k) for k in key])
                 codes[key] = (
@@ -178,17 +108,15 @@ def tile_mlp_v_kernel(tc, x, w1, w2, pre, grad_out, out_0, out_1):
                     keep.tile([P, PASS], U8, name="scales_" + label, align_bytes=64),
                 )
             words, scales = codes[key]
+            dtype = E4M3 if key[0] in ("x", "w1", "w2") else E5M2
             nc.vector.quantize_mx(
-                out=words[:, lo:hi].bitcast(dtype),
-                scales=scales[:, lo:hi],
-                in_=src[:, base + PACK * lo : base + PACK * hi],
+                out=words[:, lo:hi].bitcast(dtype), scales=scales[:, lo:hi], in_=grouped[key][:, PACK * lo : PACK * hi]
             )
 
-        def transposes(views):
-            bank = psum.tile([P, 4, P], F32, name="flipped", bufs=2)
+        def transposes(key, views, ring=FLIP_BANKS):
+            dst = bank(ring, key)
             for i in range(4):
-                nc.tensor.transpose(bank[:, i, :], views[i], ident[:])
-            return bank
+                nc.tensor.transpose(dst[:, P * i : P * i + P], views[i], ident[:])
 
         def multiply(out, left, m, right, start, stop):
             cols = slice(P * m, P * m + P)
@@ -202,132 +130,354 @@ def tile_mlp_v_kernel(tc, x, w1, w2, pre, grad_out, out_0, out_1):
                 stop=stop,
             )
 
-        def flip_g(b, half, engine):
-            dst = group_tile(("g", b), "grouped_gv", 3)
-            words = raw["g", b][:].bitcast(F32)
-            bank = transposes([words[:, 2 * half + i // 2, i % 2 :: 2] for i in range(4)])
+        def flip_g(b, half, ring=FLIP_BANKS):
+            words = raw["g", b, half][:].bitcast(F32)
+            transposes(("g", b, half), [words[:, i // 2, i % 2 :: 2] for i in range(4)], ring)
+
+        def take_g(b, half, engine):
+            dst = group_tile(("g", b), "words")[:].bitcast(F32)[:, PASS * half : PASS * half + PASS]
             copy_words(
                 engine,
-                out=dst[:].bitcast(F32)[:, PASS * half : PASS * half + PASS].rearrange(
-                    "k (j n v) -> k j n v", j=2, v=2
-                ),
-                in_=bank[:].rearrange("k (j v) n -> k j n v", v=2),
+                out=dst.rearrange("k (j n v) -> k j n v", j=2, v=2),
+                in_=banks["g", b, half][:].rearrange("k (j v n) -> k j n v", j=2, v=2),
             )
 
-        def quant_g(b, half):
-            quantise(("g", b), E5M2, grouped["g", b], 2 * P * half, 2 * P * half + 2 * P)
+        def flip_g_tile(b, j, ring):
+            words = raw["g", b, j // 2][:].bitcast(F32)
+            dst = bank(ring, ("g1", b, j))
+            for v in range(2):
+                nc.tensor.transpose(dst[:, P * v : P * v + P], words[:, j % 2, v::2], ident[:])
 
-        def flip_w2(c, u, s, engine):
-            dst = group_tile(("v", c, u), "grouped_gv", 3)
-            words = raw["v", c][:].bitcast(F32)
-            bank = transposes([words[:, s, u, i // 2, i % 2 :: 2] for i in range(4)])
+        def take_g_tile(b, j, engine):
+            dst = group_tile(("g", b), "words")[:].bitcast(F32)[:, 2 * P * j : 2 * P * j + 2 * P]
             copy_words(
                 engine,
-                out=dst[:].bitcast(F32)[:, PASS * s : PASS * s + PASS].rearrange("k (n i) -> k n i", i=4),
-                in_=bank[:].rearrange("k i n -> k n i"),
+                out=dst.rearrange("k (n v) -> k n v", v=2),
+                in_=banks["g1", b, j][:, : 2 * P].rearrange("k (v n) -> k n v", v=2),
             )
 
-        def quant_w2(c, u):
-            quantise(("v", c, u), E4M3, grouped["v", c, u], 0, PASS)
+        def flip_w2(q, u, ring=FLIP_BANKS):
+            words = raw["w2", q, u][:].bitcast(F32)
+            transposes(("w2", q, u), [words[:, i // 2, i % 2 :: 2] for i in range(4)], ring)
 
-        def group_xw(what, i, half, engine):
-            dst = group_tile((what, i), "grouped_xw", 2)
-            cols = slice(2 * P * half, 2 * P * half + 2 * P)
+        def take_w2(q, u, engine):
+            dst = group_tile(("w2", q), "words")[:].bitcast(F32)[:, PASS * u : PASS * u + PASS]
+            copy_words(
+                engine,
+                out=dst.rearrange("k (n i) -> k n i", i=4),
+                in_=banks["w2", q, u][:].rearrange("k (i n) -> k n i", i=4),
+            )
+
+        def group_rows(what, i, lo, hi, engine, name):
+            dst = group_tile((what, i), name)
             interleave(
                 engine,
-                out=dst[:, PACK * cols.start : PACK * cols.stop],
-                in_=raw[what, i][:, :, cols].rearrange("p t (c i) -> p c t i", i=4),
+                out=dst[:, PACK * lo : PACK * hi],
+                in_=raw[what, i][:, :, lo:hi].rearrange("p t (c i) -> p c t i", i=4),
             )
 
-        def make_dh(b, c, u, j):
-            bank = psum.tile([P, PASS], F32, name="dh", bufs=3)
-            multiply(bank[:], ("g", b), j, ("v", c, u), True, True)
-            banks["dh", b, c, u, j] = bank
+        def make_dh(q, b, j):
+            multiply(bank(DH_BANKS, ("dh", q, b, j))[:], ("g", b), j, ("w2", q), True, True)
 
-        def make_dz(b, c, u, j):
-            if (b, c, u) not in dz:
-                dz[b, c, u] = stream.tile([P, 4, PASS], BF16, name="dz", bufs=4, align_bytes=64)
-            rows = pre_rows[b, c, j // 2][:, j % 2, :].rearrange("p (n u e) -> p n u e", u=2, e=2)
-            nc.vector.scalar_tensor_tensor(
-                out=dz[b, c, u][:, j, :].rearrange("p (n e) -> p n e", e=2),
-                in0=rows[:, :, u, :],
-                scalar=0.0,
-                in1=banks["dh", b, c, u, j][:].rearrange("p (n e) -> p n e", e=2),
-                op0=MAX,
-                op1=MULT,
-            )
+        def make_dz(q, b, j):
+            if (q, b) not in dz:
+                dz[q, b] = stream.tile([P, 4, PASS], BF16, name="dz", bufs=DZ_BUFS, align_bytes=64)
+            rows = raw["pre", q, b, j].rearrange("p (n u e) -> p n u e", u=2, e=2)
+            for u in range(2):
+                cols = slice(2 * P * u, 2 * P * u + 2 * P)
+                nc.vector.scalar_tensor_tensor(
+                    out=dz[q, b][:, j, cols].rearrange("p (n e) -> p n e", e=2),
+                    in0=rows[:, :, u, :],
+                    scalar=0.0,
+                    in1=banks["dh", q, b, j][:, cols].rearrange("p (n e) -> p n e", e=2),
+                    op0=MAX,
+                    op1=MULT,
+                )
 
-        def flip_dz(b, c, j, engine):
-            dst = group_tile(("h", b, c), "grouped_h", 2, passes=2)
-            words = [dz[b, c, u][:, j, :].bitcast(F32) for u in range(2)]
-            bank = transposes([words[i % 2][:, P * (i // 2) : P * (i // 2) + P] for i in range(4)])
+        def flip_dz(q, b, half, ring=FLIP_BANKS):
+            words = dz[q, b][:].bitcast(F32)
+            transposes(("h", q, b, half), [words[:, 2 * half + i // 2, P * (i % 2) : P * (i % 2) + P] for i in range(4)], ring)
+
+        def take_dz(q, b, half, engine, name="words"):
+            dst = group_tile(("h", q, b), name)[:].bitcast(F32)[:, PASS * half : PASS * half + PASS]
             copy_words(
                 engine,
-                out=dst[:].bitcast(F32).rearrange("k (s n u) -> k s n u", s=2, u=2)[:, :, P * j : P * j + P, :],
-                in_=bank[:].rearrange("k (s u) n -> k s n u", u=2),
+                out=dst.rearrange("k (j n u) -> k j n u", j=2, u=2),
+                in_=banks["h", q, b, half][:].rearrange("k (j u n) -> k j n u", j=2, u=2),
             )
 
-        def quant_h(b, c, s, j, n):
-            quantise(("h", b, 2 * c + s), E5M2, grouped["h", b, c], P * j, P * (j + n), PACK * PASS * s)
+        def group_t(q, b, m0, m1, engine, name):
+            dst = group_tile(("t", q, b), name)
+            src = dz[q, b][:].rearrange("p t (c i e) -> p e c t i", i=4, e=2)[:, m0 // 2, :, :, :]
+            runs = slice(P // 4 * (m0 % 2), P // 4 * (m0 % 2 + m1 - m0))
+            interleave(engine, out=dst[:, PACK * P * m0 : PACK * P * m1], in_=src[:, runs, :, :])
 
-        def group_t(b, c, u, e, s, engine):
-            dst = group_tile(("t", b, c, u), "grouped_t", 3)
-            first, n = (2 * P * e, 2 * P) if s == 2 else (2 * P * e + P * s, P)
-            src = dz[b, c, u][:].rearrange("p t (c i e) -> p e c t i", i=4, e=2)[:, e, :, :, :]
-            runs = slice(0, 2 * P // 4) if s == 2 else slice(P // 4 * s, P // 4 * (s + 1))
-            interleave(engine, out=dst[:, PACK * first : PACK * (first + n)], in_=src[:, runs, :, :])
+        def dx_passes(b, j, qs, ring=SUM_BANKS):
+            for q in qs:
+                if q == 0:
+                    bank(ring, ("dx", b, j))
+                multiply(banks["dx", b, j][:], ("h", q, b), j, ("w1", q), q == 0, q == 3)
 
-        def quant_t(b, c, u, e):
-            lo, hi = (0, PASS) if e == 2 else (2 * P * e, 2 * P * e + 2 * P)
-            quantise(("t", b, 2 * c + u), E5M2, grouped["t", b, c, u], lo, hi)
+        def dw_passes(q, m, bs, ring=SUM_BANKS):
+            for b in bs:
+                if b == 0:
+                    bank(ring, ("dw", q, m))
+                multiply(banks["dw", q, m][:], ("t", q, b), m, ("x", b), b == 0, b == 1)
 
-        def add_pass(kind, a, m, q):
-            if q == 0:
-                tag, bufs = OTHER_BANKS.get((kind, a, m), ("out", 3))
-                banks[kind, a, m] = psum.tile([P, 4, P], F32, name=tag, bufs=bufs)[:].rearrange("p a b -> p (a b)")
-            left, right, last = (("h", a, q), ("w1", q), 3) if kind == "dx" else (("t", q, a), ("x", q), 1)
-            multiply(banks[kind, a, m], left, m, right, q == 0, q == last)
-
-        def leave(kind, a, m, engine):
-            out = stream.tile([P, DIM], F32, name="out_rows", bufs=8)
+        def scale_out(engine, out, in_):
             if engine == "s":
-                nc.scalar.activation(out=out[:], in_=banks[kind, a, m], func=COPY, scale=2.0)
+                nc.scalar.activation(out=out, in_=in_, func=COPY, scale=2.0)
             else:
-                nc.vector.tensor_scalar(out=out[:], in0=banks[kind, a, m], scalar1=2.0, scalar2=None, op0=MULT)
-            if kind == "dx":
-                dst = out_0[a].rearrange("(p j) d -> p j d", j=4)[:, m, :]
-            else:
-                c, u, e, s = a // 2, a % 2, m // 2, m % 2
-                first = HALF * c + PASS * s
-                dst = out_1[first : first + PASS, :].rearrange("(p f) d -> p f d", f=4)[:, 2 * u + e, :]
-            nc.sync.dma_start(out=dst, in_=out[:])
+                nc.vector.tensor_scalar(out=out, in0=in_, scalar1=2.0, scalar2=None, op0=MULT)
 
-        steps = {
-            "load_g": load_g,
-            "load_x": load_x,
-            "load_w1": load_w1,
-            "load_w2": load_w2,
-            "load_pre": load_pre,
-            "flip_g": flip_g,
-            "quant_g": quant_g,
-            "flip_w2": flip_w2,
-            "quant_w2": quant_w2,
-            "group_x": lambda b, half, engine: group_xw("x", b, half, engine),
-            "quant_x": lambda b: quantise(("x", b), E4M3, grouped["x", b], 0, PASS),
-            "group_w1": lambda q, half, engine: group_xw("w1", q, half, engine),
-            "quant_w1": lambda q: quantise(("w1", q), E4M3, grouped["w1", q], 0, PASS),
-            "dh": make_dh,
-            "dz": make_dz,
-            "flip": flip_dz,
-            "quant_h": quant_h,
-            "group_t": group_t,
-            "quant_t": quant_t,
-            "dx_pass": lambda b, j, q: add_pass("dx", b, j, q),
-            "dx_out": lambda b, j, engine: leave("dx", b, j, engine),
-            "dw_pass": lambda cu, m, b: add_pass("dw", cu, m, b),
-            "dw_out": lambda cu, m, engine: leave("dw", cu, m, engine),
-        }
-        for row in SCHEDULE:
-            for word in row.split():
-                name, arguments = word.split(".")
-                steps[name](*[a if a in "svg" else int(a) for a in arguments])
+        def leave(pair, i, src, rows, engine, single):
+            if pair not in staged:
+                staged[pair] = [slab(F32, [2, DIM]), 0]
+            tile = staged[pair][0]
+            scale_out(engine, tile[:, i, :], src[:])
+            staged[pair][1] = staged[pair][1] + 1
+            if single:
+                nc.sync.dma_start(out=rows[:, i, :], in_=tile[:, i, :])
+            elif staged[pair][1] == 2:
+                nc.sync.dma_start(out=rows, in_=tile[:])
+
+        def leave_dx(b, j, engine, single=False):
+            rows = out_0[b].rearrange("(p j) d -> p j d", j=4)[:, j - j % 2 : j - j % 2 + 2, :]
+            leave(("dx", b, j // 2), j % 2, banks["dx", b, j], rows, engine, single)
+
+        def leave_dw(q, m, engine, single=False):
+            e, u = m // 2, m % 2
+            rows = out_1[PASS * q : PASS * q + PASS, :].rearrange("(p f) d -> p f d", f=4)[:, 2 * u : 2 * u + 2, :]
+            leave(("dw", q, u), e, banks["dw", q, m], rows, engine, single)
+
+        units = [(0, 0), (0, 1), (1, 0), (1, 1), (2, 0), (3, 0), (2, 1), (3, 1)]
+        EARLY = FLIP_BANKS
+        J = range(4)
+
+        def dh(m, js):
+            for j in js:
+                make_dh(units[m][0], units[m][1], j)
+
+        def dzs(m, js):
+            for j in js:
+                make_dz(units[m][0], units[m][1], j)
+
+        def pre_pair(m, half):
+            load_pre(units[m][0], units[m][1], 2 * half, 2)
+
+        def w2_pair(q):
+            load_w2(q, 0)
+            load_w2(q, 1)
+
+        def flips_w2(q, ring):
+            flip_w2(q, 0, ring)
+            flip_w2(q, 1, ring)
+
+        def takes_w2(q):
+            take_w2(q, 0, "s")
+            take_w2(q, 1, "s")
+
+        def flips_dz(m, ring):
+            for h in range(2):
+                flip_dz(units[m][0], units[m][1], h, ring)
+
+        def takes_dz(m, engines="ss"):
+            for h in range(2):
+                take_dz(units[m][0], units[m][1], h, engines[h])
+
+        def pool_t(m):
+            group_t(units[m][0], units[m][1], 0, 2, "g", "pool")
+            group_t(units[m][0], units[m][1], 2, 3, "g", "pool")
+
+        def rest_t(m):
+            group_t(units[m][0], units[m][1], 3, 4, "s", "pool")
+
+        def own_t(m, engines="vv"):
+            group_t(units[m][0], units[m][1], 0, 2, engines[0], "rows")
+            group_t(units[m][0], units[m][1], 2, 4, engines[1], "rows")
+
+        def q_t(m):
+            quantise(("t",) + units[m])
+
+        def q_h(m):
+            quantise(("h",) + units[m])
+
+        def dw(q, ms, ring=SUM_BANKS, engines="ssss", single=False):
+            for m in ms:
+                dw_passes(q, m, range(2), ring)
+                leave_dw(q, m, engines[m], single)
+
+        w2_pair(0)
+        load_g(0, 0)
+        load_pre(0, 0, 0, 1)
+        load_g(0, 1)
+        load_pre(0, 0, 1, 1)
+        load_g(1, 0)
+        load_g(1, 1)
+        load_pre(0, 0, 2, 1)
+        load_pre(0, 0, 3, 1)
+        pre_pair(1, 0)
+        w2_pair(1)
+        pre_pair(1, 1)
+        load_rows("x", 0)
+        pre_pair(2, 0)
+        pre_pair(2, 1)
+
+        flips_w2(0, EARLY)
+        flip_g_tile(0, 0, EARLY)
+        flip_g_tile(0, 1, EARLY)
+        take_w2(0, 0, "s")
+        flip_g(0, 1, EARLY)
+        quantise(("w2", 0), 0, 256)
+        take_w2(0, 1, "v")
+        take_g_tile(0, 0, "s")
+        take_g_tile(0, 1, "s")
+        quantise(("w2", 0), 256, 512)
+        quantise(("g", 0), 0, 128)
+        dh(0, [0])
+        quantise(("g", 0), 128, 256)
+        dh(0, [1])
+        take_g(0, 1, "s")
+        load_rows("x", 1)
+        pre_pair(3, 0)
+        w2_pair(2)
+        pre_pair(3, 1)
+        load_rows("w1", 0)
+        pre_pair(4, 0)
+        quantise(("g", 0), 256, 512)
+        dh(0, [2, 3])
+        flip_g(1, 0, EARLY)
+        flip_g(1, 1, EARLY)
+        take_g(1, 0, "s")
+        take_g(1, 1, "s")
+        dzs(0, [0, 1, 2])
+        quantise(("g", 1), 0, 256)
+        dh(1, [0, 1])
+        quantise(("g", 1), 256, 512)
+        dzs(0, [3])
+        dh(1, [2, 3])
+        flips_w2(1, EARLY)
+        flips_dz(0, EARLY)
+        pool_t(0)
+        rest_t(0)
+        takes_w2(1)
+        takes_dz(0)
+        w2_pair(3)
+        pre_pair(4, 1)
+        dzs(1, J)
+        load_rows("w1", 1)
+        load_rows("w1", 2)
+        pre_pair(5, 0)
+        pre_pair(5, 1)
+        group_rows("x", 0, 0, 512, "s", "rows")
+        quantise(("w2", 1))
+        dh(2, J)
+        q_h(0)
+        q_t(0)
+        pool_t(1)
+        rest_t(1)
+        dzs(2, J)
+        load_rows("w1", 3)
+        pre_pair(6, 0)
+        dh(3, J)
+        flips_dz(2, EARLY)
+        flips_w2(2, EARLY)
+        quantise(("x", 0))
+        group_rows("x", 1, 0, 256, "s", "rows")
+        group_rows("x", 1, 256, 512, "v", "rows")
+        takes_dz(2)
+        quantise(("x", 1))
+        q_t(1)
+        pool_t(2)
+        takes_w2(2)
+        rest_t(2)
+        dw(0, [0, 2, 1, 3])
+        dzs(3, J)
+        pre_pair(6, 1)
+        pre_pair(7, 0)
+        flips_w2(3, FLIP_BANKS)
+        quantise(("w2", 2))
+        dh(4, J)
+        takes_w2(3)
+        q_h(2)
+        q_t(2)
+        pool_t(3)
+        rest_t(3)
+        group_rows("w1", 0, 0, 512, "s", "rows")
+        flips_dz(1, FLIP_BANKS)
+        dzs(4, J)
+        pre_pair(7, 1)
+        quantise(("w2", 3))
+        flips_dz(4, FLIP_BANKS)
+        dh(5, J)
+        group_rows("w1", 1, 0, 512, "v", "rows")
+        takes_dz(1)
+        takes_dz(4)
+        quantise(("w1", 0))
+        quantise(("w1", 1))
+        q_t(3)
+        group_rows("w1", 3, 0, 384, "g", "pool")
+        group_rows("w1", 3, 384, 512, "s", "pool")
+        dw(1, [0, 2, 1, 3])
+        dzs(5, J)
+        flips_dz(5, (4, 5))
+        dh(6, J)
+        q_h(4)
+        for j in range(2):
+            dx_passes(0, j, range(2), (6, 7))
+        group_rows("w1", 2, 0, 512, "v", "rows")
+        takes_dz(5)
+        q_h(1)
+        quantise(("w1", 2))
+        for j in range(2):
+            dx_passes(0, j, [2])
+        flips_dz(3, (4, 5))
+        q_h(5)
+        quantise(("w1", 3))
+        pool_t(4)
+        takes_dz(3)
+        rest_t(4)
+        for j in range(2):
+            dx_passes(0, j, [3])
+            leave_dx(0, j, "s")
+        for j in range(2, 4):
+            dx_passes(0, j, range(4), (4, 5))
+        dzs(6, J)
+        flips_dz(6, (6, 7))
+        for j in range(2, 4):
+            leave_dx(0, j, "s")
+        dh(7, J)
+        own_t(6, "vv")
+        takes_dz(6)
+        q_h(3)
+        q_t(6)
+        q_h(6)
+        q_t(4)
+        pool_t(5)
+        rest_t(5)
+        dw(2, [0, 2, 1, 3], (4, 5, 6, 7))
+        dzs(7, [0, 1])
+        for j in range(2):
+            dx_passes(1, j, range(3), DH_BANKS)
+        flip_dz(3, 1, 0, (4, 5))
+        dzs(7, [2, 3])
+        take_dz(3, 1, 0, "s")
+        dx_passes(1, 2, range(3), DH_BANKS)
+        flip_dz(3, 1, 1, (4, 5))
+        group_t(3, 1, 0, 2, "v", "rows")
+        take_dz(3, 1, 1, "s")
+        q_t(5)
+        quantise(("h", 3, 1), 0, 256)
+        dx_passes(1, 3, range(3), DH_BANKS)
+        for j in range(2):
+            dx_passes(1, j, [3])
+            leave_dx(1, j, "s", True)
+        quantise(("t", 3, 1), 0, 256)
+        group_t(3, 1, 2, 4, "v", "rows")
+        quantise(("h", 3, 1), 256, 512)
+        dw(3, [0, 1], (6, 7), "ss", True)
+        quantise(("t", 3, 1), 256, 512)
+        for j in range(2, 4):
+            dx_passes(1, j, [3])
+            leave_dx(1, j, "v", True)
+        dw(3, [2, 3], (4, 5), "  sv", True)

@@ -7,6 +7,7 @@ BATCH, SEQ, DIM, HIDDEN = 2, 512, 512, 2048
 P = 128
 PACK = 4
 PASS = P * PACK
+HALF = HIDDEN // 2
 FLOPS = 3 * 2 * BATCH * SEQ * DIM * HIDDEN
 
 F32 = mybir.dt.float32
@@ -22,9 +23,9 @@ DH_BANKS = (0, 1, 2, 3)
 FLIP_BANKS = (4, 5, 6, 7)
 SUM_BANKS = FLIP_BANKS
 SLABS = 8
-PRE_BUFS = {1: 4, 2: 10}
-DZ_BUFS = 6
-GROUP_BUFS = {"words": 4, "rows": 2, "pool": 1}
+PRE_BUFS = 14
+DZ_BUFS = 5
+GROUP_BUFS = {"words": 5, "rows": 4, "pool": 1}
 
 
 def tile_mlp_v_kernel(tc, x, w1, w2, pre, grad_out, out_0, out_1):
@@ -37,6 +38,8 @@ def tile_mlp_v_kernel(tc, x, w1, w2, pre, grad_out, out_0, out_1):
 
         ident = keep.tile([P, P], F32, name="ident")
         make_identity(nc, ident[:])
+        ident16 = keep.tile([P, P], BF16, name="ident16")
+        make_identity(nc, ident16[:])
 
         raw = {}
         grouped = {}
@@ -45,6 +48,7 @@ def tile_mlp_v_kernel(tc, x, w1, w2, pre, grad_out, out_0, out_1):
         codes = {}
         staged = {}
         turns = {}
+        passes = {}
 
         def bank(ring, key):
             n = turns.get(ring, 0)
@@ -60,25 +64,24 @@ def tile_mlp_v_kernel(tc, x, w1, w2, pre, grad_out, out_0, out_1):
             src = grad_out[b].rearrange("(p j) d -> p j d", j=4)
             nc.sync.dma_start(out=raw["g", b, half][:], in_=src[:, 2 * half : 2 * half + 2, :])
 
-        def load_w2(q, u):
-            raw["w2", q, u] = stream.tile([P, 2, DIM], BF16, name="w2_raw", bufs=4)
-            src = w2[PASS * q : PASS * q + PASS, :].rearrange("(p t) d -> p t d", t=4)
-            nc.sync.dma_start(out=raw["w2", q, u][:], in_=src[:, 2 * u : 2 * u + 2, :])
+        def load_w2(c, u, s):
+            raw["w2", c, u, s] = stream.tile([P, 2, DIM], BF16, name="w2_raw", bufs=4)
+            rows = w2[HALF * c + PASS * s : HALF * c + PASS * s + PASS, :]
+            src = rows.rearrange("(p u e) d -> p u e d", u=2, e=2)
+            nc.sync.dma_start(out=raw["w2", c, u, s][:], in_=src[:, u, :, :])
 
         def load_rows(what, i):
             if what == "x":
                 raw[what, i] = slab(BF16, [4, DIM])
             else:
-                raw[what, i] = stream.tile([P, 4, DIM], BF16, name="pre_rows2", bufs=PRE_BUFS[2])
+                raw[what, i] = stream.tile([P, 4, DIM], BF16, name="pre_rows", bufs=PRE_BUFS)
             rows = x[i] if what == "x" else w1[PASS * i : PASS * i + PASS, :]
             nc.sync.dma_start(out=raw[what, i][:], in_=rows.rearrange("(p t) d -> p t d", t=4))
 
-        def load_pre(q, b, j, n):
-            tile = stream.tile([P, n, PASS], F32, name="pre_rows%d" % n, bufs=PRE_BUFS[n])
+        def load_pre(b, c, j):
+            raw["pre", b, c, j] = stream.tile([P, HALF], F32, name="pre_rows", bufs=PRE_BUFS)
             src = pre[b].rearrange("(p j) h -> p j h", j=4)
-            nc.sync.dma_start(out=tile[:], in_=src[:, j : j + n, PASS * q : PASS * q + PASS])
-            for i in range(n):
-                raw["pre", q, b, j + i] = tile[:, i, :]
+            nc.sync.dma_start(out=raw["pre", b, c, j][:], in_=src[:, j, HALF * c : HALF * c + HALF])
 
         def copy_words(engine, out, in_):
             if engine == "s":
@@ -142,7 +145,7 @@ def tile_mlp_v_kernel(tc, x, w1, w2, pre, grad_out, out_0, out_1):
                 in_=banks["g", b, half][:].rearrange("k (j v n) -> k j n v", j=2, v=2),
             )
 
-        def flip_g_tile(b, j, ring):
+        def flip_g_tile(b, j, ring=FLIP_BANKS):
             words = raw["g", b, j // 2][:].bitcast(F32)
             dst = bank(ring, ("g1", b, j))
             for v in range(2):
@@ -156,16 +159,16 @@ def tile_mlp_v_kernel(tc, x, w1, w2, pre, grad_out, out_0, out_1):
                 in_=banks["g1", b, j][:, : 2 * P].rearrange("k (v n) -> k n v", v=2),
             )
 
-        def flip_w2(q, u, ring=FLIP_BANKS):
-            words = raw["w2", q, u][:].bitcast(F32)
-            transposes(("w2", q, u), [words[:, i // 2, i % 2 :: 2] for i in range(4)], ring)
+        def flip_w2(c, u, s, ring=FLIP_BANKS):
+            words = raw["w2", c, u, s][:].bitcast(F32)
+            transposes(("w2", c, u, s), [words[:, i // 2, i % 2 :: 2] for i in range(4)], ring)
 
-        def take_w2(q, u, engine):
-            dst = group_tile(("w2", q), "words")[:].bitcast(F32)[:, PASS * u : PASS * u + PASS]
+        def take_w2(c, u, s, engine):
+            dst = group_tile(("w2", c, u), "words")[:].bitcast(F32)[:, PASS * s : PASS * s + PASS]
             copy_words(
                 engine,
                 out=dst.rearrange("k (n i) -> k n i", i=4),
-                in_=banks["w2", q, u][:].rearrange("k (i n) -> k n i", i=4),
+                in_=banks["w2", c, u, s][:].rearrange("k (i n) -> k n i", i=4),
             )
 
         def group_rows(what, i, lo, hi, engine, name):
@@ -176,53 +179,72 @@ def tile_mlp_v_kernel(tc, x, w1, w2, pre, grad_out, out_0, out_1):
                 in_=raw[what, i][:, :, lo:hi].rearrange("p t (c i) -> p c t i", i=4),
             )
 
-        def make_dh(q, b, j):
-            multiply(bank(DH_BANKS, ("dh", q, b, j))[:], ("g", b), j, ("w2", q), True, True)
-
-        def make_dz(q, b, j):
-            if (q, b) not in dz:
-                dz[q, b] = stream.tile([P, 4, PASS], BF16, name="dz", bufs=DZ_BUFS, align_bytes=64)
-            rows = raw["pre", q, b, j].rearrange("p (n u e) -> p n u e", u=2, e=2)
-            for u in range(2):
-                cols = slice(2 * P * u, 2 * P * u + 2 * P)
-                nc.vector.scalar_tensor_tensor(
-                    out=dz[q, b][:, j, cols].rearrange("p (n e) -> p n e", e=2),
-                    in0=rows[:, :, u, :],
-                    scalar=0.0,
-                    in1=banks["dh", q, b, j][:, cols].rearrange("p (n e) -> p n e", e=2),
-                    op0=MAX,
-                    op1=MULT,
+        def weave(what, i, half, ring=FLIP_BANKS):
+            dst = bank(ring, (what, i, half))[:].bitcast(BF16)
+            for k in range(2):
+                lo = 2 * P * half + P * k
+                nc.tensor.matmul(
+                    out=dst[:, PASS * k : PASS * k + PASS],
+                    lhsT=ident16[:],
+                    rhs=raw[what, i][:, :, lo : lo + P].rearrange("p t d -> p d t"),
+                    start=True,
+                    stop=True,
                 )
 
-        def flip_dz(q, b, half, ring=FLIP_BANKS):
-            words = dz[q, b][:].bitcast(F32)
-            transposes(("h", q, b, half), [words[:, 2 * half + i // 2, P * (i % 2) : P * (i % 2) + P] for i in range(4)], ring)
+        def take_rows(what, i, half, engine):
+            dst = group_tile((what, i), "rows")[:].bitcast(F32)[:, PASS * half : PASS * half + PASS]
+            copy_words(engine, out=dst, in_=banks[what, i, half][:])
 
-        def take_dz(q, b, half, engine, name="words"):
-            dst = group_tile(("h", q, b), name)[:].bitcast(F32)[:, PASS * half : PASS * half + PASS]
-            copy_words(
-                engine,
-                out=dst.rearrange("k (j n u) -> k j n u", j=2, u=2),
-                in_=banks["h", q, b, half][:].rearrange("k (j u n) -> k j n u", j=2, u=2),
+        def make_dh(b, c, u, j):
+            multiply(bank(DH_BANKS, ("dh", b, c, u, j))[:], ("g", b), j, ("w2", c, u), True, True)
+
+        def make_dz(b, c, u, j):
+            if (b, c, u) not in dz:
+                dz[b, c, u] = stream.tile([P, 4, PASS], BF16, name="dz", bufs=DZ_BUFS, align_bytes=64)
+            rows = raw["pre", b, c, j][:].rearrange("p (n u e) -> p n u e", u=2, e=2)
+            nc.vector.scalar_tensor_tensor(
+                out=dz[b, c, u][:, j, :].rearrange("p (n e) -> p n e", e=2),
+                in0=rows[:, :, u, :],
+                scalar=0.0,
+                in1=banks["dh", b, c, u, j][:].rearrange("p (n e) -> p n e", e=2),
+                op0=MAX,
+                op1=MULT,
             )
 
-        def group_t(q, b, m0, m1, engine, name):
-            dst = group_tile(("t", q, b), name)
-            src = dz[q, b][:].rearrange("p t (c i e) -> p e c t i", i=4, e=2)[:, m0 // 2, :, :, :]
+        def flip_dz(b, c, j, ring=FLIP_BANKS):
+            words = [dz[b, c, u][:, j, :].bitcast(F32) for u in range(2)]
+            transposes(("h", b, c, j), [words[i % 2][:, P * (i // 2) : P * (i // 2) + P] for i in range(4)], ring)
+
+        def take_dz(b, c, j, engine, name="words"):
+            dst = group_tile(("h", b, c, j // 2), name)[:].bitcast(F32)[:, PASS * (j % 2) : PASS * (j % 2) + PASS]
+            copy_words(
+                engine,
+                out=dst.rearrange("k (s n u) -> k s n u", s=2, u=2),
+                in_=banks["h", b, c, j][:].rearrange("k (s u n) -> k s n u", s=2, u=2),
+            )
+
+        def group_t(b, c, u, m0, m1, engine, name):
+            dst = group_tile(("t", b, c, u), name)
+            src = dz[b, c, u][:].rearrange("p t (c i e) -> p e c t i", i=4, e=2)[:, m0 // 2, :, :, :]
             runs = slice(P // 4 * (m0 % 2), P // 4 * (m0 % 2 + m1 - m0))
             interleave(engine, out=dst[:, PACK * P * m0 : PACK * P * m1], in_=src[:, runs, :, :])
 
+        def open_sum(ring, key):
+            n = passes.get(key, 0)
+            passes[key] = n + 1
+            if n == 0:
+                bank(ring, key)
+            return n
+
         def dx_passes(b, j, qs, ring=SUM_BANKS):
             for q in qs:
-                if q == 0:
-                    bank(ring, ("dx", b, j))
-                multiply(banks["dx", b, j][:], ("h", q, b), j, ("w1", q), q == 0, q == 3)
+                n = open_sum(ring, ("dx", b, j))
+                multiply(banks["dx", b, j][:], ("h", b, q // 2, j // 2), 2 * (j % 2) + q % 2, ("w1", q), n == 0, n == 3)
 
-        def dw_passes(q, m, bs, ring=SUM_BANKS):
+        def dw_passes(c, u, m, bs, ring=SUM_BANKS):
             for b in bs:
-                if b == 0:
-                    bank(ring, ("dw", q, m))
-                multiply(banks["dw", q, m][:], ("t", q, b), m, ("x", b), b == 0, b == 1)
+                n = open_sum(ring, ("dw", c, u, m))
+                multiply(banks["dw", c, u, m][:], ("t", b, c, u), m, ("x", b), n == 0, n == 1)
 
         def scale_out(engine, out, in_):
             if engine == "s":
@@ -245,239 +267,254 @@ def tile_mlp_v_kernel(tc, x, w1, w2, pre, grad_out, out_0, out_1):
             rows = out_0[b].rearrange("(p j) d -> p j d", j=4)[:, j - j % 2 : j - j % 2 + 2, :]
             leave(("dx", b, j // 2), j % 2, banks["dx", b, j], rows, engine, single)
 
-        def leave_dw(q, m, engine, single=False):
-            e, u = m // 2, m % 2
-            rows = out_1[PASS * q : PASS * q + PASS, :].rearrange("(p f) d -> p f d", f=4)[:, 2 * u : 2 * u + 2, :]
-            leave(("dw", q, u), e, banks["dw", q, m], rows, engine, single)
+        def leave_dw(c, u, m, engine, single=False):
+            e, s = m // 2, m % 2
+            first = HALF * c + PASS * s
+            rows = out_1[first : first + PASS, :].rearrange("(p f) d -> p f d", f=4)[:, 2 * u : 2 * u + 2, :]
+            leave(("dw", c, u, s), e, banks["dw", c, u, m], rows, engine, single)
 
-        units = [(0, 0), (0, 1), (1, 0), (1, 1), (2, 0), (3, 0), (2, 1), (3, 1)]
-        EARLY = FLIP_BANKS
+        units = [(b, c, u) for c in range(2) for b in range(2) for u in range(2)]
         J = range(4)
 
         def dh(m, js):
             for j in js:
-                make_dh(units[m][0], units[m][1], j)
+                make_dh(*units[m], j)
 
         def dzs(m, js):
             for j in js:
-                make_dz(units[m][0], units[m][1], j)
+                make_dz(*units[m], j)
 
-        def pre_pair(m, half):
-            load_pre(units[m][0], units[m][1], 2 * half, 2)
+        def pres(b, c, js):
+            for j in js:
+                load_pre(b, c, j)
 
-        def w2_pair(q):
-            load_w2(q, 0)
-            load_w2(q, 1)
+        def w2_pair(c, u):
+            load_w2(c, u, 0)
+            load_w2(c, u, 1)
 
-        def flips_w2(q, ring):
-            flip_w2(q, 0, ring)
-            flip_w2(q, 1, ring)
+        def flips_w2(c, u, ring=FLIP_BANKS):
+            flip_w2(c, u, 0, ring)
+            flip_w2(c, u, 1, ring)
 
-        def takes_w2(q):
-            take_w2(q, 0, "s")
-            take_w2(q, 1, "s")
+        def takes_w2(c, u, engines="ss"):
+            take_w2(c, u, 0, engines[0])
+            take_w2(c, u, 1, engines[1])
 
-        def flips_dz(m, ring):
-            for h in range(2):
-                flip_dz(units[m][0], units[m][1], h, ring)
+        def flips_dz(b, c, js, ring=FLIP_BANKS):
+            for j in js:
+                flip_dz(b, c, j, ring)
 
-        def takes_dz(m, engines="ss"):
-            for h in range(2):
-                take_dz(units[m][0], units[m][1], h, engines[h])
+        def takes_dz(b, c, js, engine="s"):
+            for j in js:
+                take_dz(b, c, j, engine)
 
         def pool_t(m):
-            group_t(units[m][0], units[m][1], 0, 2, "g", "pool")
-            group_t(units[m][0], units[m][1], 2, 3, "g", "pool")
+            group_t(*units[m], 0, 2, "g", "pool")
+            group_t(*units[m], 2, 3, "g", "pool")
 
         def rest_t(m):
-            group_t(units[m][0], units[m][1], 3, 4, "s", "pool")
+            group_t(*units[m], 3, 4, "s", "pool")
 
         def own_t(m, engines="vv"):
-            group_t(units[m][0], units[m][1], 0, 2, engines[0], "rows")
-            group_t(units[m][0], units[m][1], 2, 4, engines[1], "rows")
+            group_t(*units[m], 0, 2, engines[0], "rows")
+            group_t(*units[m], 2, 4, engines[1], "rows")
+
+        def pool_rows(what, i):
+            group_rows(what, i, 0, 384, "g", "pool")
+
+        def rest_rows(what, i):
+            group_rows(what, i, 384, 512, "s", "pool")
 
         def q_t(m):
             quantise(("t",) + units[m])
 
-        def q_h(m):
-            quantise(("h",) + units[m])
+        def q_h(b, c, half):
+            quantise(("h", b, c, half))
 
-        def dw(q, ms, ring=SUM_BANKS, engines="ssss", single=False):
+        def dw(c, u, ms, ring=SUM_BANKS, engines="ssss", single=False):
             for m in ms:
-                dw_passes(q, m, range(2), ring)
-                leave_dw(q, m, engines[m], single)
+                dw_passes(c, u, m, range(2), ring)
+                leave_dw(c, u, m, engines[m], single)
 
-        w2_pair(0)
+        w2_pair(0, 0)
         load_g(0, 0)
-        load_pre(0, 0, 0, 1)
+        pres(0, 0, [0])
         load_g(0, 1)
-        load_pre(0, 0, 1, 1)
+        pres(0, 0, [1])
+        w2_pair(0, 1)
+        pres(0, 0, [2, 3])
         load_g(1, 0)
         load_g(1, 1)
-        load_pre(0, 0, 2, 1)
-        load_pre(0, 0, 3, 1)
-        pre_pair(1, 0)
-        w2_pair(1)
-        pre_pair(1, 1)
         load_rows("x", 0)
-        pre_pair(2, 0)
-        pre_pair(2, 1)
+        pres(1, 0, [0])
+        load_rows("x", 1)
+        pres(1, 0, [1, 2, 3])
 
-        flips_w2(0, EARLY)
-        flip_g_tile(0, 0, EARLY)
-        flip_g_tile(0, 1, EARLY)
-        take_w2(0, 0, "s")
-        flip_g(0, 1, EARLY)
-        quantise(("w2", 0), 0, 256)
-        take_w2(0, 1, "v")
+        flips_w2(0, 0)
+        flip_g_tile(0, 0)
+        flip_g_tile(0, 1)
+        take_w2(0, 0, 0, "s")
+        take_w2(0, 0, 1, "v")
+        flip_g(0, 1)
         take_g_tile(0, 0, "s")
         take_g_tile(0, 1, "s")
-        quantise(("w2", 0), 256, 512)
+        quantise(("w2", 0, 0), 0, 256)
+        quantise(("w2", 0, 0), 256, 512)
         quantise(("g", 0), 0, 128)
         dh(0, [0])
         quantise(("g", 0), 128, 256)
         dh(0, [1])
         take_g(0, 1, "s")
-        load_rows("x", 1)
-        pre_pair(3, 0)
-        w2_pair(2)
-        pre_pair(3, 1)
-        load_rows("w1", 0)
-        pre_pair(4, 0)
+        dzs(0, [0])
+        w2_pair(1, 0)
         quantise(("g", 0), 256, 512)
         dh(0, [2, 3])
-        flip_g(1, 0, EARLY)
-        flip_g(1, 1, EARLY)
+        flips_w2(0, 1)
+        w2_pair(1, 1)
+        load_rows("w1", 0)
+        pres(0, 1, [0, 1])
+        load_rows("w1", 1)
+        pres(0, 1, [2, 3])
+        flip_g(1, 0)
+        dzs(0, [1])
+        take_w2(0, 1, 0, "s")
+        dzs(0, [2])
+        take_w2(0, 1, 1, "s")
         take_g(1, 0, "s")
-        take_g(1, 1, "s")
-        dzs(0, [0, 1, 2])
-        quantise(("g", 1), 0, 256)
-        dh(1, [0, 1])
-        quantise(("g", 1), 256, 512)
+        quantise(("w2", 0, 1))
+        dh(1, [0, 1, 2])
         dzs(0, [3])
-        dh(1, [2, 3])
-        flips_w2(1, EARLY)
-        flips_dz(0, EARLY)
+        dh(1, [3])
+        flip_g(1, 1)
         pool_t(0)
         rest_t(0)
-        takes_w2(1)
-        takes_dz(0)
-        w2_pair(3)
-        pre_pair(4, 1)
+        take_g(1, 1, "s")
+        weave("x", 0, 0)
+        weave("x", 0, 1)
+        take_rows("x", 0, 0, "s")
+        take_rows("x", 0, 1, "s")
         dzs(1, J)
-        load_rows("w1", 1)
+        load_rows("w1", 3)
         load_rows("w1", 2)
-        pre_pair(5, 0)
-        pre_pair(5, 1)
-        group_rows("x", 0, 0, 512, "s", "rows")
-        quantise(("w2", 1))
+        pres(1, 1, [0, 1])
+        quantise(("g", 1))
+        weave("x", 1, 0)
+        weave("x", 1, 1)
         dh(2, J)
-        q_h(0)
+        quantise(("x", 0))
+        take_rows("x", 1, 0, "s")
+        take_rows("x", 1, 1, "s")
+        flips_dz(0, 0, J)
         q_t(0)
         pool_t(1)
         rest_t(1)
-        dzs(2, J)
-        load_rows("w1", 3)
-        pre_pair(6, 0)
+        takes_dz(0, 0, J)
+        dzs(2, [0])
+        pres(1, 1, [2])
+        dzs(2, [1])
+        pres(1, 1, [3])
+        dzs(2, [2, 3])
         dh(3, J)
-        flips_dz(2, EARLY)
-        flips_w2(2, EARLY)
-        quantise(("x", 0))
-        group_rows("x", 1, 0, 256, "s", "rows")
-        group_rows("x", 1, 256, 512, "v", "rows")
-        takes_dz(2)
+        flips_w2(1, 0)
+        own_t(2, "vs")
         quantise(("x", 1))
-        q_t(1)
-        pool_t(2)
-        takes_w2(2)
-        rest_t(2)
-        dw(0, [0, 2, 1, 3])
-        dzs(3, J)
-        pre_pair(6, 1)
-        pre_pair(7, 0)
-        flips_w2(3, FLIP_BANKS)
-        quantise(("w2", 2))
-        dh(4, J)
-        takes_w2(3)
-        q_h(2)
+        takes_w2(1, 0)
         q_t(2)
-        pool_t(3)
-        rest_t(3)
-        group_rows("w1", 0, 0, 512, "s", "rows")
-        flips_dz(1, FLIP_BANKS)
-        dzs(4, J)
-        pre_pair(7, 1)
-        quantise(("w2", 3))
-        flips_dz(4, FLIP_BANKS)
-        dh(5, J)
-        group_rows("w1", 1, 0, 512, "v", "rows")
-        takes_dz(1)
-        takes_dz(4)
-        quantise(("w1", 0))
-        quantise(("w1", 1))
+        quantise(("w2", 1, 0))
+        flips_w2(1, 1)
+        q_t(1)
+        pool_rows("w1", 0)
+        takes_w2(1, 1)
+        rest_rows("w1", 0)
+        dw(0, 0, [0, 2, 1], (4, 5, 6, 7))
+        dzs(3, J)
+        group_t(*units[3], 2, 4, "s", "rows")
+        dw(0, 0, [3], (4, 5, 6, 7))
+        dh(4, J)
+        flips_dz(1, 0, [0, 1], (4, 5, 6, 7))
+        group_t(*units[3], 0, 2, "v", "rows")
+        q_h(0, 0, 0)
+        takes_dz(1, 0, [0, 1])
+        flips_dz(1, 0, [2, 3], (4, 5, 6, 7))
+        quantise(("w2", 1, 1))
         q_t(3)
-        group_rows("w1", 3, 0, 384, "g", "pool")
-        group_rows("w1", 3, 384, 512, "s", "pool")
-        dw(1, [0, 2, 1, 3])
-        dzs(5, J)
-        flips_dz(5, (4, 5))
+        q_h(0, 0, 1)
+        quantise(("w1", 0))
+        pool_rows("w1", 1)
+        takes_dz(1, 0, [2, 3])
+        rest_rows("w1", 1)
+        dw(0, 1, [0, 2, 1, 3], (4, 5, 6, 7))
+        dzs(4, J)
+        dh(5, J)
+        group_rows("w1", 3, 0, 256, "s", "rows")
+        for j in range(4):
+            dx_passes(0, j, [0], (4, 5, 6, 7))
+        group_rows("w1", 3, 256, 512, "v", "rows")
+        quantise(("w1", 1))
+        pool_rows("w1", 2)
+        rest_rows("w1", 2)
+        group_t(*units[4], 0, 2, "s", "rows")
+        for j in range(4):
+            dx_passes(0, j, [1])
+        dzs(5, [0, 1])
+        flips_dz(0, 1, [0, 1], DH_BANKS)
+        takes_dz(0, 1, [0, 1])
+        dzs(5, [2, 3])
+        flips_dz(0, 1, [2, 3], DH_BANKS)
+        takes_dz(0, 1, [2, 3])
         dh(6, J)
-        q_h(4)
-        for j in range(2):
-            dx_passes(0, j, range(2), (6, 7))
-        group_rows("w1", 2, 0, 512, "v", "rows")
-        takes_dz(5)
-        q_h(1)
-        quantise(("w1", 2))
-        for j in range(2):
-            dx_passes(0, j, [2])
-        flips_dz(3, (4, 5))
-        q_h(5)
         quantise(("w1", 3))
-        pool_t(4)
-        takes_dz(3)
-        rest_t(4)
-        for j in range(2):
-            dx_passes(0, j, [3])
-            leave_dx(0, j, "s")
-        for j in range(2, 4):
-            dx_passes(0, j, range(4), (4, 5))
-        dzs(6, J)
-        flips_dz(6, (6, 7))
-        for j in range(2, 4):
-            leave_dx(0, j, "s")
-        dh(7, J)
-        own_t(6, "vv")
-        takes_dz(6)
-        q_h(3)
-        q_t(6)
-        q_h(6)
-        q_t(4)
+        q_h(0, 1, 0)
+        q_h(1, 0, 0)
+        q_h(0, 1, 1)
+        quantise(("w1", 2))
         pool_t(5)
-        rest_t(5)
-        dw(2, [0, 2, 1, 3], (4, 5, 6, 7))
-        dzs(7, [0, 1])
+        group_t(*units[4], 2, 4, "s", "rows")
+        for j in range(4):
+            dx_passes(0, j, [3])
+        for j in range(4):
+            dx_passes(0, j, [2])
+            leave_dx(0, j, "s")
         for j in range(2):
-            dx_passes(1, j, range(3), DH_BANKS)
-        flip_dz(3, 1, 0, (4, 5))
-        dzs(7, [2, 3])
-        take_dz(3, 1, 0, "s")
-        dx_passes(1, 2, range(3), DH_BANKS)
-        flip_dz(3, 1, 1, (4, 5))
-        group_t(3, 1, 0, 2, "v", "rows")
-        take_dz(3, 1, 1, "s")
-        q_t(5)
-        quantise(("h", 3, 1), 0, 256)
-        dx_passes(1, 3, range(3), DH_BANKS)
-        for j in range(2):
-            dx_passes(1, j, [3])
-            leave_dx(1, j, "s", True)
-        quantise(("t", 3, 1), 0, 256)
-        group_t(3, 1, 2, 4, "v", "rows")
-        quantise(("h", 3, 1), 256, 512)
-        dw(3, [0, 1], (6, 7), "ss", True)
-        quantise(("t", 3, 1), 256, 512)
+            dx_passes(1, j, range(2), (4, 5, 6, 7))
+        dzs(6, J)
+        q_h(1, 0, 1)
         for j in range(2, 4):
-            dx_passes(1, j, [3])
-            leave_dx(1, j, "v", True)
-        dw(3, [2, 3], (4, 5), "  sv", True)
+            dx_passes(1, j, range(2), (4, 5, 6, 7))
+        own_t(6, "vs")
+        q_t(4)
+        dh(7, [0, 1])
+        q_t(6)
+        rest_t(5)
+        dw(1, 0, [0, 2], DH_BANKS)
+        dzs(7, [0, 1])
+        flips_dz(1, 1, [0, 1], DH_BANKS)
+        q_t(5)
+        dh(7, [2, 3])
+        takes_dz(1, 1, [0, 1])
+        dzs(7, [2, 3])
+        dw(1, 0, [1, 3], DH_BANKS)
+        flips_dz(1, 1, [2, 3], DH_BANKS)
+        q_h(1, 1, 0)
+        group_t(1, 1, 1, 0, 2, "v", "rows")
+        takes_dz(1, 1, [2, 3])
+        for j in range(2):
+            dx_passes(1, j, [2, 3])
+        quantise(("t", 1, 1, 1), 0, 256)
+        group_t(1, 1, 1, 2, 4, "v", "rows")
+        for m in range(2):
+            dw_passes(1, 1, m, [0, 1], DH_BANKS)
+        q_h(1, 1, 1)
+        quantise(("t", 1, 1, 1), 256, 512)
+        leave_dx(1, 0, "s", True)
+        leave_dx(1, 1, "s", True)
+        for j in range(2, 4):
+            dx_passes(1, j, [2, 3])
+        leave_dw(1, 1, 0, "v", True)
+        leave_dw(1, 1, 1, "s", True)
+        for m in range(2, 4):
+            dw_passes(1, 1, m, [0, 1], DH_BANKS)
+        leave_dx(1, 2, "v", True)
+        leave_dx(1, 3, "s", True)
+        leave_dw(1, 1, 2, "v", True)
+        leave_dw(1, 1, 3, "s", True)

@@ -38,8 +38,6 @@ def tile_mlp_v_kernel(tc, x, w1, w2, pre, grad_out, out_0, out_1):
 
         ident = keep.tile([P, P], F32, name="ident")
         make_identity(nc, ident[:])
-        ident16 = keep.tile([P, P], BF16, name="ident16")
-        make_identity(nc, ident16[:])
 
         raw = {}
         grouped = {}
@@ -178,22 +176,6 @@ def tile_mlp_v_kernel(tc, x, w1, w2, pre, grad_out, out_0, out_1):
                 out=dst[:, PACK * lo : PACK * hi],
                 in_=raw[what, i][:, :, lo:hi].rearrange("p t (c i) -> p c t i", i=4),
             )
-
-        def weave(what, i, half, ring=FLIP_BANKS):
-            dst = bank(ring, (what, i, half))[:].bitcast(BF16)
-            for k in range(2):
-                lo = 2 * P * half + P * k
-                nc.tensor.matmul(
-                    out=dst[:, PASS * k : PASS * k + PASS],
-                    lhsT=ident16[:],
-                    rhs=raw[what, i][:, :, lo : lo + P].rearrange("p t d -> p d t"),
-                    start=True,
-                    stop=True,
-                )
-
-        def take_rows(what, i, half, engine):
-            dst = group_tile((what, i), "rows")[:].bitcast(F32)[:, PASS * half : PASS * half + PASS]
-            copy_words(engine, out=dst, in_=banks[what, i, half][:])
 
         def make_dh(b, c, u, j):
             multiply(bank(DH_BANKS, ("dh", b, c, u, j))[:], ("g", b), j, ("w2", c, u), True, True)
@@ -336,29 +318,30 @@ def tile_mlp_v_kernel(tc, x, w1, w2, pre, grad_out, out_0, out_1):
                 dw_passes(c, u, m, range(2), ring)
                 leave_dw(c, u, m, engines[m], single)
 
+        load_rows("x", 0)
+        load_rows("x", 1)
         w2_pair(0, 0)
         load_g(0, 0)
         pres(0, 0, [0])
         load_g(0, 1)
-        pres(0, 0, [1])
         w2_pair(0, 1)
-        pres(0, 0, [2, 3])
+        pres(0, 0, [1, 2, 3])
         load_g(1, 0)
         load_g(1, 1)
-        load_rows("x", 0)
-        pres(1, 0, [0])
-        load_rows("x", 1)
-        pres(1, 0, [1, 2, 3])
+        pres(1, 0, J)
 
+        group_rows("x", 0, 0, 512, "s", "rows")
+        group_rows("x", 1, 0, 512, "v", "rows")
         flips_w2(0, 0)
         flip_g_tile(0, 0)
         flip_g_tile(0, 1)
-        take_w2(0, 0, 0, "s")
-        take_w2(0, 0, 1, "v")
+        takes_w2(0, 0)
         flip_g(0, 1)
         take_g_tile(0, 0, "s")
         take_g_tile(0, 1, "s")
+        quantise(("x", 0))
         quantise(("w2", 0, 0), 0, 256)
+        quantise(("x", 1))
         quantise(("w2", 0, 0), 256, 512)
         quantise(("g", 0), 0, 128)
         dh(0, [0])
@@ -367,57 +350,53 @@ def tile_mlp_v_kernel(tc, x, w1, w2, pre, grad_out, out_0, out_1):
         take_g(0, 1, "s")
         dzs(0, [0])
         w2_pair(1, 0)
+        flips_w2(0, 1)
         quantise(("g", 0), 256, 512)
         dh(0, [2, 3])
-        flips_w2(0, 1)
         w2_pair(1, 1)
         load_rows("w1", 0)
         pres(0, 1, [0, 1])
         load_rows("w1", 1)
         pres(0, 1, [2, 3])
-        flip_g(1, 0)
+        takes_w2(0, 1)
         dzs(0, [1])
-        take_w2(0, 1, 0, "s")
-        dzs(0, [2])
-        take_w2(0, 1, 1, "s")
-        take_g(1, 0, "s")
         quantise(("w2", 0, 1))
-        dh(1, [0, 1, 2])
+        dh(1, [0, 1])
+        dzs(0, [2])
+        dh(1, [2])
+        flip_g(1, 0)
         dzs(0, [3])
         dh(1, [3])
         flip_g(1, 1)
         pool_t(0)
         rest_t(0)
+        take_g(1, 0, "s")
         take_g(1, 1, "s")
-        weave("x", 0, 0)
-        weave("x", 0, 1)
-        take_rows("x", 0, 0, "s")
-        take_rows("x", 0, 1, "s")
         dzs(1, J)
         load_rows("w1", 3)
         load_rows("w1", 2)
         pres(1, 1, [0, 1])
-        quantise(("g", 1))
-        weave("x", 1, 0)
-        weave("x", 1, 1)
-        dh(2, J)
-        quantise(("x", 0))
-        take_rows("x", 1, 0, "s")
-        take_rows("x", 1, 1, "s")
         flips_dz(0, 0, J)
+        quantise(("g", 1), 0, 256)
+        takes_dz(0, 0, [0, 1])
+        dh(2, [0, 1])
+        quantise(("g", 1), 256, 512)
+        dh(2, [2, 3])
         q_t(0)
         pool_t(1)
+        takes_dz(0, 0, [2, 3])
         rest_t(1)
-        takes_dz(0, 0, J)
         dzs(2, [0])
         pres(1, 1, [2])
         dzs(2, [1])
         pres(1, 1, [3])
         dzs(2, [2, 3])
-        dh(3, J)
+        dh(3, [0, 1])
         flips_w2(1, 0)
+        dh(3, [2, 3])
         own_t(2, "vs")
-        quantise(("x", 1))
+        q_h(0, 0, 0)
+        q_h(0, 0, 1)
         takes_w2(1, 0)
         q_t(2)
         quantise(("w2", 1, 0))
@@ -433,12 +412,10 @@ def tile_mlp_v_kernel(tc, x, w1, w2, pre, grad_out, out_0, out_1):
         dh(4, J)
         flips_dz(1, 0, [0, 1], (4, 5, 6, 7))
         group_t(*units[3], 0, 2, "v", "rows")
-        q_h(0, 0, 0)
         takes_dz(1, 0, [0, 1])
         flips_dz(1, 0, [2, 3], (4, 5, 6, 7))
         quantise(("w2", 1, 1))
         q_t(3)
-        q_h(0, 0, 1)
         quantise(("w1", 0))
         pool_rows("w1", 1)
         takes_dz(1, 0, [2, 3])
@@ -446,26 +423,27 @@ def tile_mlp_v_kernel(tc, x, w1, w2, pre, grad_out, out_0, out_1):
         dw(0, 1, [0, 2, 1, 3], (4, 5, 6, 7))
         dzs(4, J)
         dh(5, J)
-        group_rows("w1", 3, 0, 256, "s", "rows")
         for j in range(4):
             dx_passes(0, j, [0], (4, 5, 6, 7))
-        group_rows("w1", 3, 256, 512, "v", "rows")
+        group_rows("w1", 3, 0, 512, "v", "rows")
         quantise(("w1", 1))
         pool_rows("w1", 2)
         rest_rows("w1", 2)
         group_t(*units[4], 0, 2, "s", "rows")
-        for j in range(4):
+        for j in range(2):
             dx_passes(0, j, [1])
         dzs(5, [0, 1])
         flips_dz(0, 1, [0, 1], DH_BANKS)
+        for j in range(2, 4):
+            dx_passes(0, j, [1])
         takes_dz(0, 1, [0, 1])
         dzs(5, [2, 3])
         flips_dz(0, 1, [2, 3], DH_BANKS)
         takes_dz(0, 1, [2, 3])
         dh(6, J)
         quantise(("w1", 3))
-        q_h(0, 1, 0)
         q_h(1, 0, 0)
+        q_h(0, 1, 0)
         q_h(0, 1, 1)
         quantise(("w1", 2))
         pool_t(5)

@@ -26,6 +26,7 @@ SLABS = 8
 PRE_BUFS = 14
 DZ_BUFS = 5
 GROUP_BUFS = {"words": 5, "rows": 4, "pool": 1}
+POOL_SHARE = 384
 
 
 def tile_mlp_v_kernel(tc, x, w1, w2, pre, grad_out, out_0, out_1):
@@ -87,14 +88,18 @@ def tile_mlp_v_kernel(tc, x, w1, w2, pre, grad_out, out_0, out_1):
             else:
                 nc.vector.tensor_copy(out=out, in_=in_)
 
-        def interleave(engine, out, in_):
+        def interleave(engine, out, in_, factor):
             out = out.rearrange("p (c i t) -> p c t i", i=4, t=4)
-            if engine == "s":
+            if engine == "g":
+                nc.gpsimd.tensor_scalar(out=out, in0=in_, scalar1=factor, scalar2=0.0, op0=MULT, op1=ADD)
+            elif engine == "s" and factor == 1.0:
                 nc.scalar.copy(out=out, in_=in_)
-            elif engine == "v":
+            elif engine == "s":
+                nc.scalar.activation(out=out, in_=in_, func=COPY, scale=factor)
+            elif factor == 1.0:
                 nc.vector.tensor_copy(out=out, in_=in_)
             else:
-                nc.gpsimd.tensor_scalar(out=out, in0=in_, scalar1=1.0, scalar2=0.0, op0=MULT, op1=ADD)
+                nc.vector.tensor_scalar(out=out, in0=in_, scalar1=factor, scalar2=None, op0=MULT)
 
         def group_tile(key, name):
             if key not in grouped:
@@ -175,10 +180,11 @@ def tile_mlp_v_kernel(tc, x, w1, w2, pre, grad_out, out_0, out_1):
                 engine,
                 out=dst[:, PACK * lo : PACK * hi],
                 in_=raw[what, i][:, :, lo:hi].rearrange("p t (c i) -> p c t i", i=4),
+                factor=2.0,
             )
 
-        def make_dh(b, c, u, j):
-            multiply(bank(DH_BANKS, ("dh", b, c, u, j))[:], ("g", b), j, ("w2", c, u), True, True)
+        def make_dh(b, c, u, j, ring):
+            multiply(bank(ring, ("dh", b, c, u, j))[:], ("g", b), j, ("w2", c, u), True, True)
 
         def make_dz(b, c, u, j):
             if (b, c, u) not in dz:
@@ -209,7 +215,22 @@ def tile_mlp_v_kernel(tc, x, w1, w2, pre, grad_out, out_0, out_1):
             dst = group_tile(("t", b, c, u), name)
             src = dz[b, c, u][:].rearrange("p t (c i e) -> p e c t i", i=4, e=2)[:, m0 // 2, :, :, :]
             runs = slice(P // 4 * (m0 % 2), P // 4 * (m0 % 2 + m1 - m0))
-            interleave(engine, out=dst[:, PACK * P * m0 : PACK * P * m1], in_=src[:, runs, :, :])
+            interleave(engine, out=dst[:, PACK * P * m0 : PACK * P * m1], in_=src[:, runs, :, :], factor=1.0)
+
+        def group_t_share(b, c, u, lo, hi, engine):
+            dst = group_tile(("t", b, c, u), "pool")[:].rearrange("p (e n t) -> p e n t", e=2, t=4)[:, :, lo:hi, :]
+            src = dz[b, c, u][:].rearrange("p t (n e) -> p e n t", e=2)[:, :, lo:hi, :]
+            if engine == "g":
+                nc.gpsimd.tensor_scalar(out=dst, in0=src, scalar1=1.0, scalar2=0.0, op0=MULT, op1=ADD)
+            else:
+                nc.scalar.copy(
+                    out=dst.rearrange("p e (c i) t -> p e c t i", i=4), in_=src.rearrange("p e (c i) t -> p e c t i", i=4)
+                )
+
+        def pool_rows(what, i, hi):
+            dst = group_tile((what, i), "pool")[:].rearrange("p (n t) -> p n t", t=4)[:, :hi, :]
+            src = raw[what, i][:].rearrange("p t n -> p n t")[:, :hi, :]
+            nc.gpsimd.tensor_scalar(out=dst, in0=src, scalar1=2.0, scalar2=0.0, op0=MULT, op1=ADD)
 
         def open_sum(ring, key):
             n = passes.get(key, 0)
@@ -228,17 +249,11 @@ def tile_mlp_v_kernel(tc, x, w1, w2, pre, grad_out, out_0, out_1):
                 n = open_sum(ring, ("dw", c, u, m))
                 multiply(banks["dw", c, u, m][:], ("t", b, c, u), m, ("x", b), n == 0, n == 1)
 
-        def scale_out(engine, out, in_):
-            if engine == "s":
-                nc.scalar.activation(out=out, in_=in_, func=COPY, scale=2.0)
-            else:
-                nc.vector.tensor_scalar(out=out, in0=in_, scalar1=2.0, scalar2=None, op0=MULT)
-
         def leave(pair, i, src, rows, engine, single):
             if pair not in staged:
                 staged[pair] = [slab(F32, [2, DIM]), 0]
             tile = staged[pair][0]
-            scale_out(engine, tile[:, i, :], src[:])
+            copy_words(engine, tile[:, i, :], src[:])
             staged[pair][1] = staged[pair][1] + 1
             if single:
                 nc.sync.dma_start(out=rows[:, i, :], in_=tile[:, i, :])
@@ -258,9 +273,9 @@ def tile_mlp_v_kernel(tc, x, w1, w2, pre, grad_out, out_0, out_1):
         units = [(b, c, u) for c in range(2) for b in range(2) for u in range(2)]
         J = range(4)
 
-        def dh(m, js):
+        def dh(m, js, ring=DH_BANKS):
             for j in js:
-                make_dh(*units[m], j)
+                make_dh(*units[m], j, ring)
 
         def dzs(m, js):
             for j in js:
@@ -291,21 +306,17 @@ def tile_mlp_v_kernel(tc, x, w1, w2, pre, grad_out, out_0, out_1):
                 take_dz(b, c, j, engine)
 
         def pool_t(m):
-            group_t(*units[m], 0, 2, "g", "pool")
-            group_t(*units[m], 2, 3, "g", "pool")
+            group_t_share(*units[m], 0, POOL_SHARE // 2, "g")
 
         def rest_t(m):
-            group_t(*units[m], 3, 4, "s", "pool")
+            group_t_share(*units[m], POOL_SHARE // 2, 2 * P, "s")
 
         def own_t(m, engines="vv"):
             group_t(*units[m], 0, 2, engines[0], "rows")
             group_t(*units[m], 2, 4, engines[1], "rows")
 
-        def pool_rows(what, i):
-            group_rows(what, i, 0, 384, "g", "pool")
-
         def rest_rows(what, i):
-            group_rows(what, i, 384, 512, "s", "pool")
+            group_rows(what, i, POOL_SHARE, PASS, "s", "pool")
 
         def q_t(m):
             quantise(("t",) + units[m])
@@ -394,30 +405,31 @@ def tile_mlp_v_kernel(tc, x, w1, w2, pre, grad_out, out_0, out_1):
         dh(3, [0, 1])
         flips_w2(1, 0)
         dh(3, [2, 3])
-        own_t(2, "vs")
         q_h(0, 0, 0)
-        q_h(0, 0, 1)
+        own_t(2, "vs")
         takes_w2(1, 0)
         q_t(2)
-        quantise(("w2", 1, 0))
         flips_w2(1, 1)
         q_t(1)
-        pool_rows("w1", 0)
+        pool_rows("w1", 0, POOL_SHARE)
         takes_w2(1, 1)
         rest_rows("w1", 0)
         dw(0, 0, [0, 2, 1], (4, 5, 6, 7))
+        dw_passes(0, 0, 3, range(2), (4, 5, 6, 7))
         dzs(3, J)
         group_t(*units[3], 2, 4, "s", "rows")
-        dw(0, 0, [3], (4, 5, 6, 7))
-        dh(4, J)
+        leave_dw(0, 0, 3, "s")
+        quantise(("w2", 1, 0))
         flips_dz(1, 0, [0, 1], (4, 5, 6, 7))
-        group_t(*units[3], 0, 2, "v", "rows")
-        takes_dz(1, 0, [0, 1])
+        dh(4, J)
         flips_dz(1, 0, [2, 3], (4, 5, 6, 7))
+        group_t(*units[3], 0, 2, "v", "rows")
         quantise(("w2", 1, 1))
+        q_h(0, 0, 1)
+        takes_dz(1, 0, [0, 1])
         q_t(3)
         quantise(("w1", 0))
-        pool_rows("w1", 1)
+        pool_rows("w1", 1, POOL_SHARE)
         takes_dz(1, 0, [2, 3])
         rest_rows("w1", 1)
         dw(0, 1, [0, 2, 1, 3], (4, 5, 6, 7))
@@ -427,7 +439,7 @@ def tile_mlp_v_kernel(tc, x, w1, w2, pre, grad_out, out_0, out_1):
             dx_passes(0, j, [0], (4, 5, 6, 7))
         group_rows("w1", 3, 0, 512, "v", "rows")
         quantise(("w1", 1))
-        pool_rows("w1", 2)
+        pool_rows("w1", 2, POOL_SHARE)
         rest_rows("w1", 2)
         group_t(*units[4], 0, 2, "s", "rows")
         for j in range(2):
@@ -444,6 +456,7 @@ def tile_mlp_v_kernel(tc, x, w1, w2, pre, grad_out, out_0, out_1):
         quantise(("w1", 3))
         q_h(1, 0, 0)
         q_h(0, 1, 0)
+        q_h(1, 0, 1)
         q_h(0, 1, 1)
         quantise(("w1", 2))
         pool_t(5)
@@ -452,27 +465,31 @@ def tile_mlp_v_kernel(tc, x, w1, w2, pre, grad_out, out_0, out_1):
             dx_passes(0, j, [3])
         for j in range(4):
             dx_passes(0, j, [2])
+        for j in range(3):
             leave_dx(0, j, "s")
-        for j in range(2):
             dx_passes(1, j, range(2), (4, 5, 6, 7))
         dzs(6, J)
-        q_h(1, 0, 1)
-        for j in range(2, 4):
-            dx_passes(1, j, range(2), (4, 5, 6, 7))
-        own_t(6, "vs")
         q_t(4)
+        own_t(6, "vs")
+        leave_dx(0, 3, "s")
         dh(7, [0, 1])
+        for m in (0, 2):
+            dw_passes(1, 0, m, [0], DH_BANKS)
+        dx_passes(1, 3, range(2), (4, 5, 6, 7))
         q_t(6)
         rest_t(5)
-        dw(1, 0, [0, 2], DH_BANKS)
+        for m in (0, 2):
+            dw_passes(1, 0, m, [1])
+            leave_dw(1, 0, m, "s")
         dzs(7, [0, 1])
-        flips_dz(1, 1, [0, 1], DH_BANKS)
         q_t(5)
-        dh(7, [2, 3])
-        takes_dz(1, 1, [0, 1])
+        flips_dz(1, 1, [0, 1], DH_BANKS[:2])
+        dh(7, [2, 3], DH_BANKS[2:])
+        takes_dz(1, 1, [0], "v")
+        takes_dz(1, 1, [1])
         dzs(7, [2, 3])
-        dw(1, 0, [1, 3], DH_BANKS)
-        flips_dz(1, 1, [2, 3], DH_BANKS)
+        dw(1, 0, [1, 3], DH_BANKS[:2])
+        flips_dz(1, 1, [2, 3], DH_BANKS[2:])
         q_h(1, 1, 0)
         group_t(1, 1, 1, 0, 2, "v", "rows")
         takes_dz(1, 1, [2, 3])
@@ -481,17 +498,19 @@ def tile_mlp_v_kernel(tc, x, w1, w2, pre, grad_out, out_0, out_1):
         quantise(("t", 1, 1, 1), 0, 256)
         group_t(1, 1, 1, 2, 4, "v", "rows")
         for m in range(2):
-            dw_passes(1, 1, m, [0, 1], DH_BANKS)
+            dw_passes(1, 1, m, [0, 1], DH_BANKS[:2])
         q_h(1, 1, 1)
         quantise(("t", 1, 1, 1), 256, 512)
         leave_dx(1, 0, "s", True)
         leave_dx(1, 1, "s", True)
+        for m in range(2, 4):
+            dw_passes(1, 1, m, [0], DH_BANKS[2:])
         for j in range(2, 4):
             dx_passes(1, j, [2, 3])
         leave_dw(1, 1, 0, "v", True)
         leave_dw(1, 1, 1, "s", True)
         for m in range(2, 4):
-            dw_passes(1, 1, m, [0, 1], DH_BANKS)
+            dw_passes(1, 1, m, [1])
         leave_dx(1, 2, "v", True)
         leave_dx(1, 3, "s", True)
         leave_dw(1, 1, 2, "v", True)

@@ -26,7 +26,7 @@ SLABS = 8
 PRE_BUFS = 14
 DZ_BUFS = 5
 GROUP_BUFS = {"words": 5, "rows": 4, "pool": 1}
-POOL_SHARE = 384
+POOL_SHARE = 320
 
 
 def tile_mlp_v_kernel(tc, x, w1, w2, pre, grad_out, out_0, out_1):

@@ -26,7 +26,7 @@ SLABS = 8
 PRE_BUFS = 14
 DZ_BUFS = 5
 GROUP_BUFS = {"words": 5, "rows": 4, "pool": 1}
-POOL_SHARE = 320
+POOL_SHARE = 352
 
 
 def tile_mlp_v_kernel(tc, x, w1, w2, pre, grad_out, out_0, out_1):
@@ -273,9 +273,9 @@ def tile_mlp_v_kernel(tc, x, w1, w2, pre, grad_out, out_0, out_1):
         units = [(b, c, u) for c in range(2) for b in range(2) for u in range(2)]
         J = range(4)
 
-        def dh(m, js, ring=DH_BANKS):
+        def dh(m, js):
             for j in js:
-                make_dh(*units[m], j, ring)
+                make_dh(*units[m], j, DH_BANKS[j : j + 1])
 
         def dzs(m, js):
             for j in js:
@@ -408,6 +408,7 @@ def tile_mlp_v_kernel(tc, x, w1, w2, pre, grad_out, out_0, out_1):
         q_h(0, 0, 0)
         own_t(2, "vs")
         takes_w2(1, 0)
+        q_h(0, 0, 1)
         q_t(2)
         flips_w2(1, 1)
         q_t(1)
@@ -416,7 +417,7 @@ def tile_mlp_v_kernel(tc, x, w1, w2, pre, grad_out, out_0, out_1):
         rest_rows("w1", 0)
         dw(0, 0, [0, 2, 1], (4, 5, 6, 7))
         dw_passes(0, 0, 3, range(2), (4, 5, 6, 7))
-        dzs(3, J)
+        dzs(3, [3, 0, 1, 2])
         group_t(*units[3], 2, 4, "s", "rows")
         leave_dw(0, 0, 3, "s")
         quantise(("w2", 1, 0))
@@ -425,7 +426,6 @@ def tile_mlp_v_kernel(tc, x, w1, w2, pre, grad_out, out_0, out_1):
         flips_dz(1, 0, [2, 3], (4, 5, 6, 7))
         group_t(*units[3], 0, 2, "v", "rows")
         quantise(("w2", 1, 1))
-        q_h(0, 0, 1)
         takes_dz(1, 0, [0, 1])
         q_t(3)
         quantise(("w1", 0))
@@ -433,58 +433,58 @@ def tile_mlp_v_kernel(tc, x, w1, w2, pre, grad_out, out_0, out_1):
         takes_dz(1, 0, [2, 3])
         rest_rows("w1", 1)
         dw(0, 1, [0, 2, 1, 3], (4, 5, 6, 7))
-        dzs(4, J)
-        dh(5, J)
+        dzs(4, [3, 0, 1, 2])
+        dh(5, [3, 0, 1, 2])
+        group_rows("w1", 3, 0, 256, "s", "rows")
         for j in range(4):
             dx_passes(0, j, [0], (4, 5, 6, 7))
-        group_rows("w1", 3, 0, 512, "v", "rows")
+        group_rows("w1", 3, 256, 512, "v", "rows")
         quantise(("w1", 1))
         pool_rows("w1", 2, POOL_SHARE)
         rest_rows("w1", 2)
-        group_t(*units[4], 0, 2, "s", "rows")
         for j in range(2):
             dx_passes(0, j, [1])
-        dzs(5, [0, 1])
-        flips_dz(0, 1, [0, 1], DH_BANKS)
+        dzs(5, [2, 3])
+        flips_dz(0, 1, [2, 3], DH_BANKS[2:])
         for j in range(2, 4):
             dx_passes(0, j, [1])
-        takes_dz(0, 1, [0, 1])
-        dzs(5, [2, 3])
-        flips_dz(0, 1, [2, 3], DH_BANKS)
         takes_dz(0, 1, [2, 3])
-        dh(6, J)
-        quantise(("w1", 3))
+        dzs(5, [0, 1])
+        flips_dz(0, 1, [0, 1], DH_BANKS[:2])
+        takes_dz(0, 1, [0, 1])
+        dh(6, [2, 3, 0, 1])
         q_h(1, 0, 0)
-        q_h(0, 1, 0)
-        q_h(1, 0, 1)
+        quantise(("w1", 3))
         q_h(0, 1, 1)
+        q_h(1, 0, 1)
+        q_h(0, 1, 0)
         quantise(("w1", 2))
         pool_t(5)
-        group_t(*units[4], 2, 4, "s", "rows")
-        for j in range(4):
+        own_t(4, "ss")
+        for j in (2, 3, 0, 1):
             dx_passes(0, j, [3])
         for j in range(4):
             dx_passes(0, j, [2])
         for j in range(3):
             leave_dx(0, j, "s")
             dx_passes(1, j, range(2), (4, 5, 6, 7))
-        dzs(6, J)
+        dzs(6, [1, 2, 3, 0])
         q_t(4)
         own_t(6, "vs")
         leave_dx(0, 3, "s")
         dh(7, [0, 1])
         for m in (0, 2):
-            dw_passes(1, 0, m, [0], DH_BANKS)
+            dw_passes(1, 0, m, [0], DH_BANKS[2:])
         dx_passes(1, 3, range(2), (4, 5, 6, 7))
         q_t(6)
         rest_t(5)
         for m in (0, 2):
             dw_passes(1, 0, m, [1])
             leave_dw(1, 0, m, "s")
-        dzs(7, [0, 1])
+        dzs(7, [1, 0])
         q_t(5)
         flips_dz(1, 1, [0, 1], DH_BANKS[:2])
-        dh(7, [2, 3], DH_BANKS[2:])
+        dh(7, [2, 3])
         takes_dz(1, 1, [0], "v")
         takes_dz(1, 1, [1])
         dzs(7, [2, 3])
@@ -507,11 +507,11 @@ def tile_mlp_v_kernel(tc, x, w1, w2, pre, grad_out, out_0, out_1):
             dw_passes(1, 1, m, [0], DH_BANKS[2:])
         for j in range(2, 4):
             dx_passes(1, j, [2, 3])
-        leave_dw(1, 1, 0, "v", True)
+        leave_dw(1, 1, 0, "s", True)
         leave_dw(1, 1, 1, "s", True)
         for m in range(2, 4):
             dw_passes(1, 1, m, [1])
-        leave_dx(1, 2, "v", True)
-        leave_dx(1, 3, "s", True)
+        leave_dx(1, 2, "s", True)
+        leave_dx(1, 3, "v", True)
         leave_dw(1, 1, 2, "v", True)
         leave_dw(1, 1, 3, "s", True)

@@ -25,7 +25,7 @@ SUM_BANKS = FLIP_BANKS
 SLABS = 8
 PRE_BUFS = 14
 DZ_BUFS = 5
-GROUP_BUFS = {"words": 5, "rows": 4, "pool": 1}
+GROUP_BUFS = {"words": 4, "rows": 5, "pool": 1}
 POOL_SHARE = 352
 
 
@@ -217,8 +217,8 @@ def tile_mlp_v_kernel(tc, x, w1, w2, pre, grad_out, out_0, out_1):
             runs = slice(P // 4 * (m0 % 2), P // 4 * (m0 % 2 + m1 - m0))
             interleave(engine, out=dst[:, PACK * P * m0 : PACK * P * m1], in_=src[:, runs, :, :], factor=1.0)
 
-        def group_t_share(b, c, u, lo, hi, engine):
-            dst = group_tile(("t", b, c, u), "pool")[:].rearrange("p (e n t) -> p e n t", e=2, t=4)[:, :, lo:hi, :]
+        def group_t_share(b, c, u, lo, hi, engine, name="pool"):
+            dst = group_tile(("t", b, c, u), name)[:].rearrange("p (e n t) -> p e n t", e=2, t=4)[:, :, lo:hi, :]
             src = dz[b, c, u][:].rearrange("p t (n e) -> p e n t", e=2)[:, :, lo:hi, :]
             if engine == "g":
                 nc.gpsimd.tensor_scalar(out=dst, in0=src, scalar1=1.0, scalar2=0.0, op0=MULT, op1=ADD)
@@ -227,8 +227,8 @@ def tile_mlp_v_kernel(tc, x, w1, w2, pre, grad_out, out_0, out_1):
                     out=dst.rearrange("p e (c i) t -> p e c t i", i=4), in_=src.rearrange("p e (c i) t -> p e c t i", i=4)
                 )
 
-        def pool_rows(what, i, hi):
-            dst = group_tile((what, i), "pool")[:].rearrange("p (n t) -> p n t", t=4)[:, :hi, :]
+        def pool_rows(what, i, hi, name="pool"):
+            dst = group_tile((what, i), name)[:].rearrange("p (n t) -> p n t", t=4)[:, :hi, :]
             src = raw[what, i][:].rearrange("p t n -> p n t")[:, :hi, :]
             nc.gpsimd.tensor_scalar(out=dst, in0=src, scalar1=2.0, scalar2=0.0, op0=MULT, op1=ADD)
 
@@ -315,8 +315,8 @@ def tile_mlp_v_kernel(tc, x, w1, w2, pre, grad_out, out_0, out_1):
             group_t(*units[m], 0, 2, engines[0], "rows")
             group_t(*units[m], 2, 4, engines[1], "rows")
 
-        def rest_rows(what, i):
-            group_rows(what, i, POOL_SHARE, PASS, "s", "pool")
+        def rest_rows(what, i, name="pool"):
+            group_rows(what, i, POOL_SHARE, PASS, "s", name)
 
         def q_t(m):
             quantise(("t",) + units[m])
@@ -336,7 +336,9 @@ def tile_mlp_v_kernel(tc, x, w1, w2, pre, grad_out, out_0, out_1):
         pres(0, 0, [0])
         load_g(0, 1)
         w2_pair(0, 1)
-        pres(0, 0, [1, 2, 3])
+        pres(0, 0, [1])
+        load_rows("w1", 3)
+        pres(0, 0, [2, 3])
         load_g(1, 0)
         load_g(1, 1)
         pres(1, 0, J)
@@ -367,10 +369,11 @@ def tile_mlp_v_kernel(tc, x, w1, w2, pre, grad_out, out_0, out_1):
         w2_pair(1, 1)
         load_rows("w1", 0)
         pres(0, 1, [0, 1])
-        load_rows("w1", 1)
+        load_rows("w1", 2)
         pres(0, 1, [2, 3])
         takes_w2(0, 1)
         dzs(0, [1])
+        group_rows("w1", 3, 0, 512, "s", "rows")
         quantise(("w2", 0, 1))
         dh(1, [0, 1])
         dzs(0, [2])
@@ -384,8 +387,7 @@ def tile_mlp_v_kernel(tc, x, w1, w2, pre, grad_out, out_0, out_1):
         take_g(1, 0, "s")
         take_g(1, 1, "s")
         dzs(1, J)
-        load_rows("w1", 3)
-        load_rows("w1", 2)
+        load_rows("w1", 1)
         pres(1, 1, [0, 1])
         flips_dz(0, 0, J)
         quantise(("g", 1), 0, 256)
@@ -429,89 +431,89 @@ def tile_mlp_v_kernel(tc, x, w1, w2, pre, grad_out, out_0, out_1):
         takes_dz(1, 0, [0, 1])
         q_t(3)
         quantise(("w1", 0))
-        pool_rows("w1", 1, POOL_SHARE)
-        takes_dz(1, 0, [2, 3])
-        rest_rows("w1", 1)
-        dw(0, 1, [0, 2, 1, 3], (4, 5, 6, 7))
-        dzs(4, [3, 0, 1, 2])
-        dh(5, [3, 0, 1, 2])
-        group_rows("w1", 3, 0, 256, "s", "rows")
-        for j in range(4):
-            dx_passes(0, j, [0], (4, 5, 6, 7))
-        group_rows("w1", 3, 256, 512, "v", "rows")
-        quantise(("w1", 1))
         pool_rows("w1", 2, POOL_SHARE)
-        rest_rows("w1", 2)
+        pool_rows("w1", 1, POOL_SHARE, "rows")
+        takes_dz(1, 0, [2, 3])
+        dw(0, 1, [0, 2], (4, 5, 6, 7))
+        dzs(4, [3, 2])
+        dh(5, [3, 2])
+        rest_rows("w1", 1, "rows")
+        dw(0, 1, [1, 3], (4, 5, 6, 7))
+        dzs(4, [0, 1])
+        dh(5, [0, 1])
+        group_t(*units[4], 0, 2, "s", "rows")
         for j in range(2):
-            dx_passes(0, j, [1])
-        dzs(5, [2, 3])
-        flips_dz(0, 1, [2, 3], DH_BANKS[2:])
+            dx_passes(0, j, [0], (4, 5, 6, 7))
+        dzs(5, [3, 2])
+        flips_dz(0, 1, [3], DH_BANKS[3:])
+        flips_dz(0, 1, [2], DH_BANKS[2:3])
         for j in range(2, 4):
-            dx_passes(0, j, [1])
-        takes_dz(0, 1, [2, 3])
+            dx_passes(0, j, [0], (4, 5, 6, 7))
+        takes_dz(0, 1, [3, 2])
         dzs(5, [0, 1])
         flips_dz(0, 1, [0, 1], DH_BANKS[:2])
         takes_dz(0, 1, [0, 1])
-        dh(6, [2, 3, 0, 1])
+        rest_rows("w1", 2)
+        quantise(("w1", 1))
+        for j in range(4):
+            dx_passes(0, j, [1])
+        dh(6, [3, 2, 0, 1])
         q_h(1, 0, 0)
         quantise(("w1", 3))
         q_h(0, 1, 1)
-        q_h(1, 0, 1)
         q_h(0, 1, 0)
+        q_h(1, 0, 1)
         quantise(("w1", 2))
         pool_t(5)
-        own_t(4, "ss")
+        group_t(*units[4], 2, 4, "s", "rows")
         for j in (2, 3, 0, 1):
             dx_passes(0, j, [3])
         for j in range(4):
             dx_passes(0, j, [2])
-        for j in range(3):
+        rest_t(5)
+        dzs(6, [1, 0])
+        dh(7, [1, 0])
+        for j in range(2):
             leave_dx(0, j, "s")
             dx_passes(1, j, range(2), (4, 5, 6, 7))
-        dzs(6, [1, 2, 3, 0])
-        q_t(4)
-        own_t(6, "vs")
-        leave_dx(0, 3, "s")
-        dh(7, [0, 1])
-        for m in (0, 2):
-            dw_passes(1, 0, m, [0], DH_BANKS[2:])
-        dx_passes(1, 3, range(2), (4, 5, 6, 7))
-        q_t(6)
-        rest_t(5)
-        for m in (0, 2):
-            dw_passes(1, 0, m, [1])
-            leave_dw(1, 0, m, "s")
-        dzs(7, [1, 0])
-        q_t(5)
-        flips_dz(1, 1, [0, 1], DH_BANKS[:2])
+        dzs(6, [2, 3])
         dh(7, [2, 3])
-        takes_dz(1, 1, [0], "v")
-        takes_dz(1, 1, [1])
+        leave_dx(0, 2, "s")
+        leave_dx(0, 3, "s")
+        dx_passes(1, 2, range(2), (4, 5, 6, 7))
+        group_t_share(*units[6], 0, POOL_SHARE // 2, "g", "rows")
+        group_t_share(*units[6], POOL_SHARE // 2, 2 * P, "s", "rows")
+        dzs(7, [1, 0])
+        flips_dz(1, 1, [1], DH_BANKS[1:2])
+        flips_dz(1, 1, [0], DH_BANKS[:1])
+        takes_dz(1, 1, [1, 0])
+        dx_passes(1, 3, range(2), (4, 5, 6, 7))
         dzs(7, [2, 3])
-        dw(1, 0, [1, 3], DH_BANKS[:2])
         flips_dz(1, 1, [2, 3], DH_BANKS[2:])
+        takes_dz(1, 1, [2, 3])
+        q_t(4)
+        q_t(6)
+        for m in (0, 2, 1, 3):
+            dw_passes(1, 0, m, range(2), (1, 0, 2, 3))
         q_h(1, 1, 0)
         group_t(1, 1, 1, 0, 2, "v", "rows")
-        takes_dz(1, 1, [2, 3])
         for j in range(2):
             dx_passes(1, j, [2, 3])
-        quantise(("t", 1, 1, 1), 0, 256)
-        group_t(1, 1, 1, 2, 4, "v", "rows")
-        for m in range(2):
-            dw_passes(1, 1, m, [0, 1], DH_BANKS[:2])
         q_h(1, 1, 1)
-        quantise(("t", 1, 1, 1), 256, 512)
-        leave_dx(1, 0, "s", True)
-        leave_dx(1, 1, "s", True)
-        for m in range(2, 4):
-            dw_passes(1, 1, m, [0], DH_BANKS[2:])
+        group_t(1, 1, 1, 2, 4, "v", "rows")
+        q_t(5)
+        q_t(7)
+        for m in (0, 2, 1, 3):
+            leave_dw(1, 0, m, "s", True)
         for j in range(2, 4):
             dx_passes(1, j, [2, 3])
-        leave_dw(1, 1, 0, "s", True)
-        leave_dw(1, 1, 1, "s", True)
-        for m in range(2, 4):
-            dw_passes(1, 1, m, [1])
-        leave_dx(1, 2, "s", True)
+        for m in (0, 2, 1, 3):
+            dw_passes(1, 1, m, range(2), (1, 0, 2, 3))
+        leave_dx(1, 0, "s", True)
+        leave_dx(1, 1, "s", True)
+        leave_dx(1, 2, "v", True)
         leave_dx(1, 3, "v", True)
+        leave_dw(1, 1, 0, "s", True)
         leave_dw(1, 1, 2, "v", True)
-        leave_dw(1, 1, 3, "s", True)
+        leave_dw(1, 1, 1, "s", True)
+        leave_dw(1, 1, 3, "v", True)

@@ -22,9 +22,10 @@ COPY = mybir.ActivationFunctionType.Copy
 DH_BANKS = (0, 1, 2, 3)
 FLIP_BANKS = (4, 5, 6, 7)
 SUM_BANKS = FLIP_BANKS
-SLABS = 8
-PRE_BUFS = 14
-DZ_BUFS = 5
+SLABS = 7
+NARROW_BUFS = 4
+WIDE_BUFS = 6
+DZ_BUFS = 4
 GROUP_BUFS = {"words": 4, "rows": 5, "pool": 1}
 POOL_SHARE = 352
 
@@ -58,29 +59,51 @@ def tile_mlp_v_kernel(tc, x, w1, w2, pre, grad_out, out_0, out_1):
         def slab(dtype, shape):
             return stream.tile([P] + shape, dtype, name="slab", bufs=SLABS)
 
-        def load_g(b, half):
-            raw["g", b, half] = keep.tile([P, 2, DIM], BF16, name="g_raw%d%d" % (b, half))
+        def load_g(b, j, n):
+            tile = keep.tile([P, n, DIM], BF16, name="g_raw%d%d" % (b, j))
             src = grad_out[b].rearrange("(p j) d -> p j d", j=4)
-            nc.sync.dma_start(out=raw["g", b, half][:], in_=src[:, 2 * half : 2 * half + 2, :])
+            nc.sync.dma_start(out=tile[:], in_=src[:, j : j + n, :])
+            for i in range(n // 2):
+                raw["g", b, j // 2 + i] = tile[:, 2 * i : 2 * i + 2, :]
 
-        def load_w2(c, u, s):
-            raw["w2", c, u, s] = stream.tile([P, 2, DIM], BF16, name="w2_raw", bufs=4)
-            rows = w2[HALF * c + PASS * s : HALF * c + PASS * s + PASS, :]
-            src = rows.rearrange("(p u e) d -> p u e d", u=2, e=2)
-            nc.sync.dma_start(out=raw["w2", c, u, s][:], in_=src[:, u, :, :])
-
-        def load_rows(what, i):
-            if what == "x":
-                raw[what, i] = slab(BF16, [4, DIM])
+        def load_w2(c, u, n):
+            if n == 1:
+                tile = keep.tile([P, 2, 2, DIM], BF16, name="w2_raw%d" % u)
             else:
-                raw[what, i] = stream.tile([P, 4, DIM], BF16, name="pre_rows", bufs=PRE_BUFS)
-            rows = x[i] if what == "x" else w1[PASS * i : PASS * i + PASS, :]
-            nc.sync.dma_start(out=raw[what, i][:], in_=rows.rearrange("(p t) d -> p t d", t=4))
+                tile = stream.tile([P, 2, 4, DIM], BF16, name="wide", bufs=WIDE_BUFS)
+            rows = w2[HALF * c : HALF * c + HALF, :].rearrange("(s p t) d -> p s t d", s=2, t=4)
+            nc.sync.dma_start(out=tile[:], in_=rows[:, :, 2 * u : 2 * u + 2 * n, :])
+            for i in range(n):
+                for s in range(2):
+                    raw["w2", c, u + i, s] = tile[:, s, 2 * i : 2 * i + 2, :]
 
-        def load_pre(b, c, j):
-            raw["pre", b, c, j] = stream.tile([P, HALF], F32, name="pre_rows", bufs=PRE_BUFS)
+        def load_w2_first(s):
+            raw["w2", 0, 0, s] = keep.tile([P, 2, DIM], BF16, name="w2_first%d" % s)[:]
+            rows = w2[PASS * s : PASS * s + PASS, :].rearrange("(p t) d -> p t d", t=4)
+            nc.sync.dma_start(out=raw["w2", 0, 0, s], in_=rows[:, 0:2, :])
+
+        def load_x(b):
+            raw["x", b] = slab(BF16, [4, DIM])[:]
+            nc.sync.dma_start(out=raw["x", b], in_=x[b].rearrange("(p t) d -> p t d", t=4))
+
+        def narrow_or_wide(n, shape, dtype):
+            if n == 1:
+                return stream.tile([P, n] + shape, dtype, name="narrow", bufs=NARROW_BUFS)
+            return stream.tile([P, n] + shape, dtype, name="wide", bufs=WIDE_BUFS)
+
+        def load_w1(q, n):
+            tile = narrow_or_wide(n, [4, DIM], BF16)
+            rows = w1[PASS * q : PASS * (q + n), :].rearrange("(q p t) d -> p q t d", q=n, t=4)
+            nc.sync.dma_start(out=tile[:], in_=rows)
+            for i in range(n):
+                raw["w1", q + i] = tile[:, i, :, :]
+
+        def load_pre(b, c, j, n):
+            tile = narrow_or_wide(n, [HALF], F32)
             src = pre[b].rearrange("(p j) h -> p j h", j=4)
-            nc.sync.dma_start(out=raw["pre", b, c, j][:], in_=src[:, j, HALF * c : HALF * c + HALF])
+            nc.sync.dma_start(out=tile[:], in_=src[:, j : j + n, HALF * c : HALF * c + HALF])
+            for i in range(n):
+                raw["pre", b, c, j + i] = tile[:, i, :]
 
         def copy_words(engine, out, in_):
             if engine == "s":
@@ -137,7 +160,7 @@ def tile_mlp_v_kernel(tc, x, w1, w2, pre, grad_out, out_0, out_1):
             )
 
         def flip_g(b, half, ring=FLIP_BANKS):
-            words = raw["g", b, half][:].bitcast(F32)
+            words = raw["g", b, half].bitcast(F32)
             transposes(("g", b, half), [words[:, i // 2, i % 2 :: 2] for i in range(4)], ring)
 
         def take_g(b, half, engine):
@@ -149,7 +172,7 @@ def tile_mlp_v_kernel(tc, x, w1, w2, pre, grad_out, out_0, out_1):
             )
 
         def flip_g_tile(b, j, ring=FLIP_BANKS):
-            words = raw["g", b, j // 2][:].bitcast(F32)
+            words = raw["g", b, j // 2].bitcast(F32)
             dst = bank(ring, ("g1", b, j))
             for v in range(2):
                 nc.tensor.transpose(dst[:, P * v : P * v + P], words[:, j % 2, v::2], ident[:])
@@ -163,7 +186,7 @@ def tile_mlp_v_kernel(tc, x, w1, w2, pre, grad_out, out_0, out_1):
             )
 
         def flip_w2(c, u, s, ring=FLIP_BANKS):
-            words = raw["w2", c, u, s][:].bitcast(F32)
+            words = raw["w2", c, u, s].bitcast(F32)
             transposes(("w2", c, u, s), [words[:, i // 2, i % 2 :: 2] for i in range(4)], ring)
 
         def take_w2(c, u, s, engine):
@@ -189,7 +212,7 @@ def tile_mlp_v_kernel(tc, x, w1, w2, pre, grad_out, out_0, out_1):
         def make_dz(b, c, u, j):
             if (b, c, u) not in dz:
                 dz[b, c, u] = stream.tile([P, 4, PASS], BF16, name="dz", bufs=DZ_BUFS, align_bytes=64)
-            rows = raw["pre", b, c, j][:].rearrange("p (n u e) -> p n u e", u=2, e=2)
+            rows = raw["pre", b, c, j].rearrange("p (n u e) -> p n u e", u=2, e=2)
             nc.vector.scalar_tensor_tensor(
                 out=dz[b, c, u][:, j, :].rearrange("p (n e) -> p n e", e=2),
                 in0=rows[:, :, u, :],
@@ -223,13 +246,15 @@ def tile_mlp_v_kernel(tc, x, w1, w2, pre, grad_out, out_0, out_1):
             if engine == "g":
                 nc.gpsimd.tensor_scalar(out=dst, in0=src, scalar1=1.0, scalar2=0.0, op0=MULT, op1=ADD)
             else:
-                nc.scalar.copy(
-                    out=dst.rearrange("p e (c i) t -> p e c t i", i=4), in_=src.rearrange("p e (c i) t -> p e c t i", i=4)
+                copy_words(
+                    engine,
+                    out=dst.rearrange("p e (c i) t -> p e c t i", i=4),
+                    in_=src.rearrange("p e (c i) t -> p e c t i", i=4),
                 )
 
         def pool_rows(what, i, hi, name="pool"):
             dst = group_tile((what, i), name)[:].rearrange("p (n t) -> p n t", t=4)[:, :hi, :]
-            src = raw[what, i][:].rearrange("p t n -> p n t")[:, :hi, :]
+            src = raw[what, i].rearrange("p t n -> p n t")[:, :hi, :]
             nc.gpsimd.tensor_scalar(out=dst, in0=src, scalar1=2.0, scalar2=0.0, op0=MULT, op1=ADD)
 
         def open_sum(ring, key):
@@ -281,14 +306,6 @@ def tile_mlp_v_kernel(tc, x, w1, w2, pre, grad_out, out_0, out_1):
             for j in js:
                 make_dz(*units[m], j)
 
-        def pres(b, c, js):
-            for j in js:
-                load_pre(b, c, j)
-
-        def w2_pair(c, u):
-            load_w2(c, u, 0)
-            load_w2(c, u, 1)
-
         def flips_w2(c, u, ring=FLIP_BANKS):
             flip_w2(c, u, 0, ring)
             flip_w2(c, u, 1, ring)
@@ -329,20 +346,23 @@ def tile_mlp_v_kernel(tc, x, w1, w2, pre, grad_out, out_0, out_1):
                 dw_passes(c, u, m, range(2), ring)
                 leave_dw(c, u, m, engines[m], single)
 
-        load_rows("x", 0)
-        load_rows("x", 1)
-        w2_pair(0, 0)
-        load_g(0, 0)
-        pres(0, 0, [0])
-        load_g(0, 1)
-        w2_pair(0, 1)
-        pres(0, 0, [1])
-        load_rows("w1", 3)
-        pres(0, 0, [2, 3])
-        load_g(1, 0)
-        load_g(1, 1)
-        pres(1, 0, J)
-
+        load_x(0)
+        load_x(1)
+        load_w2_first(0)
+        load_w2_first(1)
+        load_g(0, 0, 2)
+        load_pre(0, 0, 0, 1)
+        load_g(0, 2, 2)
+        load_w2(0, 1, 1)
+        load_pre(0, 0, 1, 1)
+        load_pre(0, 0, 2, 2)
+        load_g(1, 0, 4)
+        load_pre(1, 0, 0, 2)
+        load_pre(1, 0, 2, 2)
+        load_w2(1, 0, 2)
+        load_w1(0, 1)
+        load_pre(0, 1, 0, 2)
+        load_w1(2, 2)
         group_rows("x", 0, 0, 512, "s", "rows")
         group_rows("x", 1, 0, 512, "v", "rows")
         flips_w2(0, 0)
@@ -362,33 +382,26 @@ def tile_mlp_v_kernel(tc, x, w1, w2, pre, grad_out, out_0, out_1):
         dh(0, [1])
         take_g(0, 1, "s")
         dzs(0, [0])
-        w2_pair(1, 0)
         flips_w2(0, 1)
         quantise(("g", 0), 256, 512)
         dh(0, [2, 3])
-        w2_pair(1, 1)
-        load_rows("w1", 0)
-        pres(0, 1, [0, 1])
-        load_rows("w1", 2)
-        pres(0, 1, [2, 3])
         takes_w2(0, 1)
         dzs(0, [1])
-        group_rows("w1", 3, 0, 512, "s", "rows")
         quantise(("w2", 0, 1))
         dh(1, [0, 1])
         dzs(0, [2])
         dh(1, [2])
-        flip_g(1, 0)
         dzs(0, [3])
         dh(1, [3])
+        flip_g(1, 0)
         flip_g(1, 1)
         pool_t(0)
         rest_t(0)
         take_g(1, 0, "s")
         take_g(1, 1, "s")
         dzs(1, J)
-        load_rows("w1", 1)
-        pres(1, 1, [0, 1])
+        load_pre(0, 1, 2, 2)
+        load_w1(1, 1)
         flips_dz(0, 0, J)
         quantise(("g", 1), 0, 256)
         takes_dz(0, 0, [0, 1])
@@ -399,14 +412,9 @@ def tile_mlp_v_kernel(tc, x, w1, w2, pre, grad_out, out_0, out_1):
         pool_t(1)
         takes_dz(0, 0, [2, 3])
         rest_t(1)
-        dzs(2, [0])
-        pres(1, 1, [2])
-        dzs(2, [1])
-        pres(1, 1, [3])
-        dzs(2, [2, 3])
-        dh(3, [0, 1])
+        dzs(2, J)
+        dh(3, J)
         flips_w2(1, 0)
-        dh(3, [2, 3])
         q_h(0, 0, 0)
         own_t(2, "vs")
         takes_w2(1, 0)
@@ -417,9 +425,11 @@ def tile_mlp_v_kernel(tc, x, w1, w2, pre, grad_out, out_0, out_1):
         pool_rows("w1", 0, POOL_SHARE)
         takes_w2(1, 1)
         rest_rows("w1", 0)
+        dzs(3, [3, 0, 1, 2])
+        load_pre(1, 1, 0, 2)
+        load_pre(1, 1, 2, 2)
         dw(0, 0, [0, 2, 1], (4, 5, 6, 7))
         dw_passes(0, 0, 3, range(2), (4, 5, 6, 7))
-        dzs(3, [3, 0, 1, 2])
         group_t(*units[3], 2, 4, "s", "rows")
         leave_dw(0, 0, 3, "s")
         quantise(("w2", 1, 0))
@@ -441,7 +451,7 @@ def tile_mlp_v_kernel(tc, x, w1, w2, pre, grad_out, out_0, out_1):
         dw(0, 1, [1, 3], (4, 5, 6, 7))
         dzs(4, [0, 1])
         dh(5, [0, 1])
-        group_t(*units[4], 0, 2, "s", "rows")
+        group_rows("w1", 3, 0, 256, "s", "rows")
         for j in range(2):
             dx_passes(0, j, [0], (4, 5, 6, 7))
         dzs(5, [3, 2])
@@ -454,6 +464,7 @@ def tile_mlp_v_kernel(tc, x, w1, w2, pre, grad_out, out_0, out_1):
         flips_dz(0, 1, [0, 1], DH_BANKS[:2])
         takes_dz(0, 1, [0, 1])
         rest_rows("w1", 2)
+        group_rows("w1", 3, 256, 512, "v", "rows")
         quantise(("w1", 1))
         for j in range(4):
             dx_passes(0, j, [1])
@@ -462,35 +473,35 @@ def tile_mlp_v_kernel(tc, x, w1, w2, pre, grad_out, out_0, out_1):
         quantise(("w1", 3))
         q_h(0, 1, 1)
         q_h(0, 1, 0)
-        q_h(1, 0, 1)
         quantise(("w1", 2))
-        pool_t(5)
-        group_t(*units[4], 2, 4, "s", "rows")
+        group_t_share(*units[5], 0, 192, "g")
+        own_t(4, "ss")
         for j in (2, 3, 0, 1):
             dx_passes(0, j, [3])
         for j in range(4):
             dx_passes(0, j, [2])
-        rest_t(5)
         dzs(6, [1, 0])
         dh(7, [1, 0])
-        for j in range(2):
-            leave_dx(0, j, "s")
-            dx_passes(1, j, range(2), (4, 5, 6, 7))
+        leave_dx(0, 0, "s")
+        leave_dx(0, 1, "s")
+        dx_passes(1, 0, range(2), (4, 5, 6, 7))
         dzs(6, [2, 3])
         dh(7, [2, 3])
+        dx_passes(1, 1, range(2), (4, 5, 6, 7))
         leave_dx(0, 2, "s")
         leave_dx(0, 3, "s")
-        dx_passes(1, 2, range(2), (4, 5, 6, 7))
         group_t_share(*units[6], 0, POOL_SHARE // 2, "g", "rows")
         group_t_share(*units[6], POOL_SHARE // 2, 2 * P, "s", "rows")
         dzs(7, [1, 0])
         flips_dz(1, 1, [1], DH_BANKS[1:2])
         flips_dz(1, 1, [0], DH_BANKS[:1])
         takes_dz(1, 1, [1, 0])
-        dx_passes(1, 3, range(2), (4, 5, 6, 7))
         dzs(7, [2, 3])
         flips_dz(1, 1, [2, 3], DH_BANKS[2:])
         takes_dz(1, 1, [2, 3])
+        q_h(1, 0, 1)
+        for j in range(2, 4):
+            dx_passes(1, j, range(2), (4, 5, 6, 7))
         q_t(4)
         q_t(6)
         for m in (0, 2, 1, 3):
@@ -501,6 +512,7 @@ def tile_mlp_v_kernel(tc, x, w1, w2, pre, grad_out, out_0, out_1):
             dx_passes(1, j, [2, 3])
         q_h(1, 1, 1)
         group_t(1, 1, 1, 2, 4, "v", "rows")
+        group_t_share(*units[5], 192, 256, "v")
         q_t(5)
         q_t(7)
         for m in (0, 2, 1, 3):

@@ -27,7 +27,7 @@ NARROW_BUFS = 4
 WIDE_BUFS = 6
 DZ_BUFS = 4
 GROUP_BUFS = {"words": 4, "rows": 5, "pool": 1}
-POOL_SHARE = 352
+POOL_SHARE = 384
 
 
 def tile_mlp_v_kernel(tc, x, w1, w2, pre, grad_out, out_0, out_1):
@@ -346,6 +346,9 @@ def tile_mlp_v_kernel(tc, x, w1, w2, pre, grad_out, out_0, out_1):
                 dw_passes(c, u, m, range(2), ring)
                 leave_dw(c, u, m, engines[m], single)
 
+        def whole_t(m, engine):
+            group_t_share(*units[m], 0, 2 * P, engine, "rows")
+
         load_x(0)
         load_x(1)
         load_w2_first(0)
@@ -473,9 +476,10 @@ def tile_mlp_v_kernel(tc, x, w1, w2, pre, grad_out, out_0, out_1):
         quantise(("w1", 3))
         q_h(0, 1, 1)
         q_h(0, 1, 0)
+        q_h(1, 0, 1)
         quantise(("w1", 2))
-        group_t_share(*units[5], 0, 192, "g")
-        own_t(4, "ss")
+        group_t_share(*units[5], 0, 208, "g")
+        group_t(*units[4], 0, 2, "s", "rows")
         for j in (2, 3, 0, 1):
             dx_passes(0, j, [3])
         for j in range(4):
@@ -490,42 +494,48 @@ def tile_mlp_v_kernel(tc, x, w1, w2, pre, grad_out, out_0, out_1):
         dx_passes(1, 1, range(2), (4, 5, 6, 7))
         leave_dx(0, 2, "s")
         leave_dx(0, 3, "s")
+        group_t(*units[4], 2, 4, "s", "rows")
         group_t_share(*units[6], 0, POOL_SHARE // 2, "g", "rows")
         group_t_share(*units[6], POOL_SHARE // 2, 2 * P, "s", "rows")
         dzs(7, [1, 0])
         flips_dz(1, 1, [1], DH_BANKS[1:2])
         flips_dz(1, 1, [0], DH_BANKS[:1])
         takes_dz(1, 1, [1, 0])
+        dx_passes(1, 2, range(2), (7,))
         dzs(7, [2, 3])
         flips_dz(1, 1, [2, 3], DH_BANKS[2:])
-        takes_dz(1, 1, [2, 3])
-        q_h(1, 0, 1)
-        for j in range(2, 4):
-            dx_passes(1, j, range(2), (4, 5, 6, 7))
         q_t(4)
+        for m in (0, 2):
+            dw_passes(1, 0, m, [0], (4, 1, 0, 2))
         q_t(6)
-        for m in (0, 2, 1, 3):
-            dw_passes(1, 0, m, range(2), (1, 0, 2, 3))
+        takes_dz(1, 1, [2])
+        for m in (0, 2):
+            dw_passes(1, 0, m, [1])
+        leave_dw(1, 0, 0, "s", True)
+        leave_dw(1, 0, 2, "s", True)
+        for m in (1, 3):
+            dw_passes(1, 0, m, range(2), (4, 1, 0, 2))
         q_h(1, 1, 0)
-        group_t(1, 1, 1, 0, 2, "v", "rows")
+        takes_dz(1, 1, [3], "v")
         for j in range(2):
             dx_passes(1, j, [2, 3])
+        whole_t(7, "v")
+        group_t_share(*units[5], 208, 256, "v")
         q_h(1, 1, 1)
-        group_t(1, 1, 1, 2, 4, "v", "rows")
-        group_t_share(*units[5], 192, 256, "v")
+        for m in (1, 3):
+            leave_dw(1, 0, m, "s", True)
+        dx_passes(1, 3, range(2), (3,))
+        for j in range(2, 4):
+            dx_passes(1, j, [2, 3])
         q_t(5)
         q_t(7)
         for m in (0, 2, 1, 3):
-            leave_dw(1, 0, m, "s", True)
-        for j in range(2, 4):
-            dx_passes(1, j, [2, 3])
-        for m in (0, 2, 1, 3):
-            dw_passes(1, 1, m, range(2), (1, 0, 2, 3))
-        leave_dx(1, 0, "s", True)
-        leave_dx(1, 1, "s", True)
-        leave_dx(1, 2, "v", True)
-        leave_dx(1, 3, "v", True)
-        leave_dw(1, 1, 0, "s", True)
-        leave_dw(1, 1, 2, "v", True)
+            dw_passes(1, 1, m, range(2), (4, 1, 0, 2))
+        leave_dx(1, 0, "s")
+        leave_dx(1, 1, "s")
+        leave_dx(1, 2, "s")
+        leave_dx(1, 3, "v")
+        leave_dw(1, 1, 0, "s")
+        leave_dw(1, 1, 2, "v")
         leave_dw(1, 1, 1, "s", True)
         leave_dw(1, 1, 3, "v", True)

@@ -27,7 +27,7 @@ NARROW_BUFS = 4
 WIDE_BUFS = 6
 DZ_BUFS = 4
 GROUP_BUFS = {"words": 4, "rows": 5, "pool": 1}
-POOL_SHARE = 384
+POOL_SHARE = 352
 
 
 def tile_mlp_v_kernel(tc, x, w1, w2, pre, grad_out, out_0, out_1):
@@ -353,9 +353,8 @@ def tile_mlp_v_kernel(tc, x, w1, w2, pre, grad_out, out_0, out_1):
         load_x(1)
         load_w2_first(0)
         load_w2_first(1)
-        load_g(0, 0, 2)
+        load_g(0, 0, 4)
         load_pre(0, 0, 0, 1)
-        load_g(0, 2, 2)
         load_w2(0, 1, 1)
         load_pre(0, 0, 1, 1)
         load_pre(0, 0, 2, 2)
@@ -478,7 +477,7 @@ def tile_mlp_v_kernel(tc, x, w1, w2, pre, grad_out, out_0, out_1):
         q_h(0, 1, 0)
         q_h(1, 0, 1)
         quantise(("w1", 2))
-        group_t_share(*units[5], 0, 208, "g")
+        group_t_share(*units[5], 0, POOL_SHARE // 2, "g")
         group_t(*units[4], 0, 2, "s", "rows")
         for j in (2, 3, 0, 1):
             dx_passes(0, j, [3])
@@ -520,7 +519,7 @@ def tile_mlp_v_kernel(tc, x, w1, w2, pre, grad_out, out_0, out_1):
         for j in range(2):
             dx_passes(1, j, [2, 3])
         whole_t(7, "v")
-        group_t_share(*units[5], 208, 256, "v")
+        group_t_share(*units[5], POOL_SHARE // 2, 2 * P, "v")
         q_h(1, 1, 1)
         for m in (1, 3):
             leave_dw(1, 0, m, "s", True)
@@ -531,11 +530,11 @@ def tile_mlp_v_kernel(tc, x, w1, w2, pre, grad_out, out_0, out_1):
         q_t(7)
         for m in (0, 2, 1, 3):
             dw_passes(1, 1, m, range(2), (4, 1, 0, 2))
-        leave_dx(1, 0, "s")
-        leave_dx(1, 1, "s")
-        leave_dx(1, 2, "s")
-        leave_dx(1, 3, "v")
-        leave_dw(1, 1, 0, "s")
-        leave_dw(1, 1, 2, "v")
+        leave_dx(1, 0, "s", True)
+        leave_dx(1, 1, "s", True)
+        leave_dx(1, 2, "s", True)
+        leave_dx(1, 3, "v", True)
+        leave_dw(1, 1, 0, "s", True)
+        leave_dw(1, 1, 2, "v", True)
         leave_dw(1, 1, 1, "s", True)
         leave_dw(1, 1, 3, "v", True)

@@ -19,15 +19,11 @@ E5M2 = mybir.dt.float8_e5m2_x4
 MULT, ADD, MAX = mybir.AluOpType.mult, mybir.AluOpType.add, mybir.AluOpType.max
 COPY = mybir.ActivationFunctionType.Copy
 
-DH_BANKS = (0, 1, 2, 3)
-FLIP_BANKS = (4, 5, 6, 7)
-SUM_BANKS = FLIP_BANKS
-SLABS = 7
-NARROW_BUFS = 4
-WIDE_BUFS = 6
+PAIRS = ((0, 0), (1, 0), (0, 1), (1, 1))
+SLABS = 12
+PRE_BUFS = 6
 DZ_BUFS = 4
-GROUP_BUFS = {"words": 4, "rows": 5, "pool": 1}
-POOL_SHARE = 352
+GROUP_BUFS = {"words": 4, "rows": 4, "pool": 1, "late": 1, "held": 1}
 
 
 def tile_mlp_v_kernel(tc, x, w1, w2, pre, grad_out, out_0, out_1):
@@ -47,82 +43,64 @@ def tile_mlp_v_kernel(tc, x, w1, w2, pre, grad_out, out_0, out_1):
         banks = {}
         codes = {}
         staged = {}
-        turns = {}
         passes = {}
 
-        def bank(ring, key):
-            n = turns.get(ring, 0)
-            turns[ring] = n + 1
-            banks[key] = psum.tile([P, PASS], F32, name="bank%d" % ring[n % len(ring)])
+        def bank(number, key):
+            banks[key] = psum.tile([P, PASS], F32, name="bank%d" % number)
             return banks[key]
 
-        def slab(dtype, shape):
-            return stream.tile([P] + shape, dtype, name="slab", bufs=SLABS)
+        def slab(dtype, width):
+            return stream.tile([P, width], dtype, name="slab", bufs=SLABS)
 
-        def load_g(b, j, n):
-            tile = keep.tile([P, n, DIM], BF16, name="g_raw%d%d" % (b, j))
-            src = grad_out[b].rearrange("(p j) d -> p j d", j=4)
-            nc.sync.dma_start(out=tile[:], in_=src[:, j : j + n, :])
-            for i in range(n // 2):
-                raw["g", b, j // 2 + i] = tile[:, 2 * i : 2 * i + 2, :]
-
-        def load_w2(c, u, n):
-            if n == 1:
-                tile = keep.tile([P, 2, 2, DIM], BF16, name="w2_raw%d" % u)
+        def load_rows(what, i, src, lo, hi):
+            if hi - lo == 4:
+                tile = slab(BF16, 4 * DIM)
             else:
-                tile = stream.tile([P, 2, 4, DIM], BF16, name="wide", bufs=WIDE_BUFS)
-            rows = w2[HALF * c : HALF * c + HALF, :].rearrange("(s p t) d -> p s t d", s=2, t=4)
-            nc.sync.dma_start(out=tile[:], in_=rows[:, :, 2 * u : 2 * u + 2 * n, :])
-            for i in range(n):
-                for s in range(2):
-                    raw["w2", c, u + i, s] = tile[:, s, 2 * i : 2 * i + 2, :]
+                tile = keep.tile([P, (hi - lo) * DIM], BF16, name="%s%d_rows%d" % (what, i, lo))
+            rows = src.rearrange("(p t) d -> p t d", t=4)[:, lo:hi, :]
+            nc.sync.dma_start(out=tile[:].rearrange("p (t d) -> p t d", d=DIM), in_=rows)
+            raw[what, i] = tile[:]
+            for half in range(lo // 2, hi // 2):
+                raw[what, i, half] = tile[:, DIM * (2 * half - lo) : DIM * (2 * half - lo + 2)]
 
-        def load_w2_first(s):
-            raw["w2", 0, 0, s] = keep.tile([P, 2, DIM], BF16, name="w2_first%d" % s)[:]
-            rows = w2[PASS * s : PASS * s + PASS, :].rearrange("(p t) d -> p t d", t=4)
-            nc.sync.dma_start(out=raw["w2", 0, 0, s], in_=rows[:, 0:2, :])
+        def load_g(b, lo=0, hi=4):
+            load_rows("g", b, grad_out[b], lo, hi)
 
         def load_x(b):
-            raw["x", b] = slab(BF16, [4, DIM])[:]
-            nc.sync.dma_start(out=raw["x", b], in_=x[b].rearrange("(p t) d -> p t d", t=4))
+            load_rows("x", b, x[b], 0, 4)
 
-        def narrow_or_wide(n, shape, dtype):
-            if n == 1:
-                return stream.tile([P, n] + shape, dtype, name="narrow", bufs=NARROW_BUFS)
-            return stream.tile([P, n] + shape, dtype, name="wide", bufs=WIDE_BUFS)
+        def load_w1(q):
+            load_rows("w1", q, w1[PASS * q : PASS * q + PASS, :], 0, 4)
 
-        def load_w1(q, n):
-            tile = narrow_or_wide(n, [4, DIM], BF16)
-            rows = w1[PASS * q : PASS * (q + n), :].rearrange("(q p t) d -> p q t d", q=n, t=4)
-            nc.sync.dma_start(out=tile[:], in_=rows)
-            for i in range(n):
-                raw["w1", q + i] = tile[:, i, :, :]
+        def load_w2(i, lo=0, hi=2):
+            c, u = divmod(i, 2)
+            if hi - lo == 2:
+                tile = slab(BF16, 4 * DIM)
+            else:
+                tile = keep.tile([P, 2 * DIM], BF16, name="w2_%d_block%d" % (i, lo))
+            rows = w2[HALF * c : HALF * c + HALF, :].rearrange("(s p t) d -> p s t d", s=2, t=4)
+            nc.sync.dma_start(
+                out=tile[:].rearrange("p (s t d) -> p s t d", t=2, d=DIM), in_=rows[:, lo:hi, 2 * u : 2 * u + 2, :]
+            )
+            for s in range(lo, hi):
+                raw["w2", i, s] = tile[:, 2 * DIM * (s - lo) : 2 * DIM * (s - lo + 1)]
 
-        def load_pre(b, c, j, n):
-            tile = narrow_or_wide(n, [HALF], F32)
-            src = pre[b].rearrange("(p j) h -> p j h", j=4)
-            nc.sync.dma_start(out=tile[:], in_=src[:, j : j + n, HALF * c : HALF * c + HALF])
-            for i in range(n):
-                raw["pre", b, c, j + i] = tile[:, i, :]
+        def load_pre(pair, lo, hi):
+            b, c = PAIRS[pair]
+            if hi - lo == 2:
+                tile = stream.tile([P, 2 * HALF], F32, name="pre", bufs=PRE_BUFS)
+            else:
+                tile = slab(F32, HALF)
+            rows = pre[b].rearrange("(p j) h -> p j h", j=4)[:, lo:hi, HALF * c : HALF * c + HALF]
+            nc.sync.dma_start(out=tile[:].rearrange("p (j h) -> p j h", h=HALF), in_=rows)
+            for j in range(lo, hi):
+                raw["pre", pair, j] = tile[:, HALF * (j - lo) : HALF * (j - lo + 1)]
 
         def copy_words(engine, out, in_):
             if engine == "s":
                 nc.scalar.copy(out=out, in_=in_)
             else:
                 nc.vector.tensor_copy(out=out, in_=in_)
-
-        def interleave(engine, out, in_, factor):
-            out = out.rearrange("p (c i t) -> p c t i", i=4, t=4)
-            if engine == "g":
-                nc.gpsimd.tensor_scalar(out=out, in0=in_, scalar1=factor, scalar2=0.0, op0=MULT, op1=ADD)
-            elif engine == "s" and factor == 1.0:
-                nc.scalar.copy(out=out, in_=in_)
-            elif engine == "s":
-                nc.scalar.activation(out=out, in_=in_, func=COPY, scale=factor)
-            elif factor == 1.0:
-                nc.vector.tensor_copy(out=out, in_=in_)
-            else:
-                nc.vector.tensor_scalar(out=out, in0=in_, scalar1=factor, scalar2=None, op0=MULT)
 
         def group_tile(key, name):
             if key not in grouped:
@@ -131,7 +109,7 @@ def tile_mlp_v_kernel(tc, x, w1, w2, pre, grad_out, out_0, out_1):
 
         def quantise(key, lo=0, hi=PASS):
             if key not in codes:
-                label = "_".join([str(k) for k in key])
+                label = "%s%d" % key
                 codes[key] = (
                     keep.tile([P, PASS], U32, name="codes_" + label, align_bytes=64),
                     keep.tile([P, PASS], U8, name="scales_" + label, align_bytes=64),
@@ -142,399 +120,418 @@ def tile_mlp_v_kernel(tc, x, w1, w2, pre, grad_out, out_0, out_1):
                 out=words[:, lo:hi].bitcast(dtype), scales=scales[:, lo:hi], in_=grouped[key][:, PACK * lo : PACK * hi]
             )
 
-        def transposes(key, views, ring=FLIP_BANKS):
-            dst = bank(ring, key)
-            for i in range(4):
-                nc.tensor.transpose(dst[:, P * i : P * i + P], views[i], ident[:])
-
-        def multiply(out, left, m, right, start, stop):
-            cols = slice(P * m, P * m + P)
+        def multiply(out, left, tile, right, lo, hi, start, stop):
+            cols = slice(P * tile, P * tile + P)
             nc.tensor.matmul_mx(
                 out=out,
                 lhsT=codes[left][0][:, cols].bitcast(E5M2),
                 lhsT_scale=codes[left][1][:, cols],
-                rhs=codes[right][0][:].bitcast(E4M3),
-                rhs_scale=codes[right][1][:],
+                rhs=codes[right][0][:, lo:hi].bitcast(E4M3),
+                rhs_scale=codes[right][1][:, lo:hi],
                 start=start,
                 stop=stop,
             )
 
-        def flip_g(b, half, ring=FLIP_BANKS):
-            words = raw["g", b, half].bitcast(F32)
-            transposes(("g", b, half), [words[:, i // 2, i % 2 :: 2] for i in range(4)], ring)
+        def flip(what, i, half, number):
+            dst = bank(number, (what, i, half))
+            for k in range(4):
+                if what == "h":
+                    first = 2 * P * (2 * (i % 2) + half) + P * (k // 2)
+                    words = dz[i - i % 2 + k % 2][:].bitcast(F32)[:, first : first + P]
+                else:
+                    words = raw[what, i, half].bitcast(F32)[:, 2 * P * (k // 2) + k % 2 : 2 * P * (k // 2 + 1) : 2]
+                nc.tensor.transpose(dst[:, P * k : P * k + P], words, ident[:])
 
-        def take_g(b, half, engine):
-            dst = group_tile(("g", b), "words")[:].bitcast(F32)[:, PASS * half : PASS * half + PASS]
-            copy_words(
-                engine,
-                out=dst.rearrange("k (j n v) -> k j n v", j=2, v=2),
-                in_=banks["g", b, half][:].rearrange("k (j v n) -> k j n v", j=2, v=2),
-            )
+        def take(what, i, half, engine="s", name="words"):
+            dst = group_tile((what, i), name)[:].bitcast(F32)[:, PASS * half : PASS * half + PASS]
+            src = banks[what, i, half][:]
+            if what == "w2":
+                copy_words(engine, dst.rearrange("k (n i) -> k n i", i=4), src.rearrange("k (i n) -> k n i", i=4))
+            else:
+                copy_words(
+                    engine,
+                    dst.rearrange("k (j n v) -> k j n v", j=2, v=2),
+                    src.rearrange("k (j v n) -> k j n v", j=2, v=2),
+                )
 
-        def flip_g_tile(b, j, ring=FLIP_BANKS):
-            words = raw["g", b, j // 2].bitcast(F32)
-            dst = bank(ring, ("g1", b, j))
-            for v in range(2):
-                nc.tensor.transpose(dst[:, P * v : P * v + P], words[:, j % 2, v::2], ident[:])
+        def group_rows(what, i, lo, hi, engine, name="rows"):
+            dst = group_tile((what, i), name)[:, PACK * lo : PACK * hi]
+            src = raw[what, i].rearrange("p (t d) -> p t d", t=4)[:, :, lo:hi]
+            if engine == "g":
+                nc.gpsimd.tensor_scalar(
+                    out=dst.rearrange("p (n t) -> p n t", t=4),
+                    in0=src.rearrange("p t n -> p n t"),
+                    scalar1=2.0,
+                    scalar2=0.0,
+                    op0=MULT,
+                    op1=ADD,
+                )
+                return
+            dst = dst.rearrange("p (c i t) -> p c t i", i=4, t=4)
+            src = src.rearrange("p t (c i) -> p c t i", i=4)
+            if engine == "s":
+                nc.scalar.activation(out=dst, in_=src, func=COPY, scale=2.0)
+            else:
+                nc.vector.tensor_scalar(out=dst, in0=src, scalar1=2.0, scalar2=None, op0=MULT)
 
-        def take_g_tile(b, j, engine):
-            dst = group_tile(("g", b), "words")[:].bitcast(F32)[:, 2 * P * j : 2 * P * j + 2 * P]
-            copy_words(
-                engine,
-                out=dst.rearrange("k (n v) -> k n v", v=2),
-                in_=banks["g1", b, j][:, : 2 * P].rearrange("k (v n) -> k n v", v=2),
-            )
+        def make_dh(m, j, number):
+            b, c = PAIRS[m // 2]
+            multiply(bank(number, ("dh", m, j))[:], ("g", b), j, ("w2", 2 * c + m % 2), 0, PASS, True, True)
 
-        def flip_w2(c, u, s, ring=FLIP_BANKS):
-            words = raw["w2", c, u, s].bitcast(F32)
-            transposes(("w2", c, u, s), [words[:, i // 2, i % 2 :: 2] for i in range(4)], ring)
-
-        def take_w2(c, u, s, engine):
-            dst = group_tile(("w2", c, u), "words")[:].bitcast(F32)[:, PASS * s : PASS * s + PASS]
-            copy_words(
-                engine,
-                out=dst.rearrange("k (n i) -> k n i", i=4),
-                in_=banks["w2", c, u, s][:].rearrange("k (i n) -> k n i", i=4),
-            )
-
-        def group_rows(what, i, lo, hi, engine, name):
-            dst = group_tile((what, i), name)
-            interleave(
-                engine,
-                out=dst[:, PACK * lo : PACK * hi],
-                in_=raw[what, i][:, :, lo:hi].rearrange("p t (c i) -> p c t i", i=4),
-                factor=2.0,
-            )
-
-        def make_dh(b, c, u, j, ring):
-            multiply(bank(ring, ("dh", b, c, u, j))[:], ("g", b), j, ("w2", c, u), True, True)
-
-        def make_dz(b, c, u, j):
-            if (b, c, u) not in dz:
-                dz[b, c, u] = stream.tile([P, 4, PASS], BF16, name="dz", bufs=DZ_BUFS, align_bytes=64)
-            rows = raw["pre", b, c, j].rearrange("p (n u e) -> p n u e", u=2, e=2)
+        def make_dz(m, j):
+            if m not in dz:
+                dz[m] = stream.tile([P, 4 * PASS], BF16, name="dz", bufs=DZ_BUFS, align_bytes=64)
             nc.vector.scalar_tensor_tensor(
-                out=dz[b, c, u][:, j, :].rearrange("p (n e) -> p n e", e=2),
-                in0=rows[:, :, u, :],
+                out=dz[m][:, PASS * j : PASS * j + PASS].rearrange("p (n e) -> p n e", e=2),
+                in0=raw["pre", m // 2, j].rearrange("p (n u e) -> p n u e", u=2, e=2)[:, :, m % 2, :],
                 scalar=0.0,
-                in1=banks["dh", b, c, u, j][:].rearrange("p (n e) -> p n e", e=2),
+                in1=banks["dh", m, j][:].rearrange("p (n e) -> p n e", e=2),
                 op0=MAX,
                 op1=MULT,
             )
 
-        def flip_dz(b, c, j, ring=FLIP_BANKS):
-            words = [dz[b, c, u][:, j, :].bitcast(F32) for u in range(2)]
-            transposes(("h", b, c, j), [words[i % 2][:, P * (i // 2) : P * (i // 2) + P] for i in range(4)], ring)
-
-        def take_dz(b, c, j, engine, name="words"):
-            dst = group_tile(("h", b, c, j // 2), name)[:].bitcast(F32)[:, PASS * (j % 2) : PASS * (j % 2) + PASS]
-            copy_words(
-                engine,
-                out=dst.rearrange("k (s n u) -> k s n u", s=2, u=2),
-                in_=banks["h", b, c, j][:].rearrange("k (s u n) -> k s n u", s=2, u=2),
-            )
-
-        def group_t(b, c, u, m0, m1, engine, name):
-            dst = group_tile(("t", b, c, u), name)
-            src = dz[b, c, u][:].rearrange("p t (c i e) -> p e c t i", i=4, e=2)[:, m0 // 2, :, :, :]
-            runs = slice(P // 4 * (m0 % 2), P // 4 * (m0 % 2 + m1 - m0))
-            interleave(engine, out=dst[:, PACK * P * m0 : PACK * P * m1], in_=src[:, runs, :, :], factor=1.0)
-
-        def group_t_share(b, c, u, lo, hi, engine, name="pool"):
-            dst = group_tile(("t", b, c, u), name)[:].rearrange("p (e n t) -> p e n t", e=2, t=4)[:, :, lo:hi, :]
-            src = dz[b, c, u][:].rearrange("p t (n e) -> p e n t", e=2)[:, :, lo:hi, :]
+        def group_t(m, lo, hi, engine, name="pool"):
+            dst = group_tile(("t", m), name)[:].rearrange("p (e n j) -> p e n j", e=2, j=4)[:, :, lo:hi, :]
+            src = dz[m][:].rearrange("p (j n e) -> p e n j", j=4, e=2)[:, :, lo:hi, :]
             if engine == "g":
                 nc.gpsimd.tensor_scalar(out=dst, in0=src, scalar1=1.0, scalar2=0.0, op0=MULT, op1=ADD)
             else:
-                copy_words(
-                    engine,
-                    out=dst.rearrange("p e (c i) t -> p e c t i", i=4),
-                    in_=src.rearrange("p e (c i) t -> p e c t i", i=4),
-                )
+                copy_words(engine, dst, src)
 
-        def pool_rows(what, i, hi, name="pool"):
-            dst = group_tile((what, i), name)[:].rearrange("p (n t) -> p n t", t=4)[:, :hi, :]
-            src = raw[what, i].rearrange("p t n -> p n t")[:, :hi, :]
-            nc.gpsimd.tensor_scalar(out=dst, in0=src, scalar1=2.0, scalar2=0.0, op0=MULT, op1=ADD)
-
-        def open_sum(ring, key):
+        def add_pass(key, number, left, tile, right, total):
             n = passes.get(key, 0)
             passes[key] = n + 1
             if n == 0:
-                bank(ring, key)
-            return n
+                bank(number, key)
+            multiply(banks[key][:], left, tile, right, 0, PASS, n == 0, n == total - 1)
 
-        def dx_passes(b, j, qs, ring=SUM_BANKS):
-            for q in qs:
-                n = open_sum(ring, ("dx", b, j))
-                multiply(banks["dx", b, j][:], ("h", b, q // 2, j // 2), 2 * (j % 2) + q % 2, ("w1", q), n == 0, n == 3)
+        def dx_pass(b, j, q, number=None):
+            pair = PAIRS.index((b, q // 2))
+            add_pass(("dx", b, j), number, ("h", 2 * pair + j // 2), 2 * (j % 2) + q % 2, ("w1", q), 4)
 
-        def dw_passes(c, u, m, bs, ring=SUM_BANKS):
-            for b in bs:
-                n = open_sum(ring, ("dw", c, u, m))
-                multiply(banks["dw", c, u, m][:], ("t", b, c, u), m, ("x", b), n == 0, n == 1)
+        def dw_pass(m, tile, number=None):
+            b, c = PAIRS[m // 2]
+            add_pass(("dw", 2 * c + m % 2, tile), number, ("t", m), tile, ("x", b), 2)
 
-        def leave(pair, i, src, rows, engine, single):
-            if pair not in staged:
-                staged[pair] = [slab(F32, [2, DIM]), 0]
-            tile = staged[pair][0]
-            copy_words(engine, tile[:, i, :], src[:])
-            staged[pair][1] = staged[pair][1] + 1
-            if single:
-                nc.sync.dma_start(out=rows[:, i, :], in_=tile[:, i, :])
-            elif staged[pair][1] == 2:
-                nc.sync.dma_start(out=rows, in_=tile[:])
+        def leave(what, i, tile, engine="s"):
+            pair, side = divmod(tile, 2) if what == "dx" else (tile % 2, tile // 2)
+            if (what, i, pair) not in staged:
+                staged[what, i, pair] = slab(F32, 2 * DIM)
+            copy_words(engine, staged[what, i, pair][:, DIM * side : DIM * side + DIM], banks[what, i, tile][:])
 
-        def leave_dx(b, j, engine, single=False):
-            rows = out_0[b].rearrange("(p j) d -> p j d", j=4)[:, j - j % 2 : j - j % 2 + 2, :]
-            leave(("dx", b, j // 2), j % 2, banks["dx", b, j], rows, engine, single)
+        def store(what, i, pair, lo=0, hi=2):
+            if what == "dx":
+                rows = out_0[i].rearrange("(p j) d -> p j d", j=4)[:, 2 * pair : 2 * pair + 2, :]
+            else:
+                first = HALF * (i // 2) + PASS * pair
+                rows = out_1[first : first + PASS, :].rearrange("(p f) d -> p f d", f=4)[:, 2 * (i % 2) : 2 * (i % 2) + 2, :]
+            src = staged[what, i, pair][:].rearrange("p (f d) -> p f d", f=2)
+            nc.sync.dma_start(out=rows[:, lo:hi, :], in_=src[:, lo:hi, :])
 
-        def leave_dw(c, u, m, engine, single=False):
-            e, s = m // 2, m % 2
-            first = HALF * c + PASS * s
-            rows = out_1[first : first + PASS, :].rearrange("(p f) d -> p f d", f=4)[:, 2 * u : 2 * u + 2, :]
-            leave(("dw", c, u, s), e, banks["dw", c, u, m], rows, engine, single)
-
-        units = [(b, c, u) for c in range(2) for b in range(2) for u in range(2)]
-        J = range(4)
-
-        def dh(m, js):
-            for j in js:
-                make_dh(*units[m], j, DH_BANKS[j : j + 1])
-
-        def dzs(m, js):
-            for j in js:
-                make_dz(*units[m], j)
-
-        def flips_w2(c, u, ring=FLIP_BANKS):
-            flip_w2(c, u, 0, ring)
-            flip_w2(c, u, 1, ring)
-
-        def takes_w2(c, u, engines="ss"):
-            take_w2(c, u, 0, engines[0])
-            take_w2(c, u, 1, engines[1])
-
-        def flips_dz(b, c, js, ring=FLIP_BANKS):
-            for j in js:
-                flip_dz(b, c, j, ring)
-
-        def takes_dz(b, c, js, engine="s"):
-            for j in js:
-                take_dz(b, c, j, engine)
-
-        def pool_t(m):
-            group_t_share(*units[m], 0, POOL_SHARE // 2, "g")
-
-        def rest_t(m):
-            group_t_share(*units[m], POOL_SHARE // 2, 2 * P, "s")
-
-        def own_t(m, engines="vv"):
-            group_t(*units[m], 0, 2, engines[0], "rows")
-            group_t(*units[m], 2, 4, engines[1], "rows")
-
-        def rest_rows(what, i, name="pool"):
-            group_rows(what, i, POOL_SHARE, PASS, "s", name)
-
-        def q_t(m):
-            quantise(("t",) + units[m])
-
-        def q_h(b, c, half):
-            quantise(("h", b, c, half))
-
-        def dw(c, u, ms, ring=SUM_BANKS, engines="ssss", single=False):
-            for m in ms:
-                dw_passes(c, u, m, range(2), ring)
-                leave_dw(c, u, m, engines[m], single)
-
-        def whole_t(m, engine):
-            group_t_share(*units[m], 0, 2 * P, engine, "rows")
-
+        load_w2(0, 0, 1)
+        load_g(0, 0, 2)
+        load_w2(0, 1, 2)
+        load_g(0, 2, 4)
         load_x(0)
+        load_pre(0, 0, 1)
+        load_w2(1)
+        load_pre(0, 1, 2)
+        load_pre(0, 2, 4)
+        flip("w2", 0, 0, 4)
+        load_g(1)
+        flip("g", 0, 0, 5)
         load_x(1)
-        load_w2_first(0)
-        load_w2_first(1)
-        load_g(0, 0, 4)
-        load_pre(0, 0, 0, 1)
-        load_w2(0, 1, 1)
-        load_pre(0, 0, 1, 1)
-        load_pre(0, 0, 2, 2)
-        load_g(1, 0, 4)
-        load_pre(1, 0, 0, 2)
-        load_pre(1, 0, 2, 2)
-        load_w2(1, 0, 2)
-        load_w1(0, 1)
-        load_pre(0, 1, 0, 2)
-        load_w1(2, 2)
-        group_rows("x", 0, 0, 512, "s", "rows")
-        group_rows("x", 1, 0, 512, "v", "rows")
-        flips_w2(0, 0)
-        flip_g_tile(0, 0)
-        flip_g_tile(0, 1)
-        takes_w2(0, 0)
-        flip_g(0, 1)
-        take_g_tile(0, 0, "s")
-        take_g_tile(0, 1, "s")
-        quantise(("x", 0))
-        quantise(("w2", 0, 0), 0, 256)
-        quantise(("x", 1))
-        quantise(("w2", 0, 0), 256, 512)
-        quantise(("g", 0), 0, 128)
-        dh(0, [0])
-        quantise(("g", 0), 128, 256)
-        dh(0, [1])
-        take_g(0, 1, "s")
-        dzs(0, [0])
-        flips_w2(0, 1)
+        take("w2", 0, 0)
+        load_pre(1, 0, 2)
+        flip("w2", 0, 1, 6)
+        quantise(("w2", 0), 0, 256)
+        take("g", 0, 0)
+        load_pre(1, 2, 4)
+        flip("g", 0, 1, 7)
+        quantise(("g", 0), 0, 256)
+        take("w2", 0, 1)
+        group_rows("x", 0, 0, 256, "v")
+        load_w2(2)
+        quantise(("w2", 0), 256, 512)
+        take("g", 0, 1)
+        group_rows("x", 0, 256, 512, "v")
+        make_dh(0, 0, 0)
+        load_w2(3)
         quantise(("g", 0), 256, 512)
-        dh(0, [2, 3])
-        takes_w2(0, 1)
-        dzs(0, [1])
-        quantise(("w2", 0, 1))
-        dh(1, [0, 1])
-        dzs(0, [2])
-        dh(1, [2])
-        dzs(0, [3])
-        dh(1, [3])
-        flip_g(1, 0)
-        flip_g(1, 1)
-        pool_t(0)
-        rest_t(0)
-        take_g(1, 0, "s")
-        take_g(1, 1, "s")
-        dzs(1, J)
-        load_pre(0, 1, 2, 2)
-        load_w1(1, 1)
-        flips_dz(0, 0, J)
+        make_dh(0, 1, 1)
+        make_dz(0, 0)
+        flip("w2", 1, 0, 4)
+        quantise(("x", 0))
+        load_w1(0)
+        flip("w2", 1, 1, 5)
+        make_dz(0, 1)
+        take("w2", 1, 0)
+        make_dh(0, 2, 2)
+        take("w2", 1, 1)
+        make_dh(0, 3, 3)
+        quantise(("w2", 1))
+        load_pre(2, 0, 2)
+        make_dz(0, 2)
+        make_dh(1, 0, 0)
+        make_dh(1, 1, 1)
+        make_dz(0, 3)
+        make_dh(1, 2, 2)
+        load_w1(2)
+        make_dz(1, 0)
+        make_dh(1, 3, 3)
+        group_t(0, 176, 256, "s")
+        group_t(0, 0, 176, "g")
+        flip("g", 1, 0, 6)
+        make_dz(1, 1)
+        load_w1(3)
+        flip("g", 1, 1, 7)
+        make_dz(1, 2)
+        take("g", 1, 0)
+        flip("h", 0, 0, 4)
+        make_dz(1, 3)
+        flip("h", 0, 1, 5)
+        take("g", 1, 1)
+        flip("h", 1, 0, 6)
+        group_rows("x", 1, 0, 256, "s")
         quantise(("g", 1), 0, 256)
-        takes_dz(0, 0, [0, 1])
-        dh(2, [0, 1])
+        flip("h", 1, 1, 7)
         quantise(("g", 1), 256, 512)
-        dh(2, [2, 3])
-        q_t(0)
-        pool_t(1)
-        takes_dz(0, 0, [2, 3])
-        rest_t(1)
-        dzs(2, J)
-        dh(3, J)
-        flips_w2(1, 0)
-        q_h(0, 0, 0)
-        own_t(2, "vs")
-        takes_w2(1, 0)
-        q_h(0, 0, 1)
-        q_t(2)
-        flips_w2(1, 1)
-        q_t(1)
-        pool_rows("w1", 0, POOL_SHARE)
-        takes_w2(1, 1)
-        rest_rows("w1", 0)
-        dzs(3, [3, 0, 1, 2])
-        load_pre(1, 1, 0, 2)
-        load_pre(1, 1, 2, 2)
-        dw(0, 0, [0, 2, 1], (4, 5, 6, 7))
-        dw_passes(0, 0, 3, range(2), (4, 5, 6, 7))
-        group_t(*units[3], 2, 4, "s", "rows")
-        leave_dw(0, 0, 3, "s")
-        quantise(("w2", 1, 0))
-        flips_dz(1, 0, [0, 1], (4, 5, 6, 7))
-        dh(4, J)
-        flips_dz(1, 0, [2, 3], (4, 5, 6, 7))
-        group_t(*units[3], 0, 2, "v", "rows")
-        quantise(("w2", 1, 1))
-        takes_dz(1, 0, [0, 1])
-        q_t(3)
+        quantise(("t", 0))
+        load_pre(2, 2, 4)
+        make_dh(2, 0, 0)
+        take("h", 0, 0)
+        make_dh(2, 1, 1)
+        group_t(1, 0, 176, "g")
+        make_dz(2, 0)
+        take("h", 0, 1)
+        make_dh(2, 2, 2)
+        make_dz(2, 1)
+        take("h", 1, 0)
+        make_dh(2, 3, 3)
+        make_dh(3, 0, 0)
+        take("h", 1, 1, "v")
+        group_t(1, 176, 256, "s")
+        load_w1(1)
+        make_dh(3, 1, 1)
+        make_dz(2, 2)
+        group_rows("x", 1, 256, 512, "s")
+        make_dz(2, 3)
+        make_dh(3, 2, 2)
+        load_pre(3, 0, 2)
+        quantise(("h", 0))
+        make_dh(3, 3, 3)
+        flip("w2", 2, 0, 4)
+        group_t(2, 128, 256, "s", "rows")
+        group_t(2, 0, 128, "v", "rows")
+        load_pre(3, 2, 4)
+        flip("w2", 2, 1, 5)
+        quantise(("h", 1))
+        flip("w2", 3, 0, 6)
+        quantise(("x", 1))
+        take("w2", 2, 0)
+        flip("w2", 3, 1, 7)
+        take("w2", 2, 1)
+        quantise(("t", 2))
+        dw_pass(0, 0, 4)
+        take("w2", 3, 0)
+        quantise(("t", 1))
+        dw_pass(2, 0)
+        take("w2", 3, 1)
+        dw_pass(0, 2, 5)
+        make_dz(3, 3)
+        group_rows("w1", 0, 0, 352, "g", "pool")
+        dw_pass(2, 2)
+        group_rows("w1", 0, 352, 512, "s", "pool")
+        dw_pass(0, 1, 6)
+        make_dz(3, 0)
+        dw_pass(2, 1)
+        dw_pass(0, 3, 7)
+        make_dz(3, 1)
+        leave("dw", 0, 0)
+        dw_pass(2, 3)
+        make_dz(3, 2)
+        leave("dw", 0, 2)
+        flip("h", 2, 0, 4)
+        quantise(("w2", 2))
+        leave("dw", 0, 1)
+        flip("h", 2, 1, 5)
+        store("dw", 0, 0)
+        group_t(3, 0, 128, "v", "rows")
+        group_t(3, 128, 256, "s", "rows")
+        make_dh(4, 0, 0)
+        make_dh(4, 1, 1)
+        quantise(("w2", 3))
+        make_dh(4, 2, 2)
+        make_dh(4, 3, 3)
+        flip("h", 3, 0, 6)
+        leave("dw", 0, 3)
+        quantise(("t", 3))
+        take("h", 2, 0)
+        flip("h", 3, 1, 7)
+        store("dw", 0, 1)
         quantise(("w1", 0))
-        pool_rows("w1", 2, POOL_SHARE)
-        pool_rows("w1", 1, POOL_SHARE, "rows")
-        takes_dz(1, 0, [2, 3])
-        dw(0, 1, [0, 2], (4, 5, 6, 7))
-        dzs(4, [3, 2])
-        dh(5, [3, 2])
-        rest_rows("w1", 1, "rows")
-        dw(0, 1, [1, 3], (4, 5, 6, 7))
-        dzs(4, [0, 1])
-        dh(5, [0, 1])
-        group_rows("w1", 3, 0, 256, "s", "rows")
-        for j in range(2):
-            dx_passes(0, j, [0], (4, 5, 6, 7))
-        dzs(5, [3, 2])
-        flips_dz(0, 1, [3], DH_BANKS[3:])
-        flips_dz(0, 1, [2], DH_BANKS[2:3])
-        for j in range(2, 4):
-            dx_passes(0, j, [0], (4, 5, 6, 7))
-        takes_dz(0, 1, [3, 2])
-        dzs(5, [0, 1])
-        flips_dz(0, 1, [0, 1], DH_BANKS[:2])
-        takes_dz(0, 1, [0, 1])
-        rest_rows("w1", 2)
-        group_rows("w1", 3, 256, 512, "v", "rows")
+        take("h", 2, 1)
+        dw_pass(1, 0, 4)
+        make_dz(4, 3)
+        dw_pass(3, 0)
+        group_rows("w1", 2, 0, 352, "g", "pool")
+        take("h", 3, 0)
+        dw_pass(1, 2, 5)
+        make_dz(4, 2)
+        dw_pass(3, 2)
+        take("h", 3, 1)
+        make_dh(5, 3, 3)
+        make_dz(4, 0)
+        make_dh(5, 2, 2)
+        leave("dw", 1, 0)
+        dw_pass(1, 1, 6)
+        make_dz(4, 1)
+        dw_pass(3, 1)
+        leave("dw", 1, 2)
+        dw_pass(1, 3, 7)
+        make_dz(5, 3)
+        group_rows("w1", 1, 0, 352, "g", "rows")
+        dw_pass(3, 3)
+        group_rows("w1", 1, 352, 512, "s")
+        make_dh(5, 0, 0)
+        store("dw", 1, 0)
+        make_dz(5, 2)
+        make_dh(5, 1, 1)
+        dx_pass(0, 0, 0, 4)
+        leave("dw", 1, 1)
+        make_dz(5, 0)
+        dx_pass(0, 1, 0, 5)
+        leave("dw", 1, 3)
+        flip("h", 5, 1, 3)
+        make_dz(5, 1)
+        flip("h", 5, 0, 2)
+        group_rows("w1", 3, 0, 256, "s")
+        group_rows("w1", 3, 256, 512, "v")
+        dx_pass(0, 2, 0, 6)
+        store("dw", 1, 1)
+        dx_pass(0, 3, 0, 7)
         quantise(("w1", 1))
-        for j in range(4):
-            dx_passes(0, j, [1])
-        dh(6, [3, 2, 0, 1])
-        q_h(1, 0, 0)
+        flip("h", 4, 0, 0)
+        flip("h", 4, 1, 1)
+        take("h", 5, 1)
+        quantise(("h", 2))
+        dx_pass(0, 0, 1)
+        take("h", 5, 0)
         quantise(("w1", 3))
-        q_h(0, 1, 1)
-        q_h(0, 1, 0)
-        q_h(1, 0, 1)
+        dx_pass(0, 1, 1)
+        dx_pass(0, 2, 1)
+        take("h", 4, 0)
+        dx_pass(0, 3, 1)
+        quantise(("h", 5))
+        make_dh(6, 3, 3)
+        take("h", 4, 1)
+        make_dh(6, 2, 2)
+        make_dh(6, 0, 0)
+        group_rows("w1", 2, 352, 512, "s", "pool")
+        make_dh(6, 1, 1)
+        quantise(("h", 4))
+        dx_pass(0, 2, 3)
+        dx_pass(0, 3, 3)
+        group_t(5, 0, 128, "s", "rows")
+        quantise(("h", 3))
+        dx_pass(0, 0, 3)
+        dx_pass(0, 1, 3)
         quantise(("w1", 2))
-        group_t_share(*units[5], 0, POOL_SHARE // 2, "g")
-        group_t(*units[4], 0, 2, "s", "rows")
-        for j in (2, 3, 0, 1):
-            dx_passes(0, j, [3])
-        for j in range(4):
-            dx_passes(0, j, [2])
-        dzs(6, [1, 0])
-        dh(7, [1, 0])
-        leave_dx(0, 0, "s")
-        leave_dx(0, 1, "s")
-        dx_passes(1, 0, range(2), (4, 5, 6, 7))
-        dzs(6, [2, 3])
-        dh(7, [2, 3])
-        dx_passes(1, 1, range(2), (4, 5, 6, 7))
-        leave_dx(0, 2, "s")
-        leave_dx(0, 3, "s")
-        group_t(*units[4], 2, 4, "s", "rows")
-        group_t_share(*units[6], 0, POOL_SHARE // 2, "g", "rows")
-        group_t_share(*units[6], POOL_SHARE // 2, 2 * P, "s", "rows")
-        dzs(7, [1, 0])
-        flips_dz(1, 1, [1], DH_BANKS[1:2])
-        flips_dz(1, 1, [0], DH_BANKS[:1])
-        takes_dz(1, 1, [1, 0])
-        dx_passes(1, 2, range(2), (7,))
-        dzs(7, [2, 3])
-        flips_dz(1, 1, [2, 3], DH_BANKS[2:])
-        q_t(4)
-        for m in (0, 2):
-            dw_passes(1, 0, m, [0], (4, 1, 0, 2))
-        q_t(6)
-        takes_dz(1, 1, [2])
-        for m in (0, 2):
-            dw_passes(1, 0, m, [1])
-        leave_dw(1, 0, 0, "s", True)
-        leave_dw(1, 0, 2, "s", True)
-        for m in (1, 3):
-            dw_passes(1, 0, m, range(2), (4, 1, 0, 2))
-        q_h(1, 1, 0)
-        takes_dz(1, 1, [3], "v")
-        for j in range(2):
-            dx_passes(1, j, [2, 3])
-        whole_t(7, "v")
-        group_t_share(*units[5], POOL_SHARE // 2, 2 * P, "v")
-        q_h(1, 1, 1)
-        for m in (1, 3):
-            leave_dw(1, 0, m, "s", True)
-        dx_passes(1, 3, range(2), (3,))
-        for j in range(2, 4):
-            dx_passes(1, j, [2, 3])
-        q_t(5)
-        q_t(7)
-        for m in (0, 2, 1, 3):
-            dw_passes(1, 1, m, range(2), (4, 1, 0, 2))
-        leave_dx(1, 0, "s", True)
-        leave_dx(1, 1, "s", True)
-        leave_dx(1, 2, "s", True)
-        leave_dx(1, 3, "v", True)
-        leave_dw(1, 1, 0, "s", True)
-        leave_dw(1, 1, 2, "v", True)
-        leave_dw(1, 1, 1, "s", True)
-        leave_dw(1, 1, 3, "v", True)
+        make_dz(6, 1)
+        group_t(4, 0, 176, "g")
+        group_t(4, 176, 256, "s")
+        dx_pass(0, 0, 2)
+        dx_pass(0, 1, 2)
+        make_dz(6, 0)
+        dx_pass(0, 2, 2)
+        leave("dx", 0, 0)
+        dx_pass(0, 3, 2)
+        make_dz(6, 2)
+        make_dh(7, 1, 1)
+        make_dh(7, 0, 0)
+        leave("dx", 0, 1)
+        make_dz(6, 3)
+        dx_pass(1, 0, 0, 4)
+        dx_pass(1, 0, 1)
+        leave("dx", 0, 2)
+        make_dz(7, 1)
+        make_dh(7, 2, 2)
+        store("dx", 0, 0)
+        group_t(6, 0, 176, "g", "rows")
+        make_dh(7, 3, 3)
+        make_dz(7, 0)
+        group_t(6, 176, 256, "s", "rows")
+        dx_pass(1, 1, 0, 5)
+        dx_pass(1, 1, 1)
+        make_dz(7, 2)
+        leave("dx", 0, 3)
+        flip("h", 6, 1, 1)
+        make_dz(7, 3)
+        flip("h", 6, 0, 0)
+        take("h", 6, 1)
+        dx_pass(1, 2, 0, 6)
+        store("dx", 0, 1)
+        dx_pass(1, 2, 1)
+        quantise(("t", 4))
+        take("h", 6, 0)
+        flip("h", 7, 0, 2)
+        group_t(5, 128, 256, "s", "rows")
+        quantise(("t", 6))
+        flip("h", 7, 1, 3)
+        dw_pass(4, 0, 7)
+        quantise(("h", 6))
+        dw_pass(4, 2, 1)
+        dw_pass(6, 0)
+        take("h", 7, 1, "v")
+        dw_pass(6, 2)
+        take("h", 7, 0)
+        dw_pass(4, 1, 0)
+        quantise(("t", 5))
+        dw_pass(6, 1)
+        leave("dw", 2, 0)
+        dw_pass(4, 3, 2)
+        group_t(7, 0, 256, "v", "rows")
+        dw_pass(6, 3)
+        leave("dw", 2, 2)
+        dx_pass(1, 0, 2)
+        store("dw", 2, 0, 0, 1)
+        dx_pass(1, 0, 3)
+        leave("dw", 2, 1)
+        dx_pass(1, 1, 2)
+        store("dw", 2, 0, 1, 2)
+        dx_pass(1, 1, 3)
+        leave("dw", 2, 3)
+        dx_pass(1, 3, 0, 3)
+        quantise(("h", 7))
+        store("dw", 2, 1, 0, 1)
+        dx_pass(1, 3, 1)
+        leave("dx", 1, 0)
+        dw_pass(5, 0, 7)
+        quantise(("t", 7))
+        store("dw", 2, 1, 1, 2)
+        dw_pass(5, 2, 1)
+        leave("dx", 1, 1)
+        dx_pass(1, 2, 2)
+        store("dx", 1, 0, 0, 1)
+        dx_pass(1, 2, 3)
+        dx_pass(1, 3, 2)
+        store("dx", 1, 0, 1, 2)
+        dx_pass(1, 3, 3)
+        leave("dx", 1, 2)
+        dw_pass(7, 0)
+        dw_pass(7, 2)
+        leave("dx", 1, 3, "v")
+        dw_pass(5, 1, 0)
+        leave("dw", 3, 0)
+        store("dx", 1, 1, 0, 1)
+        dw_pass(7, 1)
+        leave("dw", 3, 2, "v")
+        dw_pass(5, 3, 2)
+        store("dx", 1, 1, 1, 2)
+        dw_pass(7, 3)
+        leave("dw", 3, 1)
+        store("dw", 3, 0, 0, 1)
+        store("dw", 3, 0, 1, 2)
+        leave("dw", 3, 3, "v")
+        store("dw", 3, 1, 0, 1)
+        store("dw", 3, 1, 1, 2)

@@ -228,309 +228,307 @@ def tile_mlp_v_kernel(tc, x, w1, w2, pre, grad_out, out_0, out_1):
             src = staged[what, i, pair][:].rearrange("p (f d) -> p f d", f=2)
             nc.sync.dma_start(out=rows[:, lo:hi, :], in_=src[:, lo:hi, :])
 
-        load_w2(0, 0, 1)
-        load_g(0, 0, 2)
-        load_w2(0, 1, 2)
-        load_g(0, 2, 4)
         load_x(0)
+        load_w2(0, 0, 1)
+        load_w2(0, 1, 2)
+        load_g(0)
+        load_x(1)
         load_pre(0, 0, 1)
         load_w2(1)
         load_pre(0, 1, 2)
-        load_pre(0, 2, 4)
+        load_pre(0, 2, 3)
+        group_rows("x", 0, 0, 512, "s")
+        load_pre(0, 3, 4)
         flip("w2", 0, 0, 4)
         load_g(1)
-        flip("g", 0, 0, 5)
-        load_x(1)
-        take("w2", 0, 0)
+        flip("w2", 0, 1, 5)
+        take("w2", 0, 0, "v")
+        take("w2", 0, 1, "v")
         load_pre(1, 0, 2)
-        flip("w2", 0, 1, 6)
-        quantise(("w2", 0), 0, 256)
-        take("g", 0, 0)
-        load_pre(1, 2, 4)
+        flip("g", 0, 0, 6)
+        quantise(("w2", 0))
         flip("g", 0, 1, 7)
-        quantise(("g", 0), 0, 256)
-        take("w2", 0, 1)
-        group_rows("x", 0, 0, 256, "v")
-        load_w2(2)
-        quantise(("w2", 0), 256, 512)
-        take("g", 0, 1)
-        group_rows("x", 0, 256, 512, "v")
-        make_dh(0, 0, 0)
-        load_w2(3)
-        quantise(("g", 0), 256, 512)
-        make_dh(0, 1, 1)
-        make_dz(0, 0)
-        flip("w2", 1, 0, 4)
+        take("g", 0, 0)
         quantise(("x", 0))
-        load_w1(0)
+        load_pre(1, 2, 3)
+        take("g", 0, 1)
+        quantise(("g", 0), 0, 256)
+        group_rows("x", 1, 0, 512, "v")
+        load_pre(1, 3, 4)
+        make_dh(0, 0, 0)
+        make_dh(0, 1, 1)
+        quantise(("g", 0), 256, 512)
+        load_w2(2)
+        flip("w2", 1, 0, 4)
+        make_dz(0, 0)
         flip("w2", 1, 1, 5)
-        make_dz(0, 1)
+        quantise(("x", 1))
         take("w2", 1, 0)
+        load_w2(3)
+        make_dz(0, 1)
         make_dh(0, 2, 2)
         take("w2", 1, 1)
         make_dh(0, 3, 3)
+        load_w1(0)
         quantise(("w2", 1))
-        load_pre(2, 0, 2)
         make_dz(0, 2)
         make_dh(1, 0, 0)
         make_dh(1, 1, 1)
+        load_pre(2, 2, 4)
         make_dz(0, 3)
         make_dh(1, 2, 2)
-        load_w1(2)
         make_dz(1, 0)
         make_dh(1, 3, 3)
         group_t(0, 176, 256, "s")
         group_t(0, 0, 176, "g")
-        flip("g", 1, 0, 6)
+        load_w1(2)
         make_dz(1, 1)
-        load_w1(3)
-        flip("g", 1, 1, 7)
+        flip("g", 1, 0, 6)
         make_dz(1, 2)
+        flip("g", 1, 1, 7)
         take("g", 1, 0)
-        flip("h", 0, 0, 4)
         make_dz(1, 3)
+        flip("h", 0, 0, 4)
         flip("h", 0, 1, 5)
         take("g", 1, 1)
         flip("h", 1, 0, 6)
-        group_rows("x", 1, 0, 256, "s")
         quantise(("g", 1), 0, 256)
-        flip("h", 1, 1, 7)
-        quantise(("g", 1), 256, 512)
-        quantise(("t", 0))
-        load_pre(2, 2, 4)
-        make_dh(2, 0, 0)
         take("h", 0, 0)
-        make_dh(2, 1, 1)
-        group_t(1, 0, 176, "g")
-        make_dz(2, 0)
+        flip("h", 1, 1, 7)
+        load_pre(2, 0, 2)
+        quantise(("g", 1), 256, 512)
+        make_dh(2, 0, 0)
+        quantise(("t", 0))
         take("h", 0, 1)
-        make_dh(2, 2, 2)
-        make_dz(2, 1)
+        make_dh(2, 1, 1)
         take("h", 1, 0)
-        make_dh(2, 3, 3)
-        make_dh(3, 0, 0)
-        take("h", 1, 1, "v")
-        group_t(1, 176, 256, "s")
+        group_t(1, 0, 176, "g")
         load_w1(1)
-        make_dh(3, 1, 1)
+        make_dz(2, 0)
+        make_dh(2, 2, 2)
+        take("h", 1, 1)
+        make_dz(2, 1)
+        make_dh(2, 3, 3)
+        group_t(1, 176, 256, "s")
+        make_dh(3, 0, 0)
         make_dz(2, 2)
-        group_rows("x", 1, 256, 512, "s")
+        load_w1(3)
+        make_dh(3, 1, 1)
         make_dz(2, 3)
         make_dh(3, 2, 2)
-        load_pre(3, 0, 2)
         quantise(("h", 0))
         make_dh(3, 3, 3)
-        flip("w2", 2, 0, 4)
+        load_pre(3, 0, 2)
         group_t(2, 128, 256, "s", "rows")
+        flip("w2", 2, 0, 4)
         group_t(2, 0, 128, "v", "rows")
-        load_pre(3, 2, 4)
         flip("w2", 2, 1, 5)
         quantise(("h", 1))
+        load_pre(3, 2, 4)
         flip("w2", 3, 0, 6)
-        quantise(("x", 1))
         take("w2", 2, 0)
         flip("w2", 3, 1, 7)
-        take("w2", 2, 1)
         quantise(("t", 2))
+        take("w2", 2, 1)
         dw_pass(0, 0, 4)
-        take("w2", 3, 0)
         quantise(("t", 1))
+        take("w2", 3, 0)
         dw_pass(2, 0)
-        take("w2", 3, 1)
-        dw_pass(0, 2, 5)
         make_dz(3, 3)
         group_rows("w1", 0, 0, 352, "g", "pool")
-        dw_pass(2, 2)
-        group_rows("w1", 0, 352, 512, "s", "pool")
-        dw_pass(0, 1, 6)
+        take("w2", 3, 1)
+        dw_pass(0, 2, 5)
         make_dz(3, 0)
-        dw_pass(2, 1)
-        dw_pass(0, 3, 7)
+        group_rows("w1", 0, 352, 512, "s", "pool")
+        dw_pass(2, 2)
         make_dz(3, 1)
-        leave("dw", 0, 0)
-        dw_pass(2, 3)
+        dw_pass(0, 1, 6)
         make_dz(3, 2)
+        dw_pass(2, 1)
+        leave("dw", 0, 0)
+        dw_pass(0, 3, 7)
+        dw_pass(2, 3)
+        quantise(("w2", 2))
         leave("dw", 0, 2)
         flip("h", 2, 0, 4)
-        quantise(("w2", 2))
-        leave("dw", 0, 1)
+        group_t(3, 0, 160, "v", "rows")
+        group_t(3, 160, 256, "s", "rows")
         flip("h", 2, 1, 5)
         store("dw", 0, 0)
-        group_t(3, 0, 128, "v", "rows")
-        group_t(3, 128, 256, "s", "rows")
         make_dh(4, 0, 0)
-        make_dh(4, 1, 1)
         quantise(("w2", 3))
+        make_dh(4, 1, 1)
         make_dh(4, 2, 2)
+        leave("dw", 0, 1)
         make_dh(4, 3, 3)
-        flip("h", 3, 0, 6)
-        leave("dw", 0, 3)
         quantise(("t", 3))
+        leave("dw", 0, 3)
+        flip("h", 3, 0, 6)
+        quantise(("w1", 0))
         take("h", 2, 0)
         flip("h", 3, 1, 7)
+        make_dz(4, 3)
         store("dw", 0, 1)
-        quantise(("w1", 0))
+        group_rows("w1", 2, 0, 352, "g", "pool")
         take("h", 2, 1)
         dw_pass(1, 0, 4)
-        make_dz(4, 3)
-        dw_pass(3, 0)
-        group_rows("w1", 2, 0, 352, "g", "pool")
-        take("h", 3, 0)
-        dw_pass(1, 2, 5)
         make_dz(4, 2)
-        dw_pass(3, 2)
-        take("h", 3, 1)
-        make_dh(5, 3, 3)
+        dw_pass(3, 0)
+        take("h", 3, 0, "s", "late")
         make_dz(4, 0)
+        dw_pass(1, 2, 5)
+        dw_pass(3, 2)
+        take("h", 3, 1, "s", "late")
+        make_dh(5, 3, 3)
+        make_dz(4, 1)
         make_dh(5, 2, 2)
         leave("dw", 1, 0)
         dw_pass(1, 1, 6)
-        make_dz(4, 1)
-        dw_pass(3, 1)
-        leave("dw", 1, 2)
-        dw_pass(1, 3, 7)
         make_dz(5, 3)
         group_rows("w1", 1, 0, 352, "g", "rows")
-        dw_pass(3, 3)
-        group_rows("w1", 1, 352, 512, "s")
-        make_dh(5, 0, 0)
-        store("dw", 1, 0)
+        dw_pass(3, 1)
+        dw_pass(1, 3, 7)
         make_dz(5, 2)
+        leave("dw", 1, 2)
+        dw_pass(3, 3)
+        make_dh(5, 0, 0)
+        group_rows("w1", 1, 352, 512, "s")
         make_dh(5, 1, 1)
+        store("dw", 1, 0)
         dx_pass(0, 0, 0, 4)
-        leave("dw", 1, 1)
         make_dz(5, 0)
         dx_pass(0, 1, 0, 5)
-        leave("dw", 1, 3)
-        flip("h", 5, 1, 3)
         make_dz(5, 1)
+        leave("dw", 1, 1)
+        flip("h", 5, 1, 3)
         flip("h", 5, 0, 2)
-        group_rows("w1", 3, 0, 256, "s")
         group_rows("w1", 3, 256, 512, "v")
+        leave("dw", 1, 3)
         dx_pass(0, 2, 0, 6)
-        store("dw", 1, 1)
-        dx_pass(0, 3, 0, 7)
         quantise(("w1", 1))
+        group_rows("w1", 3, 0, 256, "s")
+        dx_pass(0, 3, 0, 7)
+        store("dw", 1, 1)
         flip("h", 4, 0, 0)
-        flip("h", 4, 1, 1)
-        take("h", 5, 1)
         quantise(("h", 2))
+        flip("h", 4, 1, 1)
         dx_pass(0, 0, 1)
-        take("h", 5, 0)
-        quantise(("w1", 3))
         dx_pass(0, 1, 1)
-        dx_pass(0, 2, 1)
-        take("h", 4, 0)
-        dx_pass(0, 3, 1)
-        quantise(("h", 5))
-        make_dh(6, 3, 3)
-        take("h", 4, 1)
-        make_dh(6, 2, 2)
-        make_dh(6, 0, 0)
         group_rows("w1", 2, 352, 512, "s", "pool")
+        dx_pass(0, 2, 1)
+        quantise(("w1", 3))
+        dx_pass(0, 3, 1)
+        take("h", 5, 1)
+        quantise(("w1", 2))
+        take("h", 5, 0)
+        make_dh(6, 3, 3)
+        take("h", 4, 0)
+        make_dh(6, 2, 2)
+        quantise(("h", 5))
+        take("h", 4, 1)
+        make_dh(6, 0, 0)
+        group_t(4, 0, 128, "s", "rows")
         make_dh(6, 1, 1)
         quantise(("h", 4))
         dx_pass(0, 2, 3)
-        dx_pass(0, 3, 3)
-        group_t(5, 0, 128, "s", "rows")
-        quantise(("h", 3))
-        dx_pass(0, 0, 3)
-        dx_pass(0, 1, 3)
-        quantise(("w1", 2))
-        make_dz(6, 1)
-        group_t(4, 0, 176, "g")
-        group_t(4, 176, 256, "s")
-        dx_pass(0, 0, 2)
-        dx_pass(0, 1, 2)
-        make_dz(6, 0)
         dx_pass(0, 2, 2)
-        leave("dx", 0, 0)
+        quantise(("h", 3))
+        dx_pass(0, 3, 3)
         dx_pass(0, 3, 2)
+        make_dz(6, 1)
+        dx_pass(0, 0, 3)
+        group_t(5, 0, 176, "g", "late")
+        leave("dx", 0, 2)
+        dx_pass(0, 0, 2)
+        make_dz(6, 0)
+        dx_pass(0, 1, 3)
+        leave("dx", 0, 3)
+        dx_pass(0, 1, 2)
         make_dz(6, 2)
         make_dh(7, 1, 1)
         make_dh(7, 0, 0)
-        leave("dx", 0, 1)
+        leave("dx", 0, 0)
         make_dz(6, 3)
-        dx_pass(1, 0, 0, 4)
+        dx_pass(1, 0, 0, 6)
+        store("dx", 0, 1)
         dx_pass(1, 0, 1)
-        leave("dx", 0, 2)
-        make_dz(7, 1)
+        leave("dx", 0, 1)
         make_dh(7, 2, 2)
-        store("dx", 0, 0)
-        group_t(6, 0, 176, "g", "rows")
+        make_dz(7, 1)
         make_dh(7, 3, 3)
+        group_t(6, 0, 176, "g", "rows")
+        group_t(4, 128, 256, "s", "rows")
+        dx_pass(1, 1, 0, 7)
         make_dz(7, 0)
-        group_t(6, 176, 256, "s", "rows")
-        dx_pass(1, 1, 0, 5)
+        store("dx", 0, 0)
         dx_pass(1, 1, 1)
         make_dz(7, 2)
-        leave("dx", 0, 3)
         flip("h", 6, 1, 1)
-        make_dz(7, 3)
         flip("h", 6, 0, 0)
-        take("h", 6, 1)
-        dx_pass(1, 2, 0, 6)
-        store("dx", 0, 1)
+        make_dz(7, 3)
+        dx_pass(1, 2, 0, 4)
+        group_t(6, 176, 256, "s", "rows")
         dx_pass(1, 2, 1)
         quantise(("t", 4))
-        take("h", 6, 0)
         flip("h", 7, 0, 2)
-        group_t(5, 128, 256, "s", "rows")
-        quantise(("t", 6))
         flip("h", 7, 1, 3)
-        dw_pass(4, 0, 7)
-        quantise(("h", 6))
+        take("h", 6, 1)
+        quantise(("t", 6))
+        dw_pass(4, 0, 5)
+        take("h", 6, 0)
         dw_pass(4, 2, 1)
+        group_t(5, 176, 256, "v", "late")
         dw_pass(6, 0)
-        take("h", 7, 1, "v")
-        dw_pass(6, 2)
         take("h", 7, 0)
+        dw_pass(6, 2)
+        quantise(("h", 6))
         dw_pass(4, 1, 0)
-        quantise(("t", 5))
-        dw_pass(6, 1)
         leave("dw", 2, 0)
+        dw_pass(6, 1)
+        take("h", 7, 1, "v")
         dw_pass(4, 3, 2)
-        group_t(7, 0, 256, "v", "rows")
-        dw_pass(6, 3)
         leave("dw", 2, 2)
-        dx_pass(1, 0, 2)
+        dw_pass(6, 3)
+        group_t(7, 0, 256, "v", "rows")
         store("dw", 2, 0, 0, 1)
-        dx_pass(1, 0, 3)
+        dx_pass(1, 0, 2)
         leave("dw", 2, 1)
-        dx_pass(1, 1, 2)
+        dx_pass(1, 0, 3)
         store("dw", 2, 0, 1, 2)
+        dx_pass(1, 1, 2)
         dx_pass(1, 1, 3)
         leave("dw", 2, 3)
         dx_pass(1, 3, 0, 3)
-        quantise(("h", 7))
         store("dw", 2, 1, 0, 1)
+        quantise(("h", 7))
         dx_pass(1, 3, 1)
         leave("dx", 1, 0)
-        dw_pass(5, 0, 7)
-        quantise(("t", 7))
         store("dw", 2, 1, 1, 2)
-        dw_pass(5, 2, 1)
-        leave("dx", 1, 1)
+        quantise(("t", 5))
         dx_pass(1, 2, 2)
-        store("dx", 1, 0, 0, 1)
+        leave("dx", 1, 1)
         dx_pass(1, 2, 3)
+        store("dx", 1, 0, 0, 1)
+        quantise(("t", 7))
         dx_pass(1, 3, 2)
-        store("dx", 1, 0, 1, 2)
         dx_pass(1, 3, 3)
         leave("dx", 1, 2)
+        store("dx", 1, 0, 1, 2)
+        dw_pass(5, 0, 5)
         dw_pass(7, 0)
-        dw_pass(7, 2)
         leave("dx", 1, 3, "v")
-        dw_pass(5, 1, 0)
-        leave("dw", 3, 0)
+        dw_pass(5, 2, 1)
         store("dx", 1, 1, 0, 1)
+        dw_pass(7, 2)
+        leave("dw", 3, 0)
+        dw_pass(5, 1, 0)
+        store("dx", 1, 1, 1, 2)
         dw_pass(7, 1)
         leave("dw", 3, 2, "v")
         dw_pass(5, 3, 2)
-        store("dx", 1, 1, 1, 2)
+        store("dw", 3, 0, 0, 1)
         dw_pass(7, 3)
         leave("dw", 3, 1)
-        store("dw", 3, 0, 0, 1)
         store("dw", 3, 0, 1, 2)
         leave("dw", 3, 3, "v")
         store("dw", 3, 1, 0, 1)

@@ -21,6 +21,8 @@ COPY = mybir.ActivationFunctionType.Copy
 
 PAIRS = ((0, 0), (1, 0), (0, 1), (1, 1))
 SLABS = 12
+WHOLE = (('dw', 0), ('dw', 1), ('dx', 0))
+BIG_BUFS = 1
 PRE_BUFS = 6
 DZ_BUFS = 4
 GROUP_BUFS = {"words": 4, "rows": 4, "pool": 1, "late": 1, "held": 1}
@@ -85,9 +87,26 @@ def tile_mlp_v_kernel(tc, x, w1, w2, pre, grad_out, out_0, out_1):
             for s in range(lo, hi):
                 raw["w2", i, s] = tile[:, 2 * DIM * (s - lo) : 2 * DIM * (s - lo + 1)]
 
+        def load_w2_half(c):
+            tile = stream.tile([P, 8 * DIM], BF16, name="pre", bufs=PRE_BUFS)
+            rows = w2[HALF * c : HALF * c + HALF, :].rearrange("(s p t) d -> p s t d", s=2, t=4)
+            nc.sync.dma_start(out=tile[:].rearrange("p (s t d) -> p s t d", t=4, d=DIM), in_=rows)
+            for u in range(2):
+                for s in range(2):
+                    raw["w2", 2 * c + u, s] = tile[:, DIM * (4 * s + 2 * u) : DIM * (4 * s + 2 * u + 2)]
+
+        def load_w1_pair(q):
+            tile = stream.tile([P, 8 * DIM], BF16, name="pre", bufs=PRE_BUFS)
+            rows = w1[PASS * q : PASS * (q + 2), :].rearrange("(q p t) d -> p q t d", q=2, t=4)
+            nc.sync.dma_start(out=tile[:].rearrange("p (q t d) -> p q t d", t=4, d=DIM), in_=rows)
+            for i in range(2):
+                raw["w1", q + i] = tile[:, 4 * DIM * i : 4 * DIM * (i + 1)]
+
         def load_pre(pair, lo, hi):
             b, c = PAIRS[pair]
-            if hi - lo == 2:
+            if hi - lo == 4:
+                tile = stream.tile([P, 4 * HALF], F32, name="big", bufs=BIG_BUFS)
+            elif hi - lo == 2:
                 tile = stream.tile([P, 2 * HALF], F32, name="pre", bufs=PRE_BUFS)
             else:
                 tile = slab(F32, HALF)
@@ -216,8 +235,23 @@ def tile_mlp_v_kernel(tc, x, w1, w2, pre, grad_out, out_0, out_1):
         def leave(what, i, tile, engine="s"):
             pair, side = divmod(tile, 2) if what == "dx" else (tile % 2, tile // 2)
             if (what, i, pair) not in staged:
-                staged[what, i, pair] = slab(F32, 2 * DIM)
+                if (what, i) in WHOLE:
+                    both = stream.tile([P, 4 * DIM], F32, name="pre", bufs=PRE_BUFS)
+                    staged[what, i] = both
+                    for k in range(2):
+                        staged[what, i, k] = both[:, 2 * DIM * k : 2 * DIM * (k + 1)]
+                else:
+                    staged[what, i, pair] = slab(F32, 2 * DIM)[:]
             copy_words(engine, staged[what, i, pair][:, DIM * side : DIM * side + DIM], banks[what, i, tile][:])
+
+        def store_all(what, i):
+            src = staged[what, i][:].rearrange("p (s f d) -> p s f d", s=2, f=2)
+            if what == "dx":
+                rows = out_0[i].rearrange("(p s f) d -> p s f d", s=2, f=2)
+            else:
+                rows = out_1[HALF * (i // 2) : HALF * (i // 2 + 1), :].rearrange("(s p f) d -> p s f d", s=2, f=4)
+                rows = rows[:, :, 2 * (i % 2) : 2 * (i % 2) + 2, :]
+            nc.sync.dma_start(out=rows, in_=src)
 
         def store(what, i, pair, lo=0, hi=2):
             if what == "dx":
@@ -225,7 +259,7 @@ def tile_mlp_v_kernel(tc, x, w1, w2, pre, grad_out, out_0, out_1):
             else:
                 first = HALF * (i // 2) + PASS * pair
                 rows = out_1[first : first + PASS, :].rearrange("(p f) d -> p f d", f=4)[:, 2 * (i % 2) : 2 * (i % 2) + 2, :]
-            src = staged[what, i, pair][:].rearrange("p (f d) -> p f d", f=2)
+            src = staged[what, i, pair].rearrange("p (f d) -> p f d", f=2)
             nc.sync.dma_start(out=rows[:, lo:hi, :], in_=src[:, lo:hi, :])
 
         load_x(0)
@@ -354,7 +388,6 @@ def tile_mlp_v_kernel(tc, x, w1, w2, pre, grad_out, out_0, out_1):
         group_t(3, 0, 160, "v", "rows")
         group_t(3, 160, 256, "s", "rows")
         flip("h", 2, 1, 5)
-        store("dw", 0, 0)
         make_dh(4, 0, 0)
         quantise(("w2", 3))
         make_dh(4, 1, 1)
@@ -368,7 +401,7 @@ def tile_mlp_v_kernel(tc, x, w1, w2, pre, grad_out, out_0, out_1):
         take("h", 2, 0)
         flip("h", 3, 1, 7)
         make_dz(4, 3)
-        store("dw", 0, 1)
+        store_all("dw", 0)
         group_rows("w1", 2, 0, 352, "g", "pool")
         take("h", 2, 1)
         dw_pass(1, 0, 4)
@@ -394,7 +427,6 @@ def tile_mlp_v_kernel(tc, x, w1, w2, pre, grad_out, out_0, out_1):
         make_dh(5, 0, 0)
         group_rows("w1", 1, 352, 512, "s")
         make_dh(5, 1, 1)
-        store("dw", 1, 0)
         dx_pass(0, 0, 0, 4)
         make_dz(5, 0)
         dx_pass(0, 1, 0, 5)
@@ -408,7 +440,7 @@ def tile_mlp_v_kernel(tc, x, w1, w2, pre, grad_out, out_0, out_1):
         quantise(("w1", 1))
         group_rows("w1", 3, 0, 256, "s")
         dx_pass(0, 3, 0, 7)
-        store("dw", 1, 1)
+        store_all("dw", 1)
         flip("h", 4, 0, 0)
         quantise(("h", 2))
         flip("h", 4, 1, 1)
@@ -450,7 +482,6 @@ def tile_mlp_v_kernel(tc, x, w1, w2, pre, grad_out, out_0, out_1):
         leave("dx", 0, 0)
         make_dz(6, 3)
         dx_pass(1, 0, 0, 6)
-        store("dx", 0, 1)
         dx_pass(1, 0, 1)
         leave("dx", 0, 1)
         make_dh(7, 2, 2)
@@ -460,7 +491,7 @@ def tile_mlp_v_kernel(tc, x, w1, w2, pre, grad_out, out_0, out_1):
         group_t(4, 128, 256, "s", "rows")
         dx_pass(1, 1, 0, 7)
         make_dz(7, 0)
-        store("dx", 0, 0)
+        store_all("dx", 0)
         dx_pass(1, 1, 1)
         make_dz(7, 2)
         flip("h", 6, 1, 1)
@@ -499,21 +530,19 @@ def tile_mlp_v_kernel(tc, x, w1, w2, pre, grad_out, out_0, out_1):
         dx_pass(1, 1, 3)
         leave("dw", 2, 3)
         dx_pass(1, 3, 0, 3)
-        store("dw", 2, 1, 0, 1)
         quantise(("h", 7))
         dx_pass(1, 3, 1)
         leave("dx", 1, 0)
-        store("dw", 2, 1, 1, 2)
+        store("dw", 2, 1)
         quantise(("t", 5))
         dx_pass(1, 2, 2)
         leave("dx", 1, 1)
         dx_pass(1, 2, 3)
-        store("dx", 1, 0, 0, 1)
         quantise(("t", 7))
         dx_pass(1, 3, 2)
         dx_pass(1, 3, 3)
         leave("dx", 1, 2)
-        store("dx", 1, 0, 1, 2)
+        store("dx", 1, 0)
         dw_pass(5, 0, 5)
         dw_pass(7, 0)
         leave("dx", 1, 3, "v")
@@ -526,10 +555,8 @@ def tile_mlp_v_kernel(tc, x, w1, w2, pre, grad_out, out_0, out_1):
         dw_pass(7, 1)
         leave("dw", 3, 2, "v")
         dw_pass(5, 3, 2)
-        store("dw", 3, 0, 0, 1)
         dw_pass(7, 3)
         leave("dw", 3, 1)
-        store("dw", 3, 0, 1, 2)
+        store("dw", 3, 0)
         leave("dw", 3, 3, "v")
-        store("dw", 3, 1, 0, 1)
-        store("dw", 3, 1, 1, 2)
+        store("dw", 3, 1)

@@ -432,8 +432,6 @@ def tile_mlp_v_kernel(tc, x, w1, w2, pre, grad_out, out_0, out_1):
         dx_pass(0, 1, 0, 5)
         make_dz(5, 1)
         leave("dw", 1, 1)
-        flip("h", 5, 1, 3)
-        flip("h", 5, 0, 2)
         group_rows("w1", 3, 256, 512, "v")
         leave("dw", 1, 3)
         dx_pass(0, 2, 0, 6)
@@ -441,16 +439,18 @@ def tile_mlp_v_kernel(tc, x, w1, w2, pre, grad_out, out_0, out_1):
         group_rows("w1", 3, 0, 256, "s")
         dx_pass(0, 3, 0, 7)
         store_all("dw", 1)
-        flip("h", 4, 0, 0)
+        flip("h", 5, 1, 3)
         quantise(("h", 2))
+        flip("h", 5, 0, 2)
+        flip("h", 4, 0, 0)
         flip("h", 4, 1, 1)
+        group_rows("w1", 2, 352, 512, "s", "pool")
+        quantise(("w1", 3))
         dx_pass(0, 0, 1)
         dx_pass(0, 1, 1)
-        group_rows("w1", 2, 352, 512, "s", "pool")
         dx_pass(0, 2, 1)
-        quantise(("w1", 3))
-        dx_pass(0, 3, 1)
         take("h", 5, 1)
+        dx_pass(0, 3, 1)
         quantise(("w1", 2))
         take("h", 5, 0)
         make_dh(6, 3, 3)
@@ -514,46 +514,46 @@ def tile_mlp_v_kernel(tc, x, w1, w2, pre, grad_out, out_0, out_1):
         dw_pass(6, 2)
         quantise(("h", 6))
         dw_pass(4, 1, 0)
-        leave("dw", 2, 0)
+        take("h", 7, 1)
         dw_pass(6, 1)
-        take("h", 7, 1, "v")
-        dw_pass(4, 3, 2)
-        leave("dw", 2, 2)
-        dw_pass(6, 3)
         group_t(7, 0, 256, "v", "rows")
-        store("dw", 2, 0, 0, 1)
+        dw_pass(4, 3, 2)
+        leave("dw", 2, 0)
+        dw_pass(6, 3)
         dx_pass(1, 0, 2)
-        leave("dw", 2, 1)
+        leave("dw", 2, 2)
         dx_pass(1, 0, 3)
-        store("dw", 2, 0, 1, 2)
+        store("dw", 2, 0, 0, 1)
         dx_pass(1, 1, 2)
-        dx_pass(1, 1, 3)
-        leave("dw", 2, 3)
-        dx_pass(1, 3, 0, 3)
         quantise(("h", 7))
-        dx_pass(1, 3, 1)
-        leave("dx", 1, 0)
-        store("dw", 2, 1)
+        dx_pass(1, 1, 3)
+        leave("dw", 2, 1)
+        dx_pass(1, 3, 0, 3)
+        store("dw", 2, 0, 1, 2)
         quantise(("t", 5))
+        dx_pass(1, 3, 1)
+        leave("dw", 2, 3)
         dx_pass(1, 2, 2)
-        leave("dx", 1, 1)
-        dx_pass(1, 2, 3)
         quantise(("t", 7))
+        dx_pass(1, 2, 3)
+        leave("dx", 1, 0)
         dx_pass(1, 3, 2)
+        store("dw", 2, 1)
         dx_pass(1, 3, 3)
-        leave("dx", 1, 2)
-        store("dx", 1, 0)
+        leave("dx", 1, 1)
         dw_pass(5, 0, 5)
         dw_pass(7, 0)
         leave("dx", 1, 3, "v")
         dw_pass(5, 2, 1)
-        store("dx", 1, 1, 0, 1)
+        leave("dx", 1, 2)
         dw_pass(7, 2)
-        leave("dw", 3, 0)
+        store("dx", 1, 0)
         dw_pass(5, 1, 0)
-        store("dx", 1, 1, 1, 2)
+        leave("dw", 3, 0)
         dw_pass(7, 1)
         leave("dw", 3, 2, "v")
+        store("dx", 1, 1, 0, 1)
+        store("dx", 1, 1, 1, 2)
         dw_pass(5, 3, 2)
         dw_pass(7, 3)
         leave("dw", 3, 1)

@@ -20,12 +20,14 @@ MULT, ADD, MAX = mybir.AluOpType.mult, mybir.AluOpType.add, mybir.AluOpType.max
 COPY = mybir.ActivationFunctionType.Copy
 
 PAIRS = ((0, 0), (1, 0), (0, 1), (1, 1))
-SLABS = 12
-WHOLE = (('dw', 0), ('dw', 1), ('dx', 0))
-BIG_BUFS = 1
-PRE_BUFS = 6
+
+POOL_COLUMNS = 352
+UNIT3_VECTOR_COLUMNS = 320
+
+NARROW_BUFS = 12
+WIDE_BUFS = 6
 DZ_BUFS = 4
-GROUP_BUFS = {"words": 4, "rows": 4, "pool": 1, "late": 1, "held": 1}
+GROUPED_BUFS = {"words": 4, "rows": 4, "gate": 1, "last_gate": 1}
 
 
 def tile_mlp_v_kernel(tc, x, w1, w2, pre, grad_out, out_0, out_1):
@@ -41,115 +43,70 @@ def tile_mlp_v_kernel(tc, x, w1, w2, pre, grad_out, out_0, out_1):
 
         raw = {}
         grouped = {}
+        codes = {}
         dz = {}
         banks = {}
-        codes = {}
-        staged = {}
         passes = {}
+        staged = {}
 
         def bank(number, key):
             banks[key] = psum.tile([P, PASS], F32, name="bank%d" % number)
             return banks[key]
 
-        def slab(dtype, width):
-            return stream.tile([P, width], dtype, name="slab", bufs=SLABS)
+        def narrow(dtype, width):
+            return stream.tile([P, width], dtype, name="narrow", bufs=NARROW_BUFS)
 
-        def load_rows(what, i, src, lo, hi):
-            if hi - lo == 4:
-                tile = slab(BF16, 4 * DIM)
-            else:
-                tile = keep.tile([P, (hi - lo) * DIM], BF16, name="%s%d_rows%d" % (what, i, lo))
-            rows = src.rearrange("(p t) d -> p t d", t=4)[:, lo:hi, :]
-            nc.sync.dma_start(out=tile[:].rearrange("p (t d) -> p t d", d=DIM), in_=rows)
-            raw[what, i] = tile[:]
-            for half in range(lo // 2, hi // 2):
-                raw[what, i, half] = tile[:, DIM * (2 * half - lo) : DIM * (2 * half - lo + 2)]
+        def wide(dtype, width):
+            return stream.tile([P, width], dtype, name="wide", bufs=WIDE_BUFS)
 
-        def load_g(b, lo=0, hi=4):
-            load_rows("g", b, grad_out[b], lo, hi)
+        def load_rows(key, src):
+            raw[key] = narrow(BF16, PACK * DIM)[:]
+            nc.sync.dma_start(
+                out=raw[key].rearrange("p (t d) -> p t d", d=DIM), in_=src.rearrange("(p t) d -> p t d", t=PACK)
+            )
+
+        def load_g(b):
+            load_rows(("g", b), grad_out[b])
 
         def load_x(b):
-            load_rows("x", b, x[b], 0, 4)
+            load_rows(("x", b), x[b])
 
         def load_w1(q):
-            load_rows("w1", q, w1[PASS * q : PASS * q + PASS, :], 0, 4)
+            load_rows(("w1", q), w1[PASS * q : PASS * q + PASS, :])
 
-        def load_w2(i, lo=0, hi=2):
+        def load_w2(i, blocks=(0, 1)):
             c, u = divmod(i, 2)
-            if hi - lo == 2:
-                tile = slab(BF16, 4 * DIM)
+            lo, hi = blocks[0], blocks[-1] + 1
+            if len(blocks) == 2:
+                tile = narrow(BF16, PACK * DIM)
             else:
-                tile = keep.tile([P, 2 * DIM], BF16, name="w2_%d_block%d" % (i, lo))
-            rows = w2[HALF * c : HALF * c + HALF, :].rearrange("(s p t) d -> p s t d", s=2, t=4)
+                tile = keep.tile([P, 2 * DIM], BF16, name="w2_block%d" % lo)
+            rows = w2[HALF * c : HALF * c + HALF, :].rearrange("(s p t) d -> p s t d", s=2, t=PACK)
             nc.sync.dma_start(
                 out=tile[:].rearrange("p (s t d) -> p s t d", t=2, d=DIM), in_=rows[:, lo:hi, 2 * u : 2 * u + 2, :]
             )
-            for s in range(lo, hi):
+            for s in blocks:
                 raw["w2", i, s] = tile[:, 2 * DIM * (s - lo) : 2 * DIM * (s - lo + 1)]
 
-        def load_w2_half(c):
-            tile = stream.tile([P, 8 * DIM], BF16, name="pre", bufs=PRE_BUFS)
-            rows = w2[HALF * c : HALF * c + HALF, :].rearrange("(s p t) d -> p s t d", s=2, t=4)
-            nc.sync.dma_start(out=tile[:].rearrange("p (s t d) -> p s t d", t=4, d=DIM), in_=rows)
-            for u in range(2):
-                for s in range(2):
-                    raw["w2", 2 * c + u, s] = tile[:, DIM * (4 * s + 2 * u) : DIM * (4 * s + 2 * u + 2)]
-
-        def load_w1_pair(q):
-            tile = stream.tile([P, 8 * DIM], BF16, name="pre", bufs=PRE_BUFS)
-            rows = w1[PASS * q : PASS * (q + 2), :].rearrange("(q p t) d -> p q t d", q=2, t=4)
-            nc.sync.dma_start(out=tile[:].rearrange("p (q t d) -> p q t d", t=4, d=DIM), in_=rows)
-            for i in range(2):
-                raw["w1", q + i] = tile[:, 4 * DIM * i : 4 * DIM * (i + 1)]
-
-        def load_pre(pair, lo, hi):
+        def load_pre(pair, tiles):
             b, c = PAIRS[pair]
-            if hi - lo == 4:
-                tile = stream.tile([P, 4 * HALF], F32, name="big", bufs=BIG_BUFS)
-            elif hi - lo == 2:
-                tile = stream.tile([P, 2 * HALF], F32, name="pre", bufs=PRE_BUFS)
-            else:
-                tile = slab(F32, HALF)
-            rows = pre[b].rearrange("(p j) h -> p j h", j=4)[:, lo:hi, HALF * c : HALF * c + HALF]
+            lo, hi = tiles[0], tiles[-1] + 1
+            tile = wide(F32, 2 * HALF) if len(tiles) == 2 else narrow(F32, HALF)
+            rows = pre[b].rearrange("(p j) h -> p j h", j=PACK)[:, lo:hi, HALF * c : HALF * c + HALF]
             nc.sync.dma_start(out=tile[:].rearrange("p (j h) -> p j h", h=HALF), in_=rows)
-            for j in range(lo, hi):
+            for j in tiles:
                 raw["pre", pair, j] = tile[:, HALF * (j - lo) : HALF * (j - lo + 1)]
 
-        def copy_words(engine, out, in_):
-            if engine == "s":
+        def copy(engine, out, in_):
+            if engine == "scalar":
                 nc.scalar.copy(out=out, in_=in_)
             else:
                 nc.vector.tensor_copy(out=out, in_=in_)
 
-        def group_tile(key, name):
+        def grouped_tile(key, kind):
             if key not in grouped:
-                grouped[key] = stream.tile([P, PACK * PASS], BF16, name=name, bufs=GROUP_BUFS[name], align_bytes=64)
+                grouped[key] = stream.tile([P, PACK * PASS], BF16, name=kind, bufs=GROUPED_BUFS[kind], align_bytes=64)
             return grouped[key]
-
-        def quantise(key, lo=0, hi=PASS):
-            if key not in codes:
-                label = "%s%d" % key
-                codes[key] = (
-                    keep.tile([P, PASS], U32, name="codes_" + label, align_bytes=64),
-                    keep.tile([P, PASS], U8, name="scales_" + label, align_bytes=64),
-                )
-            words, scales = codes[key]
-            dtype = E4M3 if key[0] in ("x", "w1", "w2") else E5M2
-            nc.vector.quantize_mx(
-                out=words[:, lo:hi].bitcast(dtype), scales=scales[:, lo:hi], in_=grouped[key][:, PACK * lo : PACK * hi]
-            )
-
-        def multiply(out, left, tile, right, lo, hi, start, stop):
-            cols = slice(P * tile, P * tile + P)
-            nc.tensor.matmul_mx(
-                out=out,
-                lhsT=codes[left][0][:, cols].bitcast(E5M2),
-                lhsT_scale=codes[left][1][:, cols],
-                rhs=codes[right][0][:, lo:hi].bitcast(E4M3),
-                rhs_scale=codes[right][1][:, lo:hi],
-                start=start,
-                stop=stop,
-            )
 
         def flip(what, i, half, number):
             dst = bank(number, (what, i, half))
@@ -158,27 +115,28 @@ def tile_mlp_v_kernel(tc, x, w1, w2, pre, grad_out, out_0, out_1):
                     first = 2 * P * (2 * (i % 2) + half) + P * (k // 2)
                     words = dz[i - i % 2 + k % 2][:].bitcast(F32)[:, first : first + P]
                 else:
-                    words = raw[what, i, half].bitcast(F32)[:, 2 * P * (k // 2) + k % 2 : 2 * P * (k // 2 + 1) : 2]
+                    rows = raw[what, i, half] if what == "w2" else raw[what, i][:, 2 * DIM * half : 2 * DIM * (half + 1)]
+                    words = rows.bitcast(F32)[:, 2 * P * (k // 2) + k % 2 : 2 * P * (k // 2 + 1) : 2]
                 nc.tensor.transpose(dst[:, P * k : P * k + P], words, ident[:])
 
-        def take(what, i, half, engine="s", name="words"):
-            dst = group_tile((what, i), name)[:].bitcast(F32)[:, PASS * half : PASS * half + PASS]
+        def take(what, i, half, engine="scalar", kind="words"):
+            dst = grouped_tile((what, i), kind)[:].bitcast(F32)[:, PASS * half : PASS * half + PASS]
             src = banks[what, i, half][:]
             if what == "w2":
-                copy_words(engine, dst.rearrange("k (n i) -> k n i", i=4), src.rearrange("k (i n) -> k n i", i=4))
+                copy(engine, dst.rearrange("k (n i) -> k n i", i=4), src.rearrange("k (i n) -> k n i", i=4))
             else:
-                copy_words(
+                copy(
                     engine,
                     dst.rearrange("k (j n v) -> k j n v", j=2, v=2),
                     src.rearrange("k (j v n) -> k j n v", j=2, v=2),
                 )
 
-        def group_rows(what, i, lo, hi, engine, name="rows"):
-            dst = group_tile((what, i), name)[:, PACK * lo : PACK * hi]
-            src = raw[what, i].rearrange("p (t d) -> p t d", t=4)[:, :, lo:hi]
-            if engine == "g":
+        def interleave_rows(what, i, lo, hi, engine, kind="rows"):
+            dst = grouped_tile((what, i), kind)[:, PACK * lo : PACK * hi]
+            src = raw[what, i].rearrange("p (t d) -> p t d", t=PACK)[:, :, lo:hi]
+            if engine == "gpsimd":
                 nc.gpsimd.tensor_scalar(
-                    out=dst.rearrange("p (n t) -> p n t", t=4),
+                    out=dst.rearrange("p (n t) -> p n t", t=PACK),
                     in0=src.rearrange("p t n -> p n t"),
                     scalar1=2.0,
                     scalar2=0.0,
@@ -186,20 +144,55 @@ def tile_mlp_v_kernel(tc, x, w1, w2, pre, grad_out, out_0, out_1):
                     op1=ADD,
                 )
                 return
-            dst = dst.rearrange("p (c i t) -> p c t i", i=4, t=4)
+            dst = dst.rearrange("p (c i t) -> p c t i", i=4, t=PACK)
             src = src.rearrange("p t (c i) -> p c t i", i=4)
-            if engine == "s":
+            if engine == "scalar":
                 nc.scalar.activation(out=dst, in_=src, func=COPY, scale=2.0)
             else:
                 nc.vector.tensor_scalar(out=dst, in0=src, scalar1=2.0, scalar2=None, op0=MULT)
 
-        def make_dh(m, j, number):
+        def interleave_dz(m, lo, hi, engine, kind="rows"):
+            pairs = slice(lo // 2, hi // 2)
+            dst = grouped_tile(("t", m), kind)[:].rearrange("p (e n j) -> p e n j", e=2, j=PACK)[:, :, pairs, :]
+            src = dz[m][:].rearrange("p (j n e) -> p e n j", j=PACK, e=2)[:, :, pairs, :]
+            if engine == "gpsimd":
+                nc.gpsimd.tensor_scalar(out=dst, in0=src, scalar1=1.0, scalar2=0.0, op0=MULT, op1=ADD)
+            else:
+                copy(engine, dst, src)
+
+        def quantise(what, i, lo=0, hi=PASS):
+            if (what, i) not in codes:
+                codes[what, i] = (
+                    keep.tile([P, PASS], U32, name="codes_%s%d" % (what, i), align_bytes=64),
+                    keep.tile([P, PASS], U8, name="scales_%s%d" % (what, i), align_bytes=64),
+                )
+            words, scales = codes[what, i]
+            dtype = E4M3 if what in ("x", "w1", "w2") else E5M2
+            nc.vector.quantize_mx(
+                out=words[:, lo:hi].bitcast(dtype),
+                scales=scales[:, lo:hi],
+                in_=grouped[what, i][:, PACK * lo : PACK * hi],
+            )
+
+        def multiply(out, left, tile, right, start, stop):
+            cols = slice(P * tile, P * tile + P)
+            nc.tensor.matmul_mx(
+                out=out,
+                lhsT=codes[left][0][:, cols].bitcast(E5M2),
+                lhsT_scale=codes[left][1][:, cols],
+                rhs=codes[right][0][:, :].bitcast(E4M3),
+                rhs_scale=codes[right][1][:, :],
+                start=start,
+                stop=stop,
+            )
+
+        def make_dh(m, j):
             b, c = PAIRS[m // 2]
-            multiply(bank(number, ("dh", m, j))[:], ("g", b), j, ("w2", 2 * c + m % 2), 0, PASS, True, True)
+            multiply(bank(j, ("dh", m, j))[:], ("g", b), j, ("w2", 2 * c + m % 2), True, True)
 
         def make_dz(m, j):
             if m not in dz:
-                dz[m] = stream.tile([P, 4 * PASS], BF16, name="dz", bufs=DZ_BUFS, align_bytes=64)
+                dz[m] = stream.tile([P, PACK * PASS], BF16, name="dz", bufs=DZ_BUFS, align_bytes=64)
             nc.vector.scalar_tensor_tensor(
                 out=dz[m][:, PASS * j : PASS * j + PASS].rearrange("p (n e) -> p n e", e=2),
                 in0=raw["pre", m // 2, j].rearrange("p (n u e) -> p n u e", u=2, e=2)[:, :, m % 2, :],
@@ -209,354 +202,264 @@ def tile_mlp_v_kernel(tc, x, w1, w2, pre, grad_out, out_0, out_1):
                 op1=MULT,
             )
 
-        def group_t(m, lo, hi, engine, name="pool"):
-            dst = group_tile(("t", m), name)[:].rearrange("p (e n j) -> p e n j", e=2, j=4)[:, :, lo:hi, :]
-            src = dz[m][:].rearrange("p (j n e) -> p e n j", j=4, e=2)[:, :, lo:hi, :]
-            if engine == "g":
-                nc.gpsimd.tensor_scalar(out=dst, in0=src, scalar1=1.0, scalar2=0.0, op0=MULT, op1=ADD)
-            else:
-                copy_words(engine, dst, src)
-
         def add_pass(key, number, left, tile, right, total):
-            n = passes.get(key, 0)
-            passes[key] = n + 1
-            if n == 0:
+            done = passes.get(key, 0)
+            passes[key] = done + 1
+            if done == 0:
                 bank(number, key)
-            multiply(banks[key][:], left, tile, right, 0, PASS, n == 0, n == total - 1)
+            multiply(banks[key][:], left, tile, right, done == 0, done == total - 1)
 
         def dx_pass(b, j, q, number=None):
             pair = PAIRS.index((b, q // 2))
-            add_pass(("dx", b, j), number, ("h", 2 * pair + j // 2), 2 * (j % 2) + q % 2, ("w1", q), 4)
+            add_pass(("dx", b, j), number, ("h", 2 * pair + j // 2), 2 * (j % 2) + q % 2, ("w1", q), HIDDEN // PASS)
 
         def dw_pass(m, tile, number=None):
             b, c = PAIRS[m // 2]
-            add_pass(("dw", 2 * c + m % 2, tile), number, ("t", m), tile, ("x", b), 2)
+            add_pass(("dw", 2 * c + m % 2, tile), number, ("t", m), tile, ("x", b), BATCH)
 
-        def leave(what, i, tile, engine="s"):
-            pair, side = divmod(tile, 2) if what == "dx" else (tile % 2, tile // 2)
-            if (what, i, pair) not in staged:
-                if (what, i) in WHOLE:
-                    both = stream.tile([P, 4 * DIM], F32, name="pre", bufs=PRE_BUFS)
-                    staged[what, i] = both
+        def dw_tile(block, tile, number):
+            c, u = divmod(block, 2)
+            dw_pass(2 * PAIRS.index((0, c)) + u, tile, number)
+            dw_pass(2 * PAIRS.index((1, c)) + u, tile)
+
+        def leave(what, i, tile, engine="scalar", whole=False):
+            couple, side = divmod(tile, 2) if what == "dx" else (tile % 2, tile // 2)
+            if (what, i, couple) not in staged:
+                if whole:
+                    staged[what, i] = wide(F32, 4 * DIM)
                     for k in range(2):
-                        staged[what, i, k] = both[:, 2 * DIM * k : 2 * DIM * (k + 1)]
+                        staged[what, i, k] = staged[what, i][:, 2 * DIM * k : 2 * DIM * (k + 1)]
                 else:
-                    staged[what, i, pair] = slab(F32, 2 * DIM)[:]
-            copy_words(engine, staged[what, i, pair][:, DIM * side : DIM * side + DIM], banks[what, i, tile][:])
+                    staged[what, i, couple] = narrow(F32, 2 * DIM)[:]
+            copy(engine, staged[what, i, couple][:, DIM * side : DIM * side + DIM], banks[what, i, tile][:])
 
-        def store_all(what, i):
-            src = staged[what, i][:].rearrange("p (s f d) -> p s f d", s=2, f=2)
+        def output_rows(what, i):
             if what == "dx":
-                rows = out_0[i].rearrange("(p s f) d -> p s f d", s=2, f=2)
-            else:
-                rows = out_1[HALF * (i // 2) : HALF * (i // 2 + 1), :].rearrange("(s p f) d -> p s f d", s=2, f=4)
-                rows = rows[:, :, 2 * (i % 2) : 2 * (i % 2) + 2, :]
-            nc.sync.dma_start(out=rows, in_=src)
+                return out_0[i].rearrange("(p s f) d -> p s f d", s=2, f=2)
+            c, u = divmod(i, 2)
+            rows = out_1[HALF * c : HALF * c + HALF, :].rearrange("(s p f) d -> p s f d", s=2, f=PACK)
+            return rows[:, :, 2 * u : 2 * u + 2, :]
 
-        def store(what, i, pair, lo=0, hi=2):
-            if what == "dx":
-                rows = out_0[i].rearrange("(p j) d -> p j d", j=4)[:, 2 * pair : 2 * pair + 2, :]
-            else:
-                first = HALF * (i // 2) + PASS * pair
-                rows = out_1[first : first + PASS, :].rearrange("(p f) d -> p f d", f=4)[:, 2 * (i % 2) : 2 * (i % 2) + 2, :]
-            src = staged[what, i, pair].rearrange("p (f d) -> p f d", f=2)
-            nc.sync.dma_start(out=rows[:, lo:hi, :], in_=src[:, lo:hi, :])
+        def store_whole(what, i):
+            nc.sync.dma_start(
+                out=output_rows(what, i), in_=staged[what, i][:].rearrange("p (s f d) -> p s f d", s=2, f=2)
+            )
+
+        def store(what, i, couple, lo=0, hi=2):
+            src = staged[what, i, couple].rearrange("p (f d) -> p f d", f=2)
+            nc.sync.dma_start(out=output_rows(what, i)[:, couple, lo:hi, :], in_=src[:, lo:hi, :])
+
 
         load_x(0)
-        load_w2(0, 0, 1)
-        load_w2(0, 1, 2)
+        load_w2(0, (0,))
+        load_w2(0, (1,))
         load_g(0)
         load_x(1)
-        load_pre(0, 0, 1)
+        load_pre(0, (0,))
         load_w2(1)
-        load_pre(0, 1, 2)
-        load_pre(0, 2, 3)
-        group_rows("x", 0, 0, 512, "s")
-        load_pre(0, 3, 4)
-        flip("w2", 0, 0, 4)
+        for j in (1, 2, 3):
+            load_pre(0, (j,))
         load_g(1)
-        flip("w2", 0, 1, 5)
-        take("w2", 0, 0, "v")
-        take("w2", 0, 1, "v")
-        load_pre(1, 0, 2)
-        flip("g", 0, 0, 6)
-        quantise(("w2", 0))
-        flip("g", 0, 1, 7)
-        take("g", 0, 0)
-        quantise(("x", 0))
-        load_pre(1, 2, 3)
-        take("g", 0, 1)
-        quantise(("g", 0), 0, 256)
-        group_rows("x", 1, 0, 512, "v")
-        load_pre(1, 3, 4)
-        make_dh(0, 0, 0)
-        make_dh(0, 1, 1)
-        quantise(("g", 0), 256, 512)
+        load_pre(1, (0, 1))
+        load_pre(1, (2,))
+        load_pre(1, (3,))
         load_w2(2)
-        flip("w2", 1, 0, 4)
-        make_dz(0, 0)
-        flip("w2", 1, 1, 5)
-        quantise(("x", 1))
-        take("w2", 1, 0)
+
+        interleave_rows("x", 0, 0, PASS, "scalar")
+        for half in range(2):
+            flip("w2", 0, half, 4 + half)
+            take("w2", 0, half, "vector")
+        quantise("w2", 0)
+        quantise("x", 0)
+        for half in range(2):
+            flip("g", 0, half, 6 + half)
+            take("g", 0, half)
+        quantise("g", 0, 0, PASS // 2)
+        interleave_rows("x", 1, 0, PASS, "vector")
+        quantise("g", 0, PASS // 2, PASS)
         load_w2(3)
-        make_dz(0, 1)
-        make_dh(0, 2, 2)
-        take("w2", 1, 1)
-        make_dh(0, 3, 3)
         load_w1(0)
-        quantise(("w2", 1))
-        make_dz(0, 2)
-        make_dh(1, 0, 0)
-        make_dh(1, 1, 1)
-        load_pre(2, 2, 4)
-        make_dz(0, 3)
-        make_dh(1, 2, 2)
-        make_dz(1, 0)
-        make_dh(1, 3, 3)
-        group_t(0, 176, 256, "s")
-        group_t(0, 0, 176, "g")
+        load_pre(2, (2, 3))
         load_w1(2)
-        make_dz(1, 1)
-        flip("g", 1, 0, 6)
-        make_dz(1, 2)
-        flip("g", 1, 1, 7)
-        take("g", 1, 0)
-        make_dz(1, 3)
-        flip("h", 0, 0, 4)
-        flip("h", 0, 1, 5)
-        take("g", 1, 1)
-        flip("h", 1, 0, 6)
-        quantise(("g", 1), 0, 256)
-        take("h", 0, 0)
-        flip("h", 1, 1, 7)
-        load_pre(2, 0, 2)
-        quantise(("g", 1), 256, 512)
-        make_dh(2, 0, 0)
-        quantise(("t", 0))
-        take("h", 0, 1)
-        make_dh(2, 1, 1)
-        take("h", 1, 0)
-        group_t(1, 0, 176, "g")
+        load_pre(2, (0, 1))
+
+        make_dh(0, 0)
+        make_dh(0, 1)
+        make_dz(0, 0)
+        quantise("x", 1)
+        make_dz(0, 1)
+        for half in range(2):
+            flip("w2", 1, half, 4 + half)
+            take("w2", 1, half)
+        make_dh(0, 2)
+        make_dh(0, 3)
+        quantise("w2", 1)
+        make_dz(0, 2)
+        make_dz(0, 3)
+
+        interleave_dz(0, 0, POOL_COLUMNS, "gpsimd", "gate")
+        interleave_dz(0, POOL_COLUMNS, PASS, "scalar", "gate")
+        for j in range(4):
+            make_dh(1, j)
+            make_dz(1, j)
         load_w1(1)
-        make_dz(2, 0)
-        make_dh(2, 2, 2)
-        take("h", 1, 1)
-        make_dz(2, 1)
-        make_dh(2, 3, 3)
-        group_t(1, 176, 256, "s")
-        make_dh(3, 0, 0)
-        make_dz(2, 2)
         load_w1(3)
-        make_dh(3, 1, 1)
-        make_dz(2, 3)
-        make_dh(3, 2, 2)
-        quantise(("h", 0))
-        make_dh(3, 3, 3)
-        load_pre(3, 0, 2)
-        group_t(2, 128, 256, "s", "rows")
-        flip("w2", 2, 0, 4)
-        group_t(2, 0, 128, "v", "rows")
-        flip("w2", 2, 1, 5)
-        quantise(("h", 1))
-        load_pre(3, 2, 4)
-        flip("w2", 3, 0, 6)
-        take("w2", 2, 0)
-        flip("w2", 3, 1, 7)
-        quantise(("t", 2))
-        take("w2", 2, 1)
-        dw_pass(0, 0, 4)
-        quantise(("t", 1))
-        take("w2", 3, 0)
-        dw_pass(2, 0)
-        make_dz(3, 3)
-        group_rows("w1", 0, 0, 352, "g", "pool")
-        take("w2", 3, 1)
-        dw_pass(0, 2, 5)
-        make_dz(3, 0)
-        group_rows("w1", 0, 352, 512, "s", "pool")
-        dw_pass(2, 2)
-        make_dz(3, 1)
-        dw_pass(0, 1, 6)
-        make_dz(3, 2)
-        dw_pass(2, 1)
-        leave("dw", 0, 0)
-        dw_pass(0, 3, 7)
-        dw_pass(2, 3)
-        quantise(("w2", 2))
+        load_pre(3, (0, 1))
+        load_pre(3, (2, 3))
+        for half in range(2):
+            flip("g", 1, half, 6 + half)
+            take("g", 1, half)
+            quantise("g", 1, PASS // 2 * half, PASS // 2 * (half + 1))
+        for i in range(2):
+            for half in range(2):
+                flip("h", i, half, 4 + 2 * i + half)
+                take("h", i, half)
+        quantise("t", 0)
+
+        interleave_dz(1, 0, POOL_COLUMNS, "gpsimd", "gate")
+        interleave_dz(1, POOL_COLUMNS, PASS, "scalar", "gate")
+        for j in range(4):
+            make_dh(2, j)
+            make_dz(2, j)
+        for j in range(4):
+            make_dh(3, j)
+        quantise("h", 0)
+        interleave_dz(2, 0, PASS // 2, "vector")
+        interleave_dz(2, PASS // 2, PASS, "scalar")
+        quantise("h", 1)
+        quantise("t", 2)
+        quantise("t", 1)
+
+        for i in (2, 3):
+            for half in range(2):
+                flip("w2", i, half, 4 + 2 * (i % 2) + half)
+                take("w2", i, half)
+        interleave_rows("w1", 0, 0, POOL_COLUMNS, "gpsimd", "gate")
+        interleave_rows("w1", 0, POOL_COLUMNS, PASS, "scalar", "gate")
+        for j in (3, 0, 1, 2):
+            make_dz(3, j)
+        for number, tile in enumerate((0, 2, 1, 3), 4):
+            dw_tile(0, tile, number)
+        leave("dw", 0, 0, whole=True)
         leave("dw", 0, 2)
-        flip("h", 2, 0, 4)
-        group_t(3, 0, 160, "v", "rows")
-        group_t(3, 160, 256, "s", "rows")
-        flip("h", 2, 1, 5)
-        make_dh(4, 0, 0)
-        quantise(("w2", 3))
-        make_dh(4, 1, 1)
-        make_dh(4, 2, 2)
+        quantise("w2", 2)
+        interleave_dz(3, 0, UNIT3_VECTOR_COLUMNS, "vector")
+        interleave_dz(3, UNIT3_VECTOR_COLUMNS, PASS, "scalar")
+        quantise("w2", 3)
+        quantise("t", 3)
+        quantise("w1", 0)
         leave("dw", 0, 1)
-        make_dh(4, 3, 3)
-        quantise(("t", 3))
         leave("dw", 0, 3)
-        flip("h", 3, 0, 6)
-        quantise(("w1", 0))
-        take("h", 2, 0)
-        flip("h", 3, 1, 7)
-        make_dz(4, 3)
-        store_all("dw", 0)
-        group_rows("w1", 2, 0, 352, "g", "pool")
-        take("h", 2, 1)
-        dw_pass(1, 0, 4)
-        make_dz(4, 2)
-        dw_pass(3, 0)
-        take("h", 3, 0, "s", "late")
-        make_dz(4, 0)
-        dw_pass(1, 2, 5)
-        dw_pass(3, 2)
-        take("h", 3, 1, "s", "late")
-        make_dh(5, 3, 3)
-        make_dz(4, 1)
-        make_dh(5, 2, 2)
-        leave("dw", 1, 0)
-        dw_pass(1, 1, 6)
-        make_dz(5, 3)
-        group_rows("w1", 1, 0, 352, "g", "rows")
-        dw_pass(3, 1)
-        dw_pass(1, 3, 7)
-        make_dz(5, 2)
+        store_whole("dw", 0)
+        for half in range(2):
+            flip("h", 2, half, 4 + half)
+            take("h", 2, half)
+        for j in range(4):
+            make_dh(4, j)
+        for half in range(2):
+            flip("h", 3, half, 6 + half)
+            take("h", 3, half, kind="last_gate")
+
+        interleave_rows("w1", 2, 0, POOL_COLUMNS, "gpsimd", "gate")
+        interleave_rows("w1", 1, 0, POOL_COLUMNS, "gpsimd")
+        for j in (3, 2, 0, 1):
+            make_dz(4, j)
+        for tiles, numbers, dh_tiles in (((0, 2), (4, 5), (3, 2)), ((1, 3), (6, 7), (0, 1))):
+            for tile, number in zip(tiles, numbers):
+                dw_tile(1, tile, number)
+            for j in dh_tiles:
+                make_dh(5, j)
+                make_dz(5, j)
+        leave("dw", 1, 0, whole=True)
         leave("dw", 1, 2)
-        dw_pass(3, 3)
-        make_dh(5, 0, 0)
-        group_rows("w1", 1, 352, 512, "s")
-        make_dh(5, 1, 1)
-        dx_pass(0, 0, 0, 4)
-        make_dz(5, 0)
-        dx_pass(0, 1, 0, 5)
-        make_dz(5, 1)
+        interleave_rows("w1", 1, POOL_COLUMNS, PASS, "scalar")
         leave("dw", 1, 1)
-        group_rows("w1", 3, 256, 512, "v")
         leave("dw", 1, 3)
-        dx_pass(0, 2, 0, 6)
-        quantise(("w1", 1))
-        group_rows("w1", 3, 0, 256, "s")
-        dx_pass(0, 3, 0, 7)
-        store_all("dw", 1)
-        flip("h", 5, 1, 3)
-        quantise(("h", 2))
-        flip("h", 5, 0, 2)
-        flip("h", 4, 0, 0)
-        flip("h", 4, 1, 1)
-        group_rows("w1", 2, 352, 512, "s", "pool")
-        quantise(("w1", 3))
-        dx_pass(0, 0, 1)
-        dx_pass(0, 1, 1)
-        dx_pass(0, 2, 1)
-        take("h", 5, 1)
-        dx_pass(0, 3, 1)
-        quantise(("w1", 2))
-        take("h", 5, 0)
-        make_dh(6, 3, 3)
-        take("h", 4, 0)
-        make_dh(6, 2, 2)
-        quantise(("h", 5))
-        take("h", 4, 1)
-        make_dh(6, 0, 0)
-        group_t(4, 0, 128, "s", "rows")
-        make_dh(6, 1, 1)
-        quantise(("h", 4))
-        dx_pass(0, 2, 3)
-        dx_pass(0, 2, 2)
-        quantise(("h", 3))
-        dx_pass(0, 3, 3)
-        dx_pass(0, 3, 2)
-        make_dz(6, 1)
-        dx_pass(0, 0, 3)
-        group_t(5, 0, 176, "g", "late")
-        leave("dx", 0, 2)
-        dx_pass(0, 0, 2)
-        make_dz(6, 0)
-        dx_pass(0, 1, 3)
-        leave("dx", 0, 3)
-        dx_pass(0, 1, 2)
-        make_dz(6, 2)
-        make_dh(7, 1, 1)
-        make_dh(7, 0, 0)
-        leave("dx", 0, 0)
-        make_dz(6, 3)
-        dx_pass(1, 0, 0, 6)
-        dx_pass(1, 0, 1)
-        leave("dx", 0, 1)
-        make_dh(7, 2, 2)
-        make_dz(7, 1)
-        make_dh(7, 3, 3)
-        group_t(6, 0, 176, "g", "rows")
-        group_t(4, 128, 256, "s", "rows")
-        dx_pass(1, 1, 0, 7)
-        make_dz(7, 0)
-        store_all("dx", 0)
-        dx_pass(1, 1, 1)
-        make_dz(7, 2)
-        flip("h", 6, 1, 1)
-        flip("h", 6, 0, 0)
-        make_dz(7, 3)
+        store_whole("dw", 1)
+        for j in range(4):
+            dx_pass(0, j, 0, 4 + j)
+
+        interleave_rows("w1", 3, PASS // 2, PASS, "vector")
+        interleave_rows("w1", 3, 0, PASS // 2, "scalar")
+        interleave_rows("w1", 2, POOL_COLUMNS, PASS, "scalar", "gate")
+        freed = (3, 2, 0, 1)
+        for j in freed:
+            flip("h", 4 + j // 2, j % 2, j)
+            take("h", 4 + j // 2, j % 2)
+        quantise("w1", 1)
+        quantise("h", 2)
+        quantise("w1", 3)
+        quantise("w1", 2)
+        quantise("h", 5)
+        quantise("h", 4)
+        quantise("h", 3)
+        for j in range(4):
+            dx_pass(0, j, 1)
+        for j in freed:
+            make_dh(6, j)
+
+        interleave_dz(4, 0, PASS // 2, "scalar")
+        interleave_dz(5, 0, POOL_COLUMNS, "gpsimd", "last_gate")
+        for j in (2, 3, 0, 1):
+            dx_pass(0, j, 3)
+            dx_pass(0, j, 2)
+            leave("dx", 0, j, whole=True)
+        store_whole("dx", 0)
+        for j in (1, 0, 2, 3):
+            make_dz(6, j)
+        interleave_dz(6, 0, POOL_COLUMNS, "gpsimd")
+        interleave_dz(4, PASS // 2, PASS, "scalar")
+        interleave_dz(6, POOL_COLUMNS, PASS, "scalar")
+        for j, dh_tiles in ((0, (1, 0)), (1, (2, 3))):
+            for k in dh_tiles:
+                make_dh(7, k)
+                make_dz(7, k)
+            dx_pass(1, j, 0, 6 + j)
+            dx_pass(1, j, 1)
+        for half in (1, 0):
+            flip("h", 6, half, half)
+            take("h", 6, half)
         dx_pass(1, 2, 0, 4)
-        group_t(6, 176, 256, "s", "rows")
         dx_pass(1, 2, 1)
-        quantise(("t", 4))
-        flip("h", 7, 0, 2)
-        flip("h", 7, 1, 3)
-        take("h", 6, 1)
-        quantise(("t", 6))
+        for half in range(2):
+            flip("h", 7, half, 2 + half)
+            take("h", 7, half)
+
+        quantise("t", 4)
+        quantise("t", 6)
+        interleave_dz(5, POOL_COLUMNS, PASS, "vector", "last_gate")
+        quantise("h", 6)
+        interleave_dz(7, 0, PASS, "vector")
+        quantise("h", 7)
+        quantise("t", 5)
+        quantise("t", 7)
         dw_pass(4, 0, 5)
-        take("h", 6, 0)
         dw_pass(4, 2, 1)
-        group_t(5, 176, 256, "v", "late")
         dw_pass(6, 0)
-        take("h", 7, 0)
         dw_pass(6, 2)
-        quantise(("h", 6))
-        dw_pass(4, 1, 0)
-        take("h", 7, 1)
-        dw_pass(6, 1)
-        group_t(7, 0, 256, "v", "rows")
-        dw_pass(4, 3, 2)
-        leave("dw", 2, 0)
-        dw_pass(6, 3)
-        dx_pass(1, 0, 2)
-        leave("dw", 2, 2)
-        dx_pass(1, 0, 3)
+        dw_tile(2, 1, 0)
+        dw_tile(2, 3, 2)
+        for tile in (0, 2, 1, 3):
+            leave("dw", 2, tile)
         store("dw", 2, 0, 0, 1)
-        dx_pass(1, 1, 2)
-        quantise(("h", 7))
-        dx_pass(1, 1, 3)
-        leave("dw", 2, 1)
-        dx_pass(1, 3, 0, 3)
         store("dw", 2, 0, 1, 2)
-        quantise(("t", 5))
-        dx_pass(1, 3, 1)
-        leave("dw", 2, 3)
-        dx_pass(1, 2, 2)
-        quantise(("t", 7))
-        dx_pass(1, 2, 3)
-        leave("dx", 1, 0)
-        dx_pass(1, 3, 2)
         store("dw", 2, 1)
-        dx_pass(1, 3, 3)
-        leave("dx", 1, 1)
-        dw_pass(5, 0, 5)
-        dw_pass(7, 0)
-        leave("dx", 1, 3, "v")
-        dw_pass(5, 2, 1)
-        leave("dx", 1, 2)
-        dw_pass(7, 2)
+
+        for j in range(2):
+            dx_pass(1, j, 2)
+            dx_pass(1, j, 3)
+            leave("dx", 1, j)
         store("dx", 1, 0)
-        dw_pass(5, 1, 0)
-        leave("dw", 3, 0)
-        dw_pass(7, 1)
-        leave("dw", 3, 2, "v")
-        store("dx", 1, 1, 0, 1)
-        store("dx", 1, 1, 1, 2)
-        dw_pass(5, 3, 2)
-        dw_pass(7, 3)
-        leave("dw", 3, 1)
-        store("dw", 3, 0)
-        leave("dw", 3, 3, "v")
-        store("dw", 3, 1)
+        dx_pass(1, 3, 0, 3)
+        dx_pass(1, 3, 1)
+        for j, engine in ((2, "scalar"), (3, "vector")):
+            dx_pass(1, j, 2)
+            dx_pass(1, j, 3)
+            leave("dx", 1, j, engine)
+            store("dx", 1, 1, j - 2, j - 1)
+
+        for couple, numbers in enumerate(((5, 1), (0, 2))):
+            for side, engine in enumerate(("scalar", "vector")):
+                dw_tile(3, couple + 2 * side, numbers[side])
+                leave("dw", 3, couple + 2 * side, engine)
+            store("dw", 3, couple)

@@ -7,7 +7,6 @@ BATCH, SEQ, DIM, HIDDEN = 2, 512, 512, 2048
 P = 128
 PACK = 4
 PASS = P * PACK
-HALF = HIDDEN // 2
 FLOPS = 3 * 2 * BATCH * SEQ * DIM * HIDDEN
 
 F32 = mybir.dt.float32
@@ -19,15 +18,15 @@ E5M2 = mybir.dt.float8_e5m2_x4
 MULT, ADD, MAX = mybir.AluOpType.mult, mybir.AluOpType.add, mybir.AluOpType.max
 COPY = mybir.ActivationFunctionType.Copy
 
-PAIRS = ((0, 0), (1, 0), (0, 1), (1, 1))
+UNITS = ((0, 0), (0, 1), (1, 0), (1, 1), (0, 2), (0, 3), (1, 2), (1, 3))
 
 POOL_COLUMNS = 352
-UNIT3_VECTOR_COLUMNS = 320
+UNIT3_VECTOR_COLUMNS = 384
 
-NARROW_BUFS = 12
-WIDE_BUFS = 6
+NARROW_BUFS = 14
+WIDE_BUFS = 5
 DZ_BUFS = 4
-GROUPED_BUFS = {"words": 4, "rows": 4, "gate": 1, "last_gate": 1}
+GROUPED_BUFS = {"words": 5, "rows": 4, "gate": 1, "last_gate": 1}
 
 
 def tile_mlp_v_kernel(tc, x, w1, w2, pre, grad_out, out_0, out_1):
@@ -60,10 +59,13 @@ def tile_mlp_v_kernel(tc, x, w1, w2, pre, grad_out, out_0, out_1):
             return stream.tile([P, width], dtype, name="wide", bufs=WIDE_BUFS)
 
         def load_rows(key, src):
-            raw[key] = narrow(BF16, PACK * DIM)[:]
+            tile = narrow(BF16, PACK * DIM)[:]
             nc.sync.dma_start(
-                out=raw[key].rearrange("p (t d) -> p t d", d=DIM), in_=src.rearrange("(p t) d -> p t d", t=PACK)
+                out=tile.rearrange("p (t d) -> p t d", d=DIM), in_=src.rearrange("(p t) d -> p t d", t=PACK)
             )
+            raw[key] = tile
+            for half in range(2):
+                raw[key + (half,)] = tile[:, 2 * DIM * half : 2 * DIM * (half + 1)]
 
         def load_g(b):
             load_rows(("g", b), grad_out[b])
@@ -74,28 +76,23 @@ def tile_mlp_v_kernel(tc, x, w1, w2, pre, grad_out, out_0, out_1):
         def load_w1(q):
             load_rows(("w1", q), w1[PASS * q : PASS * q + PASS, :])
 
-        def load_w2(i, blocks=(0, 1)):
-            c, u = divmod(i, 2)
-            lo, hi = blocks[0], blocks[-1] + 1
-            if len(blocks) == 2:
-                tile = narrow(BF16, PACK * DIM)
-            else:
-                tile = keep.tile([P, 2 * DIM], BF16, name="w2_block%d" % lo)
-            rows = w2[HALF * c : HALF * c + HALF, :].rearrange("(s p t) d -> p s t d", s=2, t=PACK)
-            nc.sync.dma_start(
-                out=tile[:].rearrange("p (s t d) -> p s t d", t=2, d=DIM), in_=rows[:, lo:hi, 2 * u : 2 * u + 2, :]
-            )
-            for s in blocks:
-                raw["w2", i, s] = tile[:, 2 * DIM * (s - lo) : 2 * DIM * (s - lo + 1)]
+        def load_w2(q):
+            load_rows(("w2", q), w2[PASS * q : PASS * q + PASS, :])
 
-        def load_pre(pair, tiles):
-            b, c = PAIRS[pair]
-            lo, hi = tiles[0], tiles[-1] + 1
-            tile = wide(F32, 2 * HALF) if len(tiles) == 2 else narrow(F32, HALF)
-            rows = pre[b].rearrange("(p j) h -> p j h", j=PACK)[:, lo:hi, HALF * c : HALF * c + HALF]
-            nc.sync.dma_start(out=tile[:].rearrange("p (j h) -> p j h", h=HALF), in_=rows)
-            for j in tiles:
-                raw["pre", pair, j] = tile[:, HALF * (j - lo) : HALF * (j - lo + 1)]
+        def load_w2_half(q, half):
+            tile = keep.tile([P, 2 * DIM], BF16, name="w2_half%d" % half)
+            rows = w2[PASS * q : PASS * q + PASS, :].rearrange("(p t) d -> p t d", t=PACK)
+            nc.sync.dma_start(out=tile[:].rearrange("p (t d) -> p t d", d=DIM), in_=rows[:, 2 * half : 2 * half + 2, :])
+            raw["w2", q, half] = tile[:]
+
+        def load_pre(m, halves=(0, 1)):
+            b, q = UNITS[m]
+            lo, hi = halves[0], halves[-1] + 1
+            tile = wide(F32, PACK * PASS) if len(halves) == 2 else narrow(F32, 2 * PASS)
+            rows = pre[b].rearrange("(p j) h -> p j h", j=PACK)[:, 2 * lo : 2 * hi, PASS * q : PASS * q + PASS]
+            nc.sync.dma_start(out=tile[:].rearrange("p (j h) -> p j h", h=PASS), in_=rows)
+            for half in halves:
+                raw["pre", m, half] = tile[:, 2 * PASS * (half - lo) : 2 * PASS * (half - lo + 1)]
 
         def copy(engine, out, in_):
             if engine == "scalar":
@@ -112,11 +109,10 @@ def tile_mlp_v_kernel(tc, x, w1, w2, pre, grad_out, out_0, out_1):
             dst = bank(number, (what, i, half))
             for k in range(4):
                 if what == "h":
-                    first = 2 * P * (2 * (i % 2) + half) + P * (k // 2)
-                    words = dz[i - i % 2 + k % 2][:].bitcast(F32)[:, first : first + P]
+                    first = P * (4 * half + k)
+                    words = dz[i][:].bitcast(F32)[:, first : first + P]
                 else:
-                    rows = raw[what, i, half] if what == "w2" else raw[what, i][:, 2 * DIM * half : 2 * DIM * (half + 1)]
-                    words = rows.bitcast(F32)[:, 2 * P * (k // 2) + k % 2 : 2 * P * (k // 2 + 1) : 2]
+                    words = raw[what, i, half].bitcast(F32)[:, 2 * P * (k // 2) + k % 2 : 2 * P * (k // 2 + 1) : 2]
                 nc.tensor.transpose(dst[:, P * k : P * k + P], words, ident[:])
 
         def take(what, i, half, engine="scalar", kind="words"):
@@ -174,30 +170,35 @@ def tile_mlp_v_kernel(tc, x, w1, w2, pre, grad_out, out_0, out_1):
                 in_=grouped[what, i][:, PACK * lo : PACK * hi],
             )
 
-        def multiply(out, left, tile, right, start, stop):
+        def multiply(out, left, tile, right, columns, start, stop):
             cols = slice(P * tile, P * tile + P)
             nc.tensor.matmul_mx(
                 out=out,
                 lhsT=codes[left][0][:, cols].bitcast(E5M2),
                 lhsT_scale=codes[left][1][:, cols],
-                rhs=codes[right][0][:, :].bitcast(E4M3),
-                rhs_scale=codes[right][1][:, :],
+                rhs=codes[right][0][:, columns].bitcast(E4M3),
+                rhs_scale=codes[right][1][:, columns],
                 start=start,
                 stop=stop,
             )
 
-        def make_dh(m, j):
-            b, c = PAIRS[m // 2]
-            multiply(bank(j, ("dh", m, j))[:], ("g", b), j, ("w2", 2 * c + m % 2), True, True)
+        def make_dh(m, k, number=None):
+            b, q = UNITS[m]
+            half, u = divmod(k, 2)
+            dst = bank(k if number is None else number, ("dh", m, k))
+            for side in range(2):
+                out = dst[:, 2 * P * side : 2 * P * (side + 1)]
+                multiply(out, ("g", b), 2 * half + side, ("w2", q), slice(2 * P * u, 2 * P * (u + 1)), True, True)
 
-        def make_dz(m, j):
+        def make_dz(m, k):
+            half, u = divmod(k, 2)
             if m not in dz:
                 dz[m] = stream.tile([P, PACK * PASS], BF16, name="dz", bufs=DZ_BUFS, align_bytes=64)
             nc.vector.scalar_tensor_tensor(
-                out=dz[m][:, PASS * j : PASS * j + PASS].rearrange("p (n e) -> p n e", e=2),
-                in0=raw["pre", m // 2, j].rearrange("p (n u e) -> p n u e", u=2, e=2)[:, :, m % 2, :],
+                out=dz[m][:].rearrange("p (j u n e) -> p j u n e", j=PACK, u=2, e=2)[:, 2 * half : 2 * half + 2, u, :, :],
+                in0=raw["pre", m, half].rearrange("p (j n u e) -> p j n u e", j=2, u=2, e=2)[:, :, :, u, :],
                 scalar=0.0,
-                in1=banks["dh", m, j][:].rearrange("p (n e) -> p n e", e=2),
+                in1=banks["dh", m, k][:].rearrange("p (j n e) -> p j n e", j=2, e=2),
                 op0=MAX,
                 op1=MULT,
             )
@@ -207,20 +208,18 @@ def tile_mlp_v_kernel(tc, x, w1, w2, pre, grad_out, out_0, out_1):
             passes[key] = done + 1
             if done == 0:
                 bank(number, key)
-            multiply(banks[key][:], left, tile, right, done == 0, done == total - 1)
+            multiply(banks[key][:], left, tile, right, slice(0, PASS), done == 0, done == total - 1)
 
         def dx_pass(b, j, q, number=None):
-            pair = PAIRS.index((b, q // 2))
-            add_pass(("dx", b, j), number, ("h", 2 * pair + j // 2), 2 * (j % 2) + q % 2, ("w1", q), HIDDEN // PASS)
+            add_pass(("dx", b, j), number, ("h", UNITS.index((b, q))), j, ("w1", q), HIDDEN // PASS)
 
         def dw_pass(m, tile, number=None):
-            b, c = PAIRS[m // 2]
-            add_pass(("dw", 2 * c + m % 2, tile), number, ("t", m), tile, ("x", b), BATCH)
+            b, q = UNITS[m]
+            add_pass(("dw", q, tile), number, ("t", m), tile, ("x", b), BATCH)
 
-        def dw_tile(block, tile, number):
-            c, u = divmod(block, 2)
-            dw_pass(2 * PAIRS.index((0, c)) + u, tile, number)
-            dw_pass(2 * PAIRS.index((1, c)) + u, tile)
+        def dw_tile(q, tile, number):
+            dw_pass(UNITS.index((0, q)), tile, number)
+            dw_pass(UNITS.index((1, q)), tile)
 
         def leave(what, i, tile, engine="scalar", whole=False):
             couple, side = divmod(tile, 2) if what == "dx" else (tile % 2, tile // 2)
@@ -234,11 +233,8 @@ def tile_mlp_v_kernel(tc, x, w1, w2, pre, grad_out, out_0, out_1):
             copy(engine, staged[what, i, couple][:, DIM * side : DIM * side + DIM], banks[what, i, tile][:])
 
         def output_rows(what, i):
-            if what == "dx":
-                return out_0[i].rearrange("(p s f) d -> p s f d", s=2, f=2)
-            c, u = divmod(i, 2)
-            rows = out_1[HALF * c : HALF * c + HALF, :].rearrange("(s p f) d -> p s f d", s=2, f=PACK)
-            return rows[:, :, 2 * u : 2 * u + 2, :]
+            rows = out_0[i] if what == "dx" else out_1[PASS * i : PASS * i + PASS, :]
+            return rows.rearrange("(p s f) d -> p s f d", s=2, f=2)
 
         def store_whole(what, i):
             nc.sync.dma_start(
@@ -249,216 +245,205 @@ def tile_mlp_v_kernel(tc, x, w1, w2, pre, grad_out, out_0, out_1):
             src = staged[what, i, couple].rearrange("p (f d) -> p f d", f=2)
             nc.sync.dma_start(out=output_rows(what, i)[:, couple, lo:hi, :], in_=src[:, lo:hi, :])
 
+        def flip_take(what, i, numbers, engine="scalar", kind="words"):
+            for half, number in enumerate(numbers):
+                flip(what, i, half, number)
+                take(what, i, half, engine, kind)
 
         load_x(0)
-        load_w2(0, (0,))
-        load_w2(0, (1,))
+        load_w2_half(0, 0)
+        load_w2_half(0, 1)
         load_g(0)
-        load_x(1)
-        load_pre(0, (0,))
         load_w2(1)
-        for j in (1, 2, 3):
-            load_pre(0, (j,))
+        load_pre(0, (0,))
         load_g(1)
-        load_pre(1, (0, 1))
-        load_pre(1, (2,))
-        load_pre(1, (3,))
+        load_pre(0, (1,))
+        load_pre(1, (0,))
+        load_pre(1, (1,))
+        load_x(1)
+        load_pre(2, (0,))
+        load_pre(2, (1,))
         load_w2(2)
 
         interleave_rows("x", 0, 0, PASS, "scalar")
-        for half in range(2):
-            flip("w2", 0, half, 4 + half)
-            take("w2", 0, half, "vector")
+        flip_take("w2", 0, (4, 5), "vector")
         quantise("w2", 0)
         quantise("x", 0)
         for half in range(2):
             flip("g", 0, half, 6 + half)
             take("g", 0, half)
-        quantise("g", 0, 0, PASS // 2)
-        interleave_rows("x", 1, 0, PASS, "vector")
-        quantise("g", 0, PASS // 2, PASS)
-        load_w2(3)
+            quantise("g", 0, PASS // 2 * half, PASS // 2 * (half + 1))
+        flip_take("w2", 1, (4, 5))
         load_w1(0)
-        load_pre(2, (2, 3))
+        load_pre(3)
+        load_w2(3)
+        load_pre(4)
         load_w1(2)
-        load_pre(2, (0, 1))
 
-        make_dh(0, 0)
-        make_dh(0, 1)
+        for k in range(4):
+            make_dh(0, k)
+        flip_take("g", 1, (6, 7), kind="gate")
         make_dz(0, 0)
-        quantise("x", 1)
         make_dz(0, 1)
-        for half in range(2):
-            flip("w2", 1, half, 4 + half)
-            take("w2", 1, half)
-        make_dh(0, 2)
-        make_dh(0, 3)
         quantise("w2", 1)
         make_dz(0, 2)
         make_dz(0, 3)
 
-        interleave_dz(0, 0, POOL_COLUMNS, "gpsimd", "gate")
-        interleave_dz(0, POOL_COLUMNS, PASS, "scalar", "gate")
-        for j in range(4):
-            make_dh(1, j)
-            make_dz(1, j)
+        for k in range(4):
+            make_dh(1, k)
+        interleave_dz(0, 0, POOL_COLUMNS, "gpsimd")
+        interleave_dz(0, POOL_COLUMNS, PASS, "scalar")
+        flip_take("h", 0, (4, 5))
+        for k in range(4):
+            make_dz(1, k)
+        load_pre(5, (1,))
         load_w1(1)
+        load_pre(5, (0,))
         load_w1(3)
-        load_pre(3, (0, 1))
-        load_pre(3, (2, 3))
-        for half in range(2):
-            flip("g", 1, half, 6 + half)
-            take("g", 1, half)
-            quantise("g", 1, PASS // 2 * half, PASS // 2 * (half + 1))
-        for i in range(2):
-            for half in range(2):
-                flip("h", i, half, 4 + 2 * i + half)
-                take("h", i, half)
+        load_pre(6)
+        load_pre(7)
+        interleave_rows("x", 1, 0, PASS, "scalar")
+        quantise("g", 1, 0, PASS // 2)
         quantise("t", 0)
+        quantise("h", 0)
+        quantise("g", 1, PASS // 2, PASS)
+        flip_take("h", 1, (6, 7))
 
         interleave_dz(1, 0, POOL_COLUMNS, "gpsimd", "gate")
         interleave_dz(1, POOL_COLUMNS, PASS, "scalar", "gate")
-        for j in range(4):
-            make_dh(2, j)
-            make_dz(2, j)
-        for j in range(4):
-            make_dh(3, j)
-        quantise("h", 0)
-        interleave_dz(2, 0, PASS // 2, "vector")
-        interleave_dz(2, PASS // 2, PASS, "scalar")
+        for k in range(4):
+            make_dh(2, k)
+            make_dz(2, k)
+        for k in range(4):
+            make_dh(3, k)
         quantise("h", 1)
+        interleave_dz(2, 0, 256, "vector")
+        interleave_dz(2, 256, PASS, "scalar")
+        quantise("x", 1)
+        flip_take("w2", 2, (4, 5))
+        flip_take("h", 2, (6, 7))
         quantise("t", 2)
         quantise("t", 1)
 
-        for i in (2, 3):
-            for half in range(2):
-                flip("w2", i, half, 4 + 2 * (i % 2) + half)
-                take("w2", i, half)
         interleave_rows("w1", 0, 0, POOL_COLUMNS, "gpsimd", "gate")
         interleave_rows("w1", 0, POOL_COLUMNS, PASS, "scalar", "gate")
-        for j in (3, 0, 1, 2):
-            make_dz(3, j)
-        for number, tile in enumerate((0, 2, 1, 3), 4):
+        for k in (3, 0, 1, 2):
+            make_dz(3, k)
+        for number, tile in zip((4, 5, 6, 7), (0, 2, 1, 3)):
             dw_tile(0, tile, number)
         leave("dw", 0, 0, whole=True)
         leave("dw", 0, 2)
+        flip_take("w2", 3, (3, 0))
         quantise("w2", 2)
         interleave_dz(3, 0, UNIT3_VECTOR_COLUMNS, "vector")
         interleave_dz(3, UNIT3_VECTOR_COLUMNS, PASS, "scalar")
+        flip_take("h", 3, (1, 2), kind="last_gate")
         quantise("w2", 3)
         quantise("t", 3)
         quantise("w1", 0)
         leave("dw", 0, 1)
         leave("dw", 0, 3)
         store_whole("dw", 0)
-        for half in range(2):
-            flip("h", 2, half, 4 + half)
-            take("h", 2, half)
-        for j in range(4):
-            make_dh(4, j)
-        for half in range(2):
-            flip("h", 3, half, 6 + half)
-            take("h", 3, half, kind="last_gate")
+        make_dh(4, 3)
+        make_dh(4, 0)
+        dw_pass(1, 0, 4)
+        dw_pass(1, 2, 5)
+        make_dh(4, 1)
+        make_dh(4, 2)
+        dw_pass(3, 0)
+        dw_pass(3, 2)
 
         interleave_rows("w1", 2, 0, POOL_COLUMNS, "gpsimd", "gate")
         interleave_rows("w1", 1, 0, POOL_COLUMNS, "gpsimd")
-        for j in (3, 2, 0, 1):
-            make_dz(4, j)
-        for tiles, numbers, dh_tiles in (((0, 2), (4, 5), (3, 2)), ((1, 3), (6, 7), (0, 1))):
-            for tile, number in zip(tiles, numbers):
-                dw_tile(1, tile, number)
-            for j in dh_tiles:
-                make_dh(5, j)
-                make_dz(5, j)
+        for k in (3, 0, 1, 2):
+            make_dz(4, k)
+        dw_tile(1, 1, 6)
+        make_dh(5, 3)
+        make_dh(5, 0)
+        dw_tile(1, 3, 7)
+        make_dh(5, 1)
+        make_dh(5, 2)
+        for k in (3, 0, 1, 2):
+            make_dz(5, k)
         leave("dw", 1, 0, whole=True)
         leave("dw", 1, 2)
-        interleave_rows("w1", 1, POOL_COLUMNS, PASS, "scalar")
+        interleave_rows("w1", 2, POOL_COLUMNS, PASS, "scalar", "gate")
         leave("dw", 1, 1)
         leave("dw", 1, 3)
         store_whole("dw", 1)
-        for j in range(4):
+        interleave_rows("w1", 1, POOL_COLUMNS, PASS, "scalar")
+        for j in range(3):
             dx_pass(0, j, 0, 4 + j)
 
-        interleave_rows("w1", 3, PASS // 2, PASS, "vector")
-        interleave_rows("w1", 3, 0, PASS // 2, "scalar")
-        interleave_rows("w1", 2, POOL_COLUMNS, PASS, "scalar", "gate")
-        freed = (3, 2, 0, 1)
-        for j in freed:
-            flip("h", 4 + j // 2, j % 2, j)
-            take("h", 4 + j // 2, j % 2)
+        interleave_rows("w1", 3, 256, PASS, "vector")
+        flip_take("h", 4, (3, 0))
+        interleave_rows("w1", 3, 0, 256, "scalar")
+        flip_take("h", 5, (1, 2))
+        dx_pass(0, 3, 0, 7)
         quantise("w1", 1)
+        quantise("w1", 2)
+        quantise("h", 4)
         quantise("h", 2)
         quantise("w1", 3)
-        quantise("w1", 2)
         quantise("h", 5)
-        quantise("h", 4)
         quantise("h", 3)
-        for j in range(4):
-            dx_pass(0, j, 1)
-        for j in freed:
-            make_dh(6, j)
+        for q, parts in ((1, (3, 0)), (2, (1, 2))):
+            for j in range(4):
+                dx_pass(0, j, q)
+            for k in parts:
+                make_dh(6, k)
 
         interleave_dz(4, 0, PASS // 2, "scalar")
         interleave_dz(5, 0, POOL_COLUMNS, "gpsimd", "last_gate")
-        for j in (2, 3, 0, 1):
+        for j in range(4):
             dx_pass(0, j, 3)
-            dx_pass(0, j, 2)
             leave("dx", 0, j, whole=True)
         store_whole("dx", 0)
-        for j in (1, 0, 2, 3):
-            make_dz(6, j)
+        for k in (2, 3, 0, 1):
+            make_dz(6, k)
         interleave_dz(6, 0, POOL_COLUMNS, "gpsimd")
         interleave_dz(4, PASS // 2, PASS, "scalar")
         interleave_dz(6, POOL_COLUMNS, PASS, "scalar")
-        for j, dh_tiles in ((0, (1, 0)), (1, (2, 3))):
-            for k in dh_tiles:
-                make_dh(7, k)
-                make_dz(7, k)
-            dx_pass(1, j, 0, 6 + j)
+        make_dh(7, 2)
+        for j, k in enumerate((3, 0, 1)):
+            make_dh(7, k)
+            dx_pass(1, j, 0, 4 + j)
             dx_pass(1, j, 1)
-        for half in (1, 0):
-            flip("h", 6, half, half)
-            take("h", 6, half)
-        dx_pass(1, 2, 0, 4)
-        dx_pass(1, 2, 1)
-        for half in range(2):
-            flip("h", 7, half, 2 + half)
-            take("h", 7, half)
+        for k in (2, 3, 0, 1):
+            make_dz(7, k)
+        flip_take("h", 6, (2, 3))
+        dx_pass(1, 3, 0, 7)
+        dx_pass(1, 3, 1)
+        flip_take("h", 7, (0, 1))
 
         quantise("t", 4)
         quantise("t", 6)
         interleave_dz(5, POOL_COLUMNS, PASS, "vector", "last_gate")
         quantise("h", 6)
-        interleave_dz(7, 0, PASS, "vector")
         quantise("h", 7)
+        interleave_dz(7, 0, PASS, "vector")
         quantise("t", 5)
         quantise("t", 7)
-        dw_pass(4, 0, 5)
-        dw_pass(4, 2, 1)
+        dw_pass(4, 0, 2)
+        dw_pass(4, 2, 3)
         dw_pass(6, 0)
         dw_pass(6, 2)
         dw_tile(2, 1, 0)
-        dw_tile(2, 3, 2)
+        dw_tile(2, 3, 1)
         for tile in (0, 2, 1, 3):
             leave("dw", 2, tile)
         store("dw", 2, 0, 0, 1)
         store("dw", 2, 0, 1, 2)
         store("dw", 2, 1)
 
-        for j in range(2):
-            dx_pass(1, j, 2)
-            dx_pass(1, j, 3)
-            leave("dx", 1, j)
-        store("dx", 1, 0)
-        dx_pass(1, 3, 0, 3)
-        dx_pass(1, 3, 1)
-        for j, engine in ((2, "scalar"), (3, "vector")):
+        for j, engine in enumerate(("scalar", "scalar", "scalar", "vector")):
             dx_pass(1, j, 2)
             dx_pass(1, j, 3)
             leave("dx", 1, j, engine)
-            store("dx", 1, 1, j - 2, j - 1)
+            if j % 2:
+                store("dx", 1, j // 2)
 
-        for couple, numbers in enumerate(((5, 1), (0, 2))):
+        for couple, numbers in enumerate(((2, 3), (0, 1))):
             for side, engine in enumerate(("scalar", "vector")):
                 dw_tile(3, couple + 2 * side, numbers[side])
                 leave("dw", 3, couple + 2 * side, engine)

@@ -26,7 +26,7 @@ UNIT3_VECTOR_COLUMNS = 384
 NARROW_BUFS = 14
 WIDE_BUFS = 5
 DZ_BUFS = 4
-GROUPED_BUFS = {"words": 5, "rows": 4, "gate": 1, "last_gate": 1}
+GROUPED_BUFS = {"words": 6, "rows": 4, "gate": 1, "last_gate": 1}
 
 
 def tile_mlp_v_kernel(tc, x, w1, w2, pre, grad_out, out_0, out_1):
@@ -275,7 +275,8 @@ def tile_mlp_v_kernel(tc, x, w1, w2, pre, grad_out, out_0, out_1):
             quantise("g", 0, PASS // 2 * half, PASS // 2 * (half + 1))
         flip_take("w2", 1, (4, 5))
         load_w1(0)
-        load_pre(3)
+        load_pre(3, (1,))
+        load_pre(3, (0,))
         load_w2(3)
         load_pre(4)
         load_w1(2)
@@ -327,17 +328,17 @@ def tile_mlp_v_kernel(tc, x, w1, w2, pre, grad_out, out_0, out_1):
 
         interleave_rows("w1", 0, 0, POOL_COLUMNS, "gpsimd", "gate")
         interleave_rows("w1", 0, POOL_COLUMNS, PASS, "scalar", "gate")
-        for k in (3, 0, 1, 2):
+        for k in (3, 2, 0, 1):
             make_dz(3, k)
         for number, tile in zip((4, 5, 6, 7), (0, 2, 1, 3)):
             dw_tile(0, tile, number)
         leave("dw", 0, 0, whole=True)
         leave("dw", 0, 2)
-        flip_take("w2", 3, (3, 0))
+        flip_take("w2", 3, (3, 2))
         quantise("w2", 2)
         interleave_dz(3, 0, UNIT3_VECTOR_COLUMNS, "vector")
         interleave_dz(3, UNIT3_VECTOR_COLUMNS, PASS, "scalar")
-        flip_take("h", 3, (1, 2), kind="last_gate")
+        flip_take("h", 3, (0, 1))
         quantise("w2", 3)
         quantise("t", 3)
         quantise("w1", 0)
@@ -345,25 +346,25 @@ def tile_mlp_v_kernel(tc, x, w1, w2, pre, grad_out, out_0, out_1):
         leave("dw", 0, 3)
         store_whole("dw", 0)
         make_dh(4, 3)
-        make_dh(4, 0)
+        make_dh(4, 2)
         dw_pass(1, 0, 4)
         dw_pass(1, 2, 5)
+        make_dh(4, 0)
         make_dh(4, 1)
-        make_dh(4, 2)
         dw_pass(3, 0)
         dw_pass(3, 2)
 
         interleave_rows("w1", 2, 0, POOL_COLUMNS, "gpsimd", "gate")
         interleave_rows("w1", 1, 0, POOL_COLUMNS, "gpsimd")
-        for k in (3, 0, 1, 2):
+        for k in (3, 2, 0, 1):
             make_dz(4, k)
         dw_tile(1, 1, 6)
         make_dh(5, 3)
-        make_dh(5, 0)
-        dw_tile(1, 3, 7)
-        make_dh(5, 1)
         make_dh(5, 2)
-        for k in (3, 0, 1, 2):
+        dw_tile(1, 3, 7)
+        make_dh(5, 0)
+        make_dh(5, 1)
+        for k in (3, 2, 0, 1):
             make_dz(5, k)
         leave("dw", 1, 0, whole=True)
         leave("dw", 1, 2)
@@ -375,61 +376,57 @@ def tile_mlp_v_kernel(tc, x, w1, w2, pre, grad_out, out_0, out_1):
         for j in range(3):
             dx_pass(0, j, 0, 4 + j)
 
-        interleave_rows("w1", 3, 256, PASS, "vector")
-        flip_take("h", 4, (3, 0))
-        interleave_rows("w1", 3, 0, 256, "scalar")
-        flip_take("h", 5, (1, 2))
+        interleave_rows("w1", 3, 320, PASS, "vector")
+        flip_take("h", 4, (3, 2))
+        interleave_rows("w1", 3, 0, 320, "scalar")
+        flip_take("h", 5, (0, 1), kind="last_gate")
         dx_pass(0, 3, 0, 7)
-        quantise("w1", 1)
-        quantise("w1", 2)
-        quantise("h", 4)
-        quantise("h", 2)
-        quantise("w1", 3)
-        quantise("h", 5)
-        quantise("h", 3)
-        for q, parts in ((1, (3, 0)), (2, (1, 2))):
+        for what, i in (("w1", 1), ("w1", 2), ("h", 4), ("h", 2), ("w1", 3), ("h", 5), ("h", 3)):
+            quantise(what, i)
+        for q, parts in ((1, (3, 2)), (2, (0, 1))):
             for j in range(4):
                 dx_pass(0, j, q)
             for k in parts:
                 make_dh(6, k)
 
-        interleave_dz(4, 0, PASS // 2, "scalar")
+        interleave_dz(4, 0, 512, "scalar")
         interleave_dz(5, 0, POOL_COLUMNS, "gpsimd", "last_gate")
         for j in range(4):
             dx_pass(0, j, 3)
             leave("dx", 0, j, whole=True)
         store_whole("dx", 0)
-        for k in (2, 3, 0, 1):
+        for k in (3, 2, 0, 1):
             make_dz(6, k)
         interleave_dz(6, 0, POOL_COLUMNS, "gpsimd")
-        interleave_dz(4, PASS // 2, PASS, "scalar")
         interleave_dz(6, POOL_COLUMNS, PASS, "scalar")
-        make_dh(7, 2)
-        for j, k in enumerate((3, 0, 1)):
-            make_dh(7, k)
+        interleave_dz(5, POOL_COLUMNS, PASS, "scalar", "last_gate")
+        make_dh(7, 0, 3)
+        for j, number in enumerate((2, 0)):
+            make_dh(7, j + 1, number)
             dx_pass(1, j, 0, 4 + j)
             dx_pass(1, j, 1)
-        for k in (2, 3, 0, 1):
+        make_dh(7, 3, 1)
+        for k in range(4):
             make_dz(7, k)
-        flip_take("h", 6, (2, 3))
-        dx_pass(1, 3, 0, 7)
-        dx_pass(1, 3, 1)
+        flip_take("h", 6, (7, 3))
+        dx_pass(1, 2, 0, 6)
+        dx_pass(1, 2, 1)
         flip_take("h", 7, (0, 1))
 
         quantise("t", 4)
         quantise("t", 6)
-        interleave_dz(5, POOL_COLUMNS, PASS, "vector", "last_gate")
         quantise("h", 6)
+        interleave_dz(7, 0, 256, "vector")
         quantise("h", 7)
-        interleave_dz(7, 0, PASS, "vector")
+        interleave_dz(7, 256, PASS, "vector")
         quantise("t", 5)
         quantise("t", 7)
         dw_pass(4, 0, 2)
-        dw_pass(4, 2, 3)
+        dw_pass(4, 2, 7)
         dw_pass(6, 0)
         dw_pass(6, 2)
-        dw_tile(2, 1, 0)
-        dw_tile(2, 3, 1)
+        dw_tile(2, 1, 3)
+        dw_tile(2, 3, 0)
         for tile in (0, 2, 1, 3):
             leave("dw", 2, tile)
         store("dw", 2, 0, 0, 1)
@@ -437,13 +434,16 @@ def tile_mlp_v_kernel(tc, x, w1, w2, pre, grad_out, out_0, out_1):
         store("dw", 2, 1)
 
         for j, engine in enumerate(("scalar", "scalar", "scalar", "vector")):
+            if j == 2:
+                dx_pass(1, 3, 0, 1)
+                dx_pass(1, 3, 1)
             dx_pass(1, j, 2)
             dx_pass(1, j, 3)
             leave("dx", 1, j, engine)
             if j % 2:
                 store("dx", 1, j // 2)
 
-        for couple, numbers in enumerate(((2, 3), (0, 1))):
+        for couple, numbers in enumerate(((2, 7), (3, 0))):
             for side, engine in enumerate(("scalar", "vector")):
                 dw_tile(3, couple + 2 * side, numbers[side])
                 leave("dw", 3, couple + 2 * side, engine)

@@ -279,7 +279,7 @@ def tile_mlp_v_kernel(tc, x, w1, w2, pre, grad_out, out_0, out_1):
         load_pre(3, (0,))
         load_w2(3)
         load_pre(4)
-        load_w1(2)
+        load_w1(1)
 
         for k in range(4):
             make_dh(0, k)
@@ -298,7 +298,7 @@ def tile_mlp_v_kernel(tc, x, w1, w2, pre, grad_out, out_0, out_1):
         for k in range(4):
             make_dz(1, k)
         load_pre(5, (1,))
-        load_w1(1)
+        load_w1(2)
         load_pre(5, (0,))
         load_w1(3)
         load_pre(6)
@@ -340,8 +340,8 @@ def tile_mlp_v_kernel(tc, x, w1, w2, pre, grad_out, out_0, out_1):
         interleave_dz(3, UNIT3_VECTOR_COLUMNS, PASS, "scalar")
         flip_take("h", 3, (0, 1))
         quantise("w2", 3)
-        quantise("t", 3)
         quantise("w1", 0)
+        quantise("t", 3)
         leave("dw", 0, 1)
         leave("dw", 0, 3)
         store_whole("dw", 0)
@@ -354,8 +354,8 @@ def tile_mlp_v_kernel(tc, x, w1, w2, pre, grad_out, out_0, out_1):
         dw_pass(3, 0)
         dw_pass(3, 2)
 
-        interleave_rows("w1", 2, 0, POOL_COLUMNS, "gpsimd", "gate")
-        interleave_rows("w1", 1, 0, POOL_COLUMNS, "gpsimd")
+        interleave_rows("w1", 1, 0, 320, "gpsimd", "gate")
+        interleave_rows("w1", 1, 320, PASS, "scalar", "gate")
         for k in (3, 2, 0, 1):
             make_dz(4, k)
         dw_tile(1, 1, 6)
@@ -364,30 +364,39 @@ def tile_mlp_v_kernel(tc, x, w1, w2, pre, grad_out, out_0, out_1):
         dw_tile(1, 3, 7)
         make_dh(5, 0)
         make_dh(5, 1)
+        quantise("w1", 1)
+        interleave_rows("w1", 2, 0, 320, "gpsimd", "gate")
         for k in (3, 2, 0, 1):
             make_dz(5, k)
-        leave("dw", 1, 0, whole=True)
-        leave("dw", 1, 2)
-        interleave_rows("w1", 2, POOL_COLUMNS, PASS, "scalar", "gate")
-        leave("dw", 1, 1)
-        leave("dw", 1, 3)
+        for tile in (0, 2, 1, 3):
+            leave("dw", 1, tile, whole=True)
         store_whole("dw", 1)
-        interleave_rows("w1", 1, POOL_COLUMNS, PASS, "scalar")
-        for j in range(3):
+        interleave_rows("w1", 2, 320, PASS, "scalar", "gate")
+        for j in range(1):
             dx_pass(0, j, 0, 4 + j)
-
-        interleave_rows("w1", 3, 320, PASS, "vector")
+            dx_pass(0, j, 1)
         flip_take("h", 4, (3, 2))
+        for j in range(1, 3):
+            dx_pass(0, j, 0, 4 + j)
+            dx_pass(0, j, 1)
         interleave_rows("w1", 3, 0, 320, "scalar")
         flip_take("h", 5, (0, 1), kind="last_gate")
-        dx_pass(0, 3, 0, 7)
-        for what, i in (("w1", 1), ("w1", 2), ("h", 4), ("h", 2), ("w1", 3), ("h", 5), ("h", 3)):
-            quantise(what, i)
-        for q, parts in ((1, (3, 2)), (2, (0, 1))):
-            for j in range(4):
-                dx_pass(0, j, q)
-            for k in parts:
-                make_dh(6, k)
+        for j in range(3, 4):
+            dx_pass(0, j, 0, 4 + j)
+            dx_pass(0, j, 1)
+        interleave_rows("w1", 3, 320, PASS, "vector")
+        quantise("w1", 2)
+        quantise("h", 4)
+        quantise("h", 2)
+        quantise("w1", 3)
+        quantise("h", 5)
+        quantise("h", 3)
+        make_dh(6, 3)
+        make_dh(6, 2)
+        for j in range(4):
+            dx_pass(0, j, 2)
+        make_dh(6, 0)
+        make_dh(6, 1)
 
         interleave_dz(4, 0, 512, "scalar")
         interleave_dz(5, 0, POOL_COLUMNS, "gpsimd", "last_gate")

from contextlib import ExitStack

import concourse.mybir as mybir
from concourse.masks import make_identity

BATCH, SEQ, DIM, HIDDEN = 2, 512, 512, 2048
P = 128
PACK = 4
PASS = P * PACK
FLOPS = 3 * 2 * BATCH * SEQ * DIM * HIDDEN

F32 = mybir.dt.float32
BF16 = mybir.dt.bfloat16
U32 = mybir.dt.uint32
U8 = mybir.dt.uint8
E4M3 = mybir.dt.float8_e4m3fn_x4
E5M2 = mybir.dt.float8_e5m2_x4
MULT, ADD, MAX = mybir.AluOpType.mult, mybir.AluOpType.add, mybir.AluOpType.max
COPY = mybir.ActivationFunctionType.Copy

UNITS = ((0, 0), (0, 1), (1, 0), (1, 1), (0, 2), (0, 3), (1, 2), (1, 3))

POOL_COLUMNS = 352
UNIT3_VECTOR_COLUMNS = 384

NARROW_BUFS = 14
WIDE_BUFS = 5
DZ_BUFS = 4
GROUPED_BUFS = {"words": 6, "rows": 4, "gate": 1, "last_gate": 1}


def tile_mlp_v_kernel(tc, x, w1, w2, pre, grad_out, out_0, out_1):
    nc = tc.nc
    with ExitStack() as ctx:
        keep = ctx.enter_context(tc.tile_pool(name="keep", bufs=1))
        stream = ctx.enter_context(tc.tile_pool(name="stream", bufs=2))
        psum = ctx.enter_context(tc.psum_pool(name="psum", bufs=1))
        ctx.enter_context(tc.manual_schedule())

        ident = keep.tile([P, P], F32, name="ident")
        make_identity(nc, ident[:])

        raw = {}
        grouped = {}
        codes = {}
        dz = {}
        banks = {}
        passes = {}
        staged = {}

        def bank(number, key):
            banks[key] = psum.tile([P, PASS], F32, name="bank%d" % number)
            return banks[key]

        def narrow(dtype, width):
            return stream.tile([P, width], dtype, name="narrow", bufs=NARROW_BUFS)

        def wide(dtype, width):
            return stream.tile([P, width], dtype, name="wide", bufs=WIDE_BUFS)

        def load_rows(key, src):
            tile = narrow(BF16, PACK * DIM)[:]
            nc.sync.dma_start(
                out=tile.rearrange("p (t d) -> p t d", d=DIM), in_=src.rearrange("(p t) d -> p t d", t=PACK)
            )
            raw[key] = tile
            for half in range(2):
                raw[key + (half,)] = tile[:, 2 * DIM * half : 2 * DIM * (half + 1)]

        def load_g(b):
            load_rows(("g", b), grad_out[b])

        def load_x(b):
            load_rows(("x", b), x[b])

        def load_w1(q):
            load_rows(("w1", q), w1[PASS * q : PASS * q + PASS, :])

        def load_w2(q):
            load_rows(("w2", q), w2[PASS * q : PASS * q + PASS, :])

        def load_w2_half(q, half):
            tile = keep.tile([P, 2 * DIM], BF16, name="w2_half%d" % half)
            rows = w2[PASS * q : PASS * q + PASS, :].rearrange("(p t) d -> p t d", t=PACK)
            nc.sync.dma_start(out=tile[:].rearrange("p (t d) -> p t d", d=DIM), in_=rows[:, 2 * half : 2 * half + 2, :])
            raw["w2", q, half] = tile[:]

        def load_pre(m, halves=(0, 1)):
            b, q = UNITS[m]
            lo, hi = halves[0], halves[-1] + 1
            tile = wide(F32, PACK * PASS) if len(halves) == 2 else narrow(F32, 2 * PASS)
            rows = pre[b].rearrange("(p j) h -> p j h", j=PACK)[:, 2 * lo : 2 * hi, PASS * q : PASS * q + PASS]
            nc.sync.dma_start(out=tile[:].rearrange("p (j h) -> p j h", h=PASS), in_=rows)
            for half in halves:
                raw["pre", m, half] = tile[:, 2 * PASS * (half - lo) : 2 * PASS * (half - lo + 1)]

        def copy(engine, out, in_):
            if engine == "scalar":
                nc.scalar.copy(out=out, in_=in_)
            else:
                nc.vector.tensor_copy(out=out, in_=in_)

        def grouped_tile(key, kind):
            if key not in grouped:
                grouped[key] = stream.tile([P, PACK * PASS], BF16, name=kind, bufs=GROUPED_BUFS[kind], align_bytes=64)
            return grouped[key]

        def flip(what, i, half, number):
            dst = bank(number, (what, i, half))
            for k in range(4):
                if what == "h":
                    first = P * (4 * half + k)
                    words = dz[i][:].bitcast(F32)[:, first : first + P]
                else:
                    words = raw[what, i, half].bitcast(F32)[:, 2 * P * (k // 2) + k % 2 : 2 * P * (k // 2 + 1) : 2]
                nc.tensor.transpose(dst[:, P * k : P * k + P], words, ident[:])

        def take(what, i, half, engine="scalar", kind="words"):
            dst = grouped_tile((what, i), kind)[:].bitcast(F32)[:, PASS * half : PASS * half + PASS]
            src = banks[what, i, half][:]
            if what == "w2":
                copy(engine, dst.rearrange("k (n i) -> k n i", i=4), src.rearrange("k (i n) -> k n i", i=4))
            else:
                copy(
                    engine,
                    dst.rearrange("k (j n v) -> k j n v", j=2, v=2),
                    src.rearrange("k (j v n) -> k j n v", j=2, v=2),
                )

        def interleave_rows(what, i, lo, hi, engine, kind="rows"):
            dst = grouped_tile((what, i), kind)[:, PACK * lo : PACK * hi]
            src = raw[what, i].rearrange("p (t d) -> p t d", t=PACK)[:, :, lo:hi]
            if engine == "gpsimd":
                nc.gpsimd.tensor_scalar(
                    out=dst.rearrange("p (n t) -> p n t", t=PACK),
                    in0=src.rearrange("p t n -> p n t"),
                    scalar1=2.0,
                    scalar2=0.0,
                    op0=MULT,
                    op1=ADD,
                )
                return
            dst = dst.rearrange("p (c i t) -> p c t i", i=4, t=PACK)
            src = src.rearrange("p t (c i) -> p c t i", i=4)
            if engine == "scalar":
                nc.scalar.activation(out=dst, in_=src, func=COPY, scale=2.0)
            else:
                nc.vector.tensor_scalar(out=dst, in0=src, scalar1=2.0, scalar2=None, op0=MULT)

        def interleave_dz(m, lo, hi, engine, kind="rows"):
            pairs = slice(lo // 2, hi // 2)
            dst = grouped_tile(("t", m), kind)[:].rearrange("p (e n j) -> p e n j", e=2, j=PACK)[:, :, pairs, :]
            src = dz[m][:].rearrange("p (j n e) -> p e n j", j=PACK, e=2)[:, :, pairs, :]
            if engine == "gpsimd":
                nc.gpsimd.tensor_scalar(out=dst, in0=src, scalar1=1.0, scalar2=0.0, op0=MULT, op1=ADD)
            else:
                copy(engine, dst, src)

        def quantise(what, i, lo=0, hi=PASS):
            if (what, i) not in codes:
                codes[what, i] = (
                    keep.tile([P, PASS], U32, name="codes_%s%d" % (what, i), align_bytes=64),
                    keep.tile([P, PASS], U8, name="scales_%s%d" % (what, i), align_bytes=64),
                )
            words, scales = codes[what, i]
            dtype = E4M3 if what in ("x", "w1", "w2") else E5M2
            nc.vector.quantize_mx(
                out=words[:, lo:hi].bitcast(dtype),
                scales=scales[:, lo:hi],
                in_=grouped[what, i][:, PACK * lo : PACK * hi],
            )

        def multiply(out, left, tile, right, columns, start, stop):
            cols = slice(P * tile, P * tile + P)
            nc.tensor.matmul_mx(
                out=out,
                lhsT=codes[left][0][:, cols].bitcast(E5M2),
                lhsT_scale=codes[left][1][:, cols],
                rhs=codes[right][0][:, columns].bitcast(E4M3),
                rhs_scale=codes[right][1][:, columns],
                start=start,
                stop=stop,
            )

        def make_dh(m, k, number=None):
            b, q = UNITS[m]
            half, u = divmod(k, 2)
            dst = bank(k if number is None else number, ("dh", m, k))
            for side in range(2):
                out = dst[:, 2 * P * side : 2 * P * (side + 1)]
                multiply(out, ("g", b), 2 * half + side, ("w2", q), slice(2 * P * u, 2 * P * (u + 1)), True, True)

        def make_dz(m, k):
            half, u = divmod(k, 2)
            if m not in dz:
                dz[m] = stream.tile([P, PACK * PASS], BF16, name="dz", bufs=DZ_BUFS, align_bytes=64)
            nc.vector.scalar_tensor_tensor(
                out=dz[m][:].rearrange("p (j u n e) -> p j u n e", j=PACK, u=2, e=2)[:, 2 * half : 2 * half + 2, u, :, :],
                in0=raw["pre", m, half].rearrange("p (j n u e) -> p j n u e", j=2, u=2, e=2)[:, :, :, u, :],
                scalar=0.0,
                in1=banks["dh", m, k][:].rearrange("p (j n e) -> p j n e", j=2, e=2),
                op0=MAX,
                op1=MULT,
            )

        def add_pass(key, number, left, tile, right, total):
            done = passes.get(key, 0)
            passes[key] = done + 1
            if done == 0:
                bank(number, key)
            multiply(banks[key][:], left, tile, right, slice(0, PASS), done == 0, done == total - 1)

        def dx_pass(b, j, q, number=None):
            add_pass(("dx", b, j), number, ("h", UNITS.index((b, q))), j, ("w1", q), HIDDEN // PASS)

        def dw_pass(m, tile, number=None):
            b, q = UNITS[m]
            add_pass(("dw", q, tile), number, ("t", m), tile, ("x", b), BATCH)

        def dw_tile(q, tile, number):
            dw_pass(UNITS.index((0, q)), tile, number)
            dw_pass(UNITS.index((1, q)), tile)

        def leave(what, i, tile, engine="scalar", whole=False):
            couple, side = divmod(tile, 2) if what == "dx" else (tile % 2, tile // 2)
            if (what, i, couple) not in staged:
                if whole:
                    staged[what, i] = wide(F32, 4 * DIM)
                    for k in range(2):
                        staged[what, i, k] = staged[what, i][:, 2 * DIM * k : 2 * DIM * (k + 1)]
                else:
                    staged[what, i, couple] = narrow(F32, 2 * DIM)[:]
            copy(engine, staged[what, i, couple][:, DIM * side : DIM * side + DIM], banks[what, i, tile][:])

        def output_rows(what, i):
            rows = out_0[i] if what == "dx" else out_1[PASS * i : PASS * i + PASS, :]
            return rows.rearrange("(p s f) d -> p s f d", s=2, f=2)

        def store_whole(what, i):
            nc.sync.dma_start(
                out=output_rows(what, i), in_=staged[what, i][:].rearrange("p (s f d) -> p s f d", s=2, f=2)
            )

        def store(what, i, couple, lo=0, hi=2):
            src = staged[what, i, couple].rearrange("p (f d) -> p f d", f=2)
            nc.sync.dma_start(out=output_rows(what, i)[:, couple, lo:hi, :], in_=src[:, lo:hi, :])

        def flip_take(what, i, numbers, engine="scalar", kind="words"):
            for half, number in enumerate(numbers):
                flip(what, i, half, number)
                take(what, i, half, engine, kind)

        load_x(0)
        load_w2_half(0, 0)
        load_w2_half(0, 1)
        load_g(0)
        load_w2(1)
        load_pre(0, (0,))
        load_g(1)
        load_pre(0, (1,))
        load_pre(1, (0,))
        load_pre(1, (1,))
        load_x(1)
        load_pre(2, (0,))
        load_pre(2, (1,))
        load_w2(2)

        interleave_rows("x", 0, 0, PASS, "scalar")
        flip_take("w2", 0, (4, 5), "vector")
        quantise("w2", 0)
        quantise("x", 0)
        for half in range(2):
            flip("g", 0, half, 6 + half)
            take("g", 0, half)
            quantise("g", 0, PASS // 2 * half, PASS // 2 * (half + 1))
        flip_take("w2", 1, (4, 5))
        load_w1(0)
        load_pre(3, (1,))
        load_pre(3, (0,))
        load_w2(3)
        load_pre(4)
        load_w1(1)

        for k in range(4):
            make_dh(0, k)
        flip_take("g", 1, (6, 7), kind="gate")
        make_dz(0, 0)
        make_dz(0, 1)
        quantise("w2", 1)
        make_dz(0, 2)
        make_dz(0, 3)

        for k in range(4):
            make_dh(1, k)
        interleave_dz(0, 0, POOL_COLUMNS, "gpsimd")
        interleave_dz(0, POOL_COLUMNS, PASS, "scalar")
        flip_take("h", 0, (4, 5))
        for k in range(4):
            make_dz(1, k)
        load_pre(5, (1,))
        load_w1(2)
        load_pre(5, (0,))
        load_w1(3)
        load_pre(6)
        load_pre(7)
        interleave_rows("x", 1, 0, PASS, "scalar")
        quantise("g", 1, 0, PASS // 2)
        quantise("t", 0)
        quantise("h", 0)
        quantise("g", 1, PASS // 2, PASS)
        flip_take("h", 1, (6, 7))

        interleave_dz(1, 0, POOL_COLUMNS, "gpsimd", "gate")
        interleave_dz(1, POOL_COLUMNS, PASS, "scalar", "gate")
        for k in range(4):
            make_dh(2, k)
            make_dz(2, k)
        for k in range(4):
            make_dh(3, k)
        quantise("h", 1)
        interleave_dz(2, 0, 256, "vector")
        interleave_dz(2, 256, PASS, "scalar")
        quantise("x", 1)
        flip_take("w2", 2, (4, 5))
        flip_take("h", 2, (6, 7))
        quantise("t", 2)
        quantise("t", 1)

        interleave_rows("w1", 0, 0, POOL_COLUMNS, "gpsimd", "gate")
        interleave_rows("w1", 0, POOL_COLUMNS, PASS, "scalar", "gate")
        for k in (3, 2, 0, 1):
            make_dz(3, k)
        for number, tile in zip((4, 5, 6, 7), (0, 2, 1, 3)):
            dw_tile(0, tile, number)
        leave("dw", 0, 0, whole=True)
        leave("dw", 0, 2)
        flip_take("w2", 3, (3, 2))
        quantise("w2", 2)
        interleave_dz(3, 0, UNIT3_VECTOR_COLUMNS, "vector")
        interleave_dz(3, UNIT3_VECTOR_COLUMNS, PASS, "scalar")
        flip_take("h", 3, (0, 1))
        quantise("w2", 3)
        quantise("w1", 0)
        quantise("t", 3)
        leave("dw", 0, 1)
        leave("dw", 0, 3)
        store_whole("dw", 0)
        make_dh(4, 3)
        make_dh(4, 2)
        dw_pass(1, 0, 4)
        dw_pass(1, 2, 5)
        make_dh(4, 0)
        make_dh(4, 1)
        dw_pass(3, 0)
        dw_pass(3, 2)

        interleave_rows("w1", 1, 0, 320, "gpsimd", "gate")
        interleave_rows("w1", 1, 320, PASS, "scalar", "gate")
        for k in (3, 2, 0, 1):
            make_dz(4, k)
        dw_tile(1, 1, 6)
        make_dh(5, 3)
        make_dh(5, 2)
        dw_tile(1, 3, 7)
        make_dh(5, 0)
        make_dh(5, 1)
        quantise("w1", 1)
        interleave_rows("w1", 2, 0, 320, "gpsimd", "gate")
        for k in (3, 2, 0, 1):
            make_dz(5, k)
        for tile in (0, 2, 1, 3):
            leave("dw", 1, tile, whole=True)
        store_whole("dw", 1)
        interleave_rows("w1", 2, 320, PASS, "scalar", "gate")
        for j in range(1):
            dx_pass(0, j, 0, 4 + j)
            dx_pass(0, j, 1)
        flip_take("h", 4, (3, 2))
        for j in range(1, 3):
            dx_pass(0, j, 0, 4 + j)
            dx_pass(0, j, 1)
        interleave_rows("w1", 3, 0, 320, "scalar")
        flip_take("h", 5, (0, 1), kind="last_gate")
        for j in range(3, 4):
            dx_pass(0, j, 0, 4 + j)
            dx_pass(0, j, 1)
        interleave_rows("w1", 3, 320, PASS, "vector")
        quantise("w1", 2)
        quantise("h", 4)
        quantise("h", 2)
        quantise("w1", 3)
        quantise("h", 5)
        quantise("h", 3)
        make_dh(6, 3)
        make_dh(6, 2)
        for j in range(4):
            dx_pass(0, j, 2)
        make_dh(6, 0)
        make_dh(6, 1)

        interleave_dz(4, 0, 512, "scalar")
        interleave_dz(5, 0, POOL_COLUMNS, "gpsimd", "last_gate")
        for j in range(4):
            dx_pass(0, j, 3)
            leave("dx", 0, j, whole=True)
        store_whole("dx", 0)
        for k in (3, 2, 0, 1):
            make_dz(6, k)
        interleave_dz(6, 0, POOL_COLUMNS, "gpsimd")
        interleave_dz(6, POOL_COLUMNS, PASS, "scalar")
        interleave_dz(5, POOL_COLUMNS, PASS, "scalar", "last_gate")
        make_dh(7, 0, 3)
        for j, number in enumerate((2, 0)):
            make_dh(7, j + 1, number)
            dx_pass(1, j, 0, 4 + j)
            dx_pass(1, j, 1)
        make_dh(7, 3, 1)
        for k in range(4):
            make_dz(7, k)
        flip_take("h", 6, (7, 3))
        dx_pass(1, 2, 0, 6)
        dx_pass(1, 2, 1)
        flip_take("h", 7, (0, 1))

        quantise("t", 4)
        quantise("t", 6)
        quantise("h", 6)
        interleave_dz(7, 0, 256, "vector")
        quantise("h", 7)
        interleave_dz(7, 256, PASS, "vector")
        quantise("t", 5)
        quantise("t", 7)
        dw_pass(4, 0, 2)
        dw_pass(4, 2, 7)
        dw_pass(6, 0)
        dw_pass(6, 2)
        dw_tile(2, 1, 3)
        dw_tile(2, 3, 0)
        for tile in (0, 2, 1, 3):
            leave("dw", 2, tile)
        store("dw", 2, 0, 0, 1)
        store("dw", 2, 0, 1, 2)
        store("dw", 2, 1)

        for j, engine in enumerate(("scalar", "scalar", "scalar", "vector")):
            if j == 2:
                dx_pass(1, 3, 0, 1)
                dx_pass(1, 3, 1)
            dx_pass(1, j, 2)
            dx_pass(1, j, 3)
            leave("dx", 1, j, engine)
            if j % 2:
                store("dx", 1, j // 2)

        for couple, numbers in enumerate(((2, 7), (3, 0))):
            for side, engine in enumerate(("scalar", "vector")):
                dw_tile(3, couple + 2 * side, numbers[side])
                leave("dw", 3, couple + 2 * side, engine)
            store("dw", 3, couple)
